import numpy as np
import ml_dtypes


def mxq(x, axis, fmt="e4m3"):
    dtype, down = {"e4m3": (ml_dtypes.float8_e4m3fn, 7), "e5m2": (ml_dtypes.float8_e5m2, 14)}[fmt]
    v = np.moveaxis(np.asarray(x, np.float32).astype(ml_dtypes.bfloat16).astype(np.float64), axis, -1)
    blocks = v.reshape(v.shape[:-1] + (-1, 32))
    amax = np.abs(blocks).max(-1, keepdims=True)
    byte = np.maximum(np.where(amax > 0, np.frexp(amax)[1] - 1 + 127, 0) - down, 1)
    scale = np.exp2(byte - 127.0)
    codes = (blocks / scale).astype(np.float32).astype(dtype).astype(np.float64)
    return np.moveaxis((codes * scale).reshape(v.shape), -1, axis)


WIDE = False


def mx_kscale(k):
    if not WIDE:
        return np.ones(k)
    levels = np.array([10, -10, 5, -5, 0])
    a = np.random.permutation(np.resize(levels, k // 512 * 4)).reshape(k // 512, 4)
    idx = np.arange(k)
    return np.exp2(a[idx // 512, idx % 128 // 32])


BF16 = ml_dtypes.bfloat16


def bf(x):
    return np.asarray(x, np.float32).astype(BF16)


def f64(x):
    return np.asarray(x).astype(np.float64)


B, CIN, CK, CV, COUT, H, W, KS, DA, DB, DC = 2, 512, 512, 512, 512, 32, 64, 3, 1, 2, 4
DILS = (DA, DB, DC)
NN = KS * KS * len(DILS)
P = H * W


def rn(*shape):
    return np.random.standard_normal(shape)


def shifted(a, d, i, j):
    ap = np.pad(a, ((0, 0), (0, 0), (d, d), (d, d)))
    return ap[:, :, i * d:i * d + H, j * d:j * d + W]


def setup_inputs():
    s, t = mx_kscale(CIN), mx_kscale(CV)
    z = 1.2 * rn(B, NN, H, W)
    e = np.exp(z - z.max(axis=1, keepdims=True))
    return {"x": bf(rn(B, CIN, H, W) * s[None, :, None, None]),
            "attn": bf(e / e.sum(axis=1, keepdims=True)),
            "v_w": bf(rn(CV, CIN) / np.sqrt(CIN) / s[None, :] * t[:, None]),
            "v_b": bf(0.2 * rn(CV) * t),
            "w_w": bf(rn(COUT, CV) * 1.5 / np.sqrt(CV) / t[None, :]),
            "w_b": bf(0.3 * rn(COUT))}


def reference(x, attn, v_w, v_b, w_w, w_b):
    value = (mxq(f64(v_w), 1, "e4m3") @ mxq(f64(x).reshape(B, CIN, P), 1, "e4m3")) + f64(v_b)[None, :, None]
    vf = value.reshape(B, CV, H, W)
    a = f64(attn)
    offs = [(d, i, j) for d in DILS for i in range(KS) for j in range(KS)]
    context = sum(a[:, n:n + 1] * shifted(vf, d, i, j) for n, (d, i, j) in enumerate(offs))
    out = (mxq(f64(w_w), 1, "e4m3") @ mxq(context.reshape(B, CV, P), 1, "e4m3")) + f64(w_b)[None, :, None]
    return out.reshape(B, COUT, H, W)

@@ -1,0 +1,427 @@
+from contextlib import ExitStack
+
+import concourse.mybir as mybir
+from concourse.masks import make_identity
+
+FP8X4 = mybir.dt.float8_e4m3fn_x4
+F32 = mybir.dt.float32
+BF16 = mybir.dt.bfloat16
+U32 = mybir.dt.uint32
+U8 = mybir.dt.uint8
+ALU = mybir.AluOpType
+ACT = mybir.ActivationFunctionType
+AX = mybir.AxisListType
+
+P = 128
+B, C, H, W = 2, 512, 32, 64
+ROW = B * W
+NPIX = H * ROW
+PAD = 8
+CHUNK_ROWS = 4
+CHUNK = CHUNK_ROWS * ROW
+SPLIT_ROW = 21
+V_BANKS = 3
+S_BANKS = 2
+V_LAG = 2
+G_START = 3
+
+FLOPS = 2 * 2 * C * C * B * H * W + 2 * 27 * C * B * H * W
+
+
+def tile_selfattentionmodulev2_pb_kernel(tc, x, attn, v_w, v_b, w_w, w_b, out):
+    nc = tc.nc
+
+    taps = {}
+    for lvl, d in enumerate((1, 2, 4)):
+        for i in range(3):
+            for jj in range(3):
+                di, dj = (i - 1) * d, (jj - 1) * d
+                if di == 0 and dj == 0 and lvl > 0:
+                    continue
+                if dj not in taps:
+                    taps[dj] = []
+                taps[dj].append((di, 9 * lvl + 3 * i + jj))
+    shifts = (0, -1, 1, -2, 2, -4, 4)
+
+    def band_steps(lo, hi, descending):
+        steps = []
+        rows = list(range(max(0, lo - 4), min(H, hi + 4)))
+        if descending:
+            rows = list(reversed(rows))
+        for src in rows:
+            for dj in shifts:
+                uses = [(src - di, n) for (di, n) in taps[dj] if lo <= src - di < hi]
+                if uses:
+                    steps.append((src, dj, uses))
+        return steps
+
+    with ExitStack() as ctx:
+        const = ctx.enter_context(tc.tile_pool(name="const", bufs=1))
+        wpool = ctx.enter_context(tc.tile_pool(name="wpool", bufs=1))
+        xpool = ctx.enter_context(tc.tile_pool(name="xpool", bufs=2))
+        accp = ctx.enter_context(tc.tile_pool(name="accp", bufs=10))
+        prodp = ctx.enter_context(tc.tile_pool(name="prodp", bufs=4))
+        cpool = ctx.enter_context(tc.tile_pool(name="cpool", bufs=2))
+        gpool = ctx.enter_context(tc.tile_pool(name="gpool", bufs=3))
+        opool = ctx.enter_context(tc.tile_pool(name="opool", bufs=2))
+        ps_v = ctx.enter_context(tc.psum_pool(name="ps_v", bufs=V_BANKS))
+        ps_s = ctx.enter_context(tc.psum_pool(name="ps_s", bufs=S_BANKS))
+        ps_m = ctx.enter_context(tc.psum_pool(name="ps_m", bufs=2))
+        ps_c = ctx.enter_context(tc.psum_pool(name="ps_c", bufs=1))
+        ctx.enter_context(tc.manual_schedule())
+
+        def load_weight(w_dram, label):
+            w_sb = wpool.tile([P, 4 * C], BF16, name="w_sb_" + label)
+            nc.sync.dma_start(out=w_sb[:], in_=w_dram.rearrange("(q j) k -> q (j k)", j=4))
+            return w_sb
+
+        def transpose_weight(w_sb, copy):
+            words = w_sb[:].bitcast(F32).rearrange("q (j w u) -> q j u w", j=4, u=2)
+            grouped = wpool.tile([P, 4 * C], BF16, tag="w_grouped", align_bytes=64)
+            gwords = grouped[:].bitcast(F32).rearrange("q (j o u) -> q j o u", j=4, u=2)
+            for half in range(2):
+                pt = ps_m.tile([P, 4, P], F32, tag="mx")
+                for a in range(2):
+                    for u in range(2):
+                        nc.tensor.transpose(pt[:, 2 * a + u, :], words[:, 2 * half + a, u, :], ident_f[:])
+                copy[half](out=gwords[:, 2 * half : 2 * half + 2], in_=pt[:].rearrange("q (a u) o -> q a o u", u=2))
+            return grouped
+
+        def quantise_weight(grouped, label):
+            codes = const.tile([P, C], U32, name="codes_" + label, align_bytes=64)
+            plane = const.tile([P, C], U8, name="plane_" + label, align_bytes=64)
+            nc.vector.quantize_mx(out=codes[:].bitcast(FP8X4), scales=plane[:], in_=grouped[:])
+            return codes, plane
+
+        raw_tiles, gx_tiles = {}, {}
+
+        def load_x(s):
+            raw_tiles[s] = xpool.tile([P, B, 4, CHUNK_ROWS * W], BF16, tag="raw", name="raw%d" % s, bufs=4)
+            for b in range(B):
+                nc.sync.dma_start(
+                    out=raw_tiles[s][:, b],
+                    in_=x[b].rearrange("(q j) r c -> q j (r c)", j=4)[
+                        :, :, s * CHUNK_ROWS * W : (s + 1) * CHUNK_ROWS * W
+                    ],
+                )
+
+        def regroup_x(s, b, copy):
+            if s not in gx_tiles:
+                gx_tiles[s] = xpool.tile([P, CHUNK_ROWS, B, W, 4], BF16, tag="gx", name="gx%d" % s, align_bytes=64)
+            copy(out=gx_tiles[s][:, :, b], in_=raw_tiles[s][:, b].rearrange("q j (r c) -> q r c j", r=CHUNK_ROWS))
+
+        def quantise_x(s):
+            cols = slice(s * CHUNK, (s + 1) * CHUNK)
+            nc.vector.quantize_mx(
+                out=x_codes[:, cols].bitcast(FP8X4),
+                scales=x_plane[:, cols],
+                in_=gx_tiles[s][:].rearrange("q r b c j -> q (r b c j)"),
+            )
+
+        def first_conv(s, chunks, vector_helps):
+            pix = slice(s * CHUNK, (s + 1) * CHUNK)
+            for j in chunks:
+                ps = ps_m.tile([P, CHUNK], F32, tag="mx")
+                nc.tensor.matmul_mx(
+                    out=ps[:],
+                    lhsT=vw_codes[:, j * P : (j + 1) * P].bitcast(FP8X4),
+                    lhsT_scale=vw_plane[:, j * P : (j + 1) * P],
+                    rhs=x_codes[:, pix].bitcast(FP8X4),
+                    rhs_scale=x_plane[:, pix],
+                    start=True,
+                    stop=True,
+                )
+                dst = val[:, j, PAD + s * CHUNK : PAD + (s + 1) * CHUNK]
+                if vector_helps and j % 2 == 1:
+                    nc.vector.tensor_scalar(out=dst, in0=ps[:], scalar1=vb[:, j : j + 1], scalar2=None, op0=ALU.add)
+                else:
+                    nc.scalar.activation(out=dst, in_=ps[:], func=ACT.Identity, bias=vb[:, j : j + 1], scale=1.0)
+
+        ident_f = const.tile([P, P], F32)
+        make_identity(nc, ident_f[:])
+        ident_b = const.tile([P, P], BF16)
+        make_identity(nc, ident_b[:])
+        at3 = const.tile([P, 8 * ROW], BF16)
+        nc.vector.memset(at3[:], 0.0)
+        val = const.tile([P, 4, NPIX + 2 * PAD], F32)
+        nc.vector.memset(val[:, :, 0:PAD], 0.0)
+        nc.vector.memset(val[:, :, PAD + NPIX : PAD + NPIX + PAD], 0.0)
+        x_codes = const.tile([P, NPIX], U32, align_bytes=64)
+        x_plane = const.tile([P, NPIX], U8, align_bytes=64)
+
+        def load_attn(queue, g, b):
+            queue.dma_start(
+                out=at3[32 * g : 32 * g + 27, :].rearrange("n (i b c) -> n i b c", i=8, b=B)[:, :, b, :],
+                in_=attn[b, :, 8 * g : 8 * g + 8, :],
+            )
+
+        vb_bf = const.tile([P, 4], BF16)
+        wb_bf = const.tile([P, 4], BF16)
+        nc.scalar.dma_start(out=vb_bf[:], in_=v_b.rearrange("(q j) -> q j", j=4))
+        nc.scalar.dma_start(out=wb_bf[:], in_=w_b.rearrange("(q j) -> q j", j=4))
+        vw_sb = load_weight(v_w, "vw")
+        load_x(0)
+        for g in range(4):
+            load_attn(nc.scalar, g, 0)
+            load_attn(nc.sync, g, 1)
+        load_x(7)
+        load_x(1)
+        load_x(6)
+        ww_sb = load_weight(w_w, "ww")
+
+        vw_grouped = transpose_weight(vw_sb, (nc.vector.tensor_copy, nc.scalar.copy))
+        regroup_x(0, 0, nc.vector.tensor_copy)
+        regroup_x(0, 1, nc.scalar.copy)
+        vw_codes, vw_plane = quantise_weight(vw_grouped, "vw")
+        vb = const.tile([P, 4], F32)
+        wb = const.tile([P, 4], F32)
+        nc.vector.tensor_copy(out=vb[:], in_=vb_bf[:])
+        nc.vector.tensor_copy(out=wb[:], in_=wb_bf[:])
+        quantise_x(0)
+
+        pa = ps_c.tile([P, 8, P], BF16, tag="ct")
+        for i in range(8):
+            nc.tensor.transpose(pa[:, i, :], at3[:, i * ROW : (i + 1) * ROW], ident_b[:])
+        first_conv(0, range(4), False)
+        a_t = const.tile([P, 8, 4, 32], F32)
+        nc.vector.tensor_copy(out=a_t[:].rearrange("p i g n -> p i (g n)"), in_=pa[:])
+        mk = const.tile([P, 8], F32)
+        idv = ident_f[:].rearrange("p (h c) -> p h c", h=2)
+        for lvl, d in enumerate((1, 2, 4)):
+            nc.vector.tensor_reduce(out=mk[:, 2 * lvl : 2 * lvl + 1], in_=idv[:, :, 0:d], axis=AX.XY, op=ALU.add)
+            nc.vector.tensor_reduce(
+                out=mk[:, 2 * lvl + 1 : 2 * lvl + 2], in_=idv[:, :, W - d : W], axis=AX.XY, op=ALU.add
+            )
+        nc.vector.tensor_scalar(
+            out=mk[:, 0:6], in0=mk[:, 0:6], scalar1=-1.0, scalar2=1.0, op0=ALU.mult, op1=ALU.add
+        )
+        a_taps = a_t[:, :, :, 0:27].rearrange("p i g (l a j) -> p i g l a j", l=3, a=3)
+        for lvl in range(3):
+            for side in range(2):
+                view = a_taps[:, :, :, lvl, :, 2 * side]
+                nc.vector.tensor_scalar(
+                    out=view,
+                    in0=view,
+                    scalar1=mk[:, 2 * lvl + side : 2 * lvl + side + 1],
+                    scalar2=None,
+                    op0=ALU.mult,
+                )
+        for n in (13, 22):
+            nc.vector.tensor_tensor(out=a_t[:, :, :, 4], in0=a_t[:, :, :, 4], in1=a_t[:, :, :, n], op=ALU.add)
+
+        def gpsimd_copy(out, in_):
+            nc.gpsimd.tensor_scalar(out=out, in0=in_, scalar1=1.0, scalar2=0.0, op0=ALU.mult, op1=ALU.add)
+
+        regroup_x(7, 0, gpsimd_copy)
+        regroup_x(7, 1, gpsimd_copy)
+        quantise_x(7)
+
+        total = {}
+        for dj in shifts:
+            for di, n in taps[dj]:
+                for r in range(H):
+                    if 0 <= r + di < H:
+                        total[r] = total.get(r, 0) + 1
+        seen = {}
+        acc = {}
+        pair_tiles = {}
+        pair_done = {}
+        pair_codes = {}
+        ww_grouped, ww_q = [], []
+
+        def row_to_words(r, ctx_row):
+            pair = r // 2
+            if pair not in pair_tiles:
+                if 2 * pair < SPLIT_ROW < 2 * pair + 2:
+                    pair_tiles[pair] = gpool.tile(
+                        [P, 2, ROW, 4], BF16, tag="g2_split", name="g2_split", bufs=1, align_bytes=64
+                    )
+                else:
+                    pair_tiles[pair] = gpool.tile(
+                        [P, 2, ROW, 4], BF16, tag="g2", name="g2_%d" % pair, bufs=4, align_bytes=64
+                    )
+                pair_done[pair] = 0
+            ct = ps_c.tile([P, 4, P], BF16, tag="ct")
+            for j in range(4):
+                nc.tensor.transpose(ct[:, j, :], ctx_row[:, j * P : (j + 1) * P], ident_b[:])
+            nc.scalar.copy(out=pair_tiles[pair][:, r % 2], in_=ct[:].rearrange("q j x -> q x j"))
+            pair_done[pair] += 1
+            return pair_done[pair] == 2
+
+        def quantise_pair(pair):
+            c_codes = gpool.tile([P, 2 * ROW], U32, tag="c_codes", name="c_codes%d" % pair, align_bytes=64)
+            c_plane = gpool.tile([P, 2 * ROW], U8, tag="c_plane", name="c_plane%d" % pair, align_bytes=64)
+            nc.vector.quantize_mx(
+                out=c_codes[:].bitcast(FP8X4),
+                scales=c_plane[:],
+                in_=pair_tiles[pair][:].rearrange("q r x j -> q (r x j)"),
+            )
+            pair_codes[pair] = (c_codes, c_plane)
+
+        def second_conv(pair):
+            c_codes, c_plane = pair_codes[pair]
+            ww_codes, ww_plane = ww_q[0]
+            ot = opool.tile([P, 4, B, 2, W], F32, tag="ot")
+            banks = []
+            for half in range(2):
+                po = ps_m.tile([P, 2, 2 * ROW], F32, tag="mx")
+                banks.append(po)
+                for a in range(2):
+                    j = 2 * half + a
+                    nc.tensor.matmul_mx(
+                        out=po[:, a, :],
+                        lhsT=ww_codes[:, j * P : (j + 1) * P].bitcast(FP8X4),
+                        lhsT_scale=ww_plane[:, j * P : (j + 1) * P],
+                        rhs=c_codes[:].bitcast(FP8X4),
+                        rhs_scale=c_plane[:],
+                        start=True,
+                        stop=True,
+                    )
+            for j in range(4):
+                nc.scalar.activation(
+                    out=ot[:, j].rearrange("q b r c -> q r b c"),
+                    in_=banks[j // 2][:, j % 2, :].rearrange("q (r b c) -> q r b c", r=2, b=B),
+                    func=ACT.Identity,
+                    bias=wb[:, j : j + 1],
+                    scale=1.0,
+                )
+            for b in range(B):
+                nc.sync.dma_start(
+                    out=out[b].rearrange("(q j) r c -> q j (r c)", j=4)[:, :, pair * 2 * W : (pair + 1) * 2 * W],
+                    in_=ot[:, :, b].rearrange("q j r c -> q j (r c)"),
+                )
+
+        def shifted_tile(pool, tag, src, dj):
+            vt = pool.tile([P, C], F32, tag=tag)
+            start = PAD + src * ROW + dj
+            for j in range(4):
+                nc.tensor.transpose(vt[:, j * P : (j + 1) * P], val[:, j, start : start + ROW], ident_f[:])
+            return vt
+
+        v_steps = band_steps(0, SPLIT_ROW, False)
+        g_steps = band_steps(SPLIT_ROW, H, True)
+        n_v, n_g = len(v_steps), len(g_steps)
+        v_uses = sum([len(st[2]) for st in v_steps])
+        g_uses = sum([len(st[2]) for st in g_steps])
+        v_tiles, g_tiles = {}, {}
+        pe_tasks, vec_tasks, g_pe_tasks = {}, {}, {}
+        cursor = {"v": 0}
+
+        def defer(table, key, fn):
+            if key not in table:
+                table[key] = []
+            table[key].append(fn)
+
+        def run(table, key):
+            for fn in table.get(key, []):
+                fn()
+
+        def make_v_tile(k):
+            if k < n_v:
+                v_tiles[k] = shifted_tile(ps_v, "vt_v", v_steps[k][0], v_steps[k][1])
+
+        def make_g_tile(m):
+            if m < n_g:
+                g_tiles[m] = shifted_tile(ps_s, "vt_s", g_steps[m][0], g_steps[m][1])
+
+        def v_row_done(k, r, ctx_row):
+            def words():
+                if row_to_words(r, ctx_row):
+                    defer(vec_tasks, k + 1 + V_LAG, lambda: quantise_pair(r // 2))
+                    defer(pe_tasks, k + 2 + V_LAG, lambda: second_conv(r // 2))
+
+            defer(pe_tasks, k + 1, words)
+
+        def g_row_done(m, r, ctx_row):
+            def words():
+                if row_to_words(r, ctx_row):
+                    defer(vec_tasks, cursor["v"] + 1, lambda: quantise_pair(r // 2))
+                    defer(pe_tasks, cursor["v"] + 2, lambda: second_conv(r // 2))
+
+            defer(g_pe_tasks, m + 2, words)
+
+        def vector_step(k):
+            cursor["v"] = k + 1
+            make_v_tile(k + V_BANKS - 1)
+            run(pe_tasks, k)
+            if k < n_v:
+                vt = v_tiles[k]
+                for r, n in v_steps[k][2]:
+                    a = a_t[:, r % 8, r // 8, n : n + 1]
+                    seen[r] = seen.get(r, 0) + 1
+                    if seen[r] == 1:
+                        acc[r] = accp.tile([P, C], F32, tag="acc_v", name="acc_v%d" % r)
+                        nc.vector.tensor_scalar(out=acc[r][:], in0=vt[:], scalar1=a, scalar2=None, op0=ALU.mult)
+                    elif seen[r] < total[r]:
+                        nc.vector.scalar_tensor_tensor(
+                            out=acc[r][:], in0=vt[:], scalar=a, in1=acc[r][:], op0=ALU.mult, op1=ALU.add
+                        )
+                    else:
+                        ctx_row = cpool.tile([P, C], BF16, tag="ctx_v", name="ctx_v%d" % r)
+                        nc.vector.scalar_tensor_tensor(
+                            out=ctx_row[:], in0=vt[:], scalar=a, in1=acc[r][:], op0=ALU.mult, op1=ALU.add
+                        )
+                        v_row_done(k, r, ctx_row)
+            run(vec_tasks, k)
+
+        def gpsimd_step(m):
+            make_g_tile(m + S_BANKS - 1)
+            run(g_pe_tasks, m)
+            if m < n_g:
+                vt = g_tiles[m]
+                for r, n in g_steps[m][2]:
+                    a = a_t[:, r % 8, r // 8, n : n + 1]
+                    seen[r] = seen.get(r, 0) + 1
+                    if seen[r] == 1:
+                        acc[r] = accp.tile([P, C], F32, tag="acc_g", name="acc_g%d" % r)
+                        nc.scalar.activation(out=acc[r][:], in_=vt[:], func=ACT.Copy, scale=a)
+                        continue
+                    prod = prodp.tile([P, C], F32, tag="prod")
+                    nc.scalar.activation(out=prod[:], in_=vt[:], func=ACT.Copy, scale=a)
+                    if seen[r] < total[r]:
+                        nc.gpsimd.tensor_tensor(out=acc[r][:], in0=acc[r][:], in1=prod[:], op=ALU.add)
+                    else:
+                        ctx_row = cpool.tile([P, C], BF16, tag="ctx_g", name="ctx_g%d" % r)
+                        nc.gpsimd.tensor_tensor(out=ctx_row[:], in0=acc[r][:], in1=prod[:], op=ALU.add)
+                        g_row_done(m, r, ctx_row)
+
+        def later_chunk(s, k0, next_load):
+            def regroup():
+                regroup_x(s, 0, nc.scalar.copy)
+                regroup_x(s, 1, nc.scalar.copy)
+                if next_load is not None:
+                    load_x(next_load)
+
+            defer(pe_tasks, k0, regroup)
+            defer(vec_tasks, k0 + 4, lambda: quantise_x(s))
+            defer(pe_tasks, k0 + 5, lambda: first_conv(s, (0, 1), False))
+            defer(pe_tasks, k0 + 7, lambda: first_conv(s, (2, 3), False))
+
+        defer(pe_tasks, 0, lambda: first_conv(7, (0, 1), False))
+        defer(pe_tasks, 1, lambda: first_conv(7, (2, 3), False))
+        defer(pe_tasks, G_START - 1, lambda: make_g_tile(0))
+        later_chunk(1, 5, 2)
+        defer(pe_tasks, 10, lambda: ww_grouped.append(transpose_weight(ww_sb, (nc.scalar.copy, nc.scalar.copy))))
+        defer(vec_tasks, 14, lambda: ww_q.append(quantise_weight(ww_grouped[0], "ww")))
+        later_chunk(6, 12, 5)
+        later_chunk(2, 22, 3)
+        later_chunk(5, 32, 4)
+        later_chunk(3, 42, None)
+        later_chunk(4, 52, None)
+
+        for k in range(V_BANKS - 1):
+            make_v_tile(k)
+        iv, ig = 0, 0
+        tv, tg = 0.0, 0.0
+        for step in range(n_v + n_g + 3):
+            take_v = ig >= n_g + 3 or iv < G_START or (iv < n_v and tv <= tg)
+            if take_v:
+                vector_step(iv)
+                tv += len(v_steps[iv][2]) / v_uses
+                iv += 1
+            else:
+                gpsimd_step(ig)
+                tg += (len(g_steps[ig][2]) if ig < n_g else 1) / g_uses
+                ig += 1
+        for k in range(n_v, n_v + 2 * V_LAG + 4):
+            vector_step(k)

@@ -19,7 +19,7 @@ NPIX = H * ROW
 PAD = 8
 CHUNK_ROWS = 4
 CHUNK = CHUNK_ROWS * ROW
-SPLIT_ROW = 21
+SPLIT_ROW = 23
 V_BANKS = 3
 S_BANKS = 2
 V_LAG = 2

@@ -24,6 +24,11 @@ V_BANKS = 3
 S_BANKS = 2
 V_LAG = 2
 G_START = 3
+BAND_LO, BAND_HI = 3, 28
+BAND_GROUP = 5
+APAD = 16
+BAND_W = 144
+BAND_PITCH = P * (BAND_W + 1)
 
 FLOPS = 2 * 2 * C * C * B * H * W + 2 * 27 * C * B * H * W
 
@@ -50,9 +55,15 @@ def tile_selfattentionmodulev2_pb_kernel(tc, x, attn, v_w, v_b, w_w, w_b, out):
             rows = list(reversed(rows))
         for src in rows:
             for dj in shifts:
-                uses = [(src - di, n) for (di, n) in taps[dj] if lo <= src - di < hi]
+                uses = [
+                    (src - di, n)
+                    for (di, n) in taps[dj]
+                    if lo <= src - di < hi and not (di == 0 and BAND_LO <= src < BAND_HI)
+                ]
                 if uses:
                     steps.append((src, dj, uses))
+            if lo <= src < hi and BAND_LO <= src < BAND_HI:
+                steps.append((src, None, [(src, None)]))
         return steps
 
     with ExitStack() as ctx:
@@ -64,6 +75,7 @@ def tile_selfattentionmodulev2_pb_kernel(tc, x, attn, v_w, v_b, w_w, w_b, out):
         cpool = ctx.enter_context(tc.tile_pool(name="cpool", bufs=2))
         gpool = ctx.enter_context(tc.tile_pool(name="gpool", bufs=3))
         opool = ctx.enter_context(tc.tile_pool(name="opool", bufs=2))
+        bpool = ctx.enter_context(tc.tile_pool(name="bpool", bufs=3))
         ps_v = ctx.enter_context(tc.psum_pool(name="ps_v", bufs=V_BANKS))
         ps_s = ctx.enter_context(tc.psum_pool(name="ps_s", bufs=S_BANKS))
         ps_m = ctx.enter_context(tc.psum_pool(name="ps_m", bufs=2))
@@ -141,8 +153,13 @@ def tile_selfattentionmodulev2_pb_kernel(tc, x, attn, v_w, v_b, w_w, w_b, out):
         make_identity(nc, ident_f[:])
         ident_b = const.tile([P, P], BF16)
         make_identity(nc, ident_b[:])
-        at3 = const.tile([P, 8 * ROW], BF16)
+        at3 = const.tile([P, 8 * ROW + 2 * APAD], BF16)
         nc.vector.memset(at3[:], 0.0)
+        bt = const.tile([P, H, 16], F32)
+        nc.gpsimd.memset(bt[:], 0.0)
+        zeros = const.tile([P, BAND_W + 1], F32)
+        nc.gpsimd.memset(zeros[:], 0.0)
+        scratch = out.rearrange("b o r c -> (b o r c)")
         val = const.tile([P, 4, NPIX + 2 * PAD], F32)
         nc.vector.memset(val[:, :, 0:PAD], 0.0)
         nc.vector.memset(val[:, :, PAD + NPIX : PAD + NPIX + PAD], 0.0)
@@ -151,7 +168,9 @@ def tile_selfattentionmodulev2_pb_kernel(tc, x, attn, v_w, v_b, w_w, w_b, out):
 
         def load_attn(queue, g, b):
             queue.dma_start(
-                out=at3[32 * g : 32 * g + 27, :].rearrange("n (i b c) -> n i b c", i=8, b=B)[:, :, b, :],
+                out=at3[32 * g : 32 * g + 27, APAD : APAD + 8 * ROW].rearrange("n (i b c) -> n i b c", i=8, b=B)[
+                    :, :, b, :
+                ],
                 in_=attn[b, :, 8 * g : 8 * g + 8, :],
             )
 
@@ -168,6 +187,10 @@ def tile_selfattentionmodulev2_pb_kernel(tc, x, attn, v_w, v_b, w_w, w_b, out):
         load_x(1)
         load_x(6)
         ww_sb = load_weight(w_w, "ww")
+        for ri in range(BAND_HI - BAND_LO):
+            nc.sync.dma_start(
+                out=scratch[ri * BAND_PITCH : (ri + 1) * BAND_PITCH].rearrange("(p f) -> p f", p=P), in_=zeros[:]
+            )
 
         vw_grouped = transpose_weight(vw_sb, (nc.vector.tensor_copy, nc.scalar.copy))
         regroup_x(0, 0, nc.vector.tensor_copy)
@@ -181,7 +204,7 @@ def tile_selfattentionmodulev2_pb_kernel(tc, x, attn, v_w, v_b, w_w, w_b, out):
 
         pa = ps_c.tile([P, 8, P], BF16, tag="ct")
         for i in range(8):
-            nc.tensor.transpose(pa[:, i, :], at3[:, i * ROW : (i + 1) * ROW], ident_b[:])
+            nc.tensor.transpose(pa[:, i, :], at3[:, APAD + i * ROW : APAD + (i + 1) * ROW], ident_b[:])
         first_conv(0, range(4), False)
         a_t = const.tile([P, 8, 4, 32], F32)
         nc.vector.tensor_copy(out=a_t[:].rearrange("p i g n -> p i (g n)"), in_=pa[:])
@@ -222,6 +245,8 @@ def tile_selfattentionmodulev2_pb_kernel(tc, x, attn, v_w, v_b, w_w, w_b, out):
                 for r in range(H):
                     if 0 <= r + di < H:
                         total[r] = total.get(r, 0) + 1
+        for r in range(BAND_LO, BAND_HI):
+            total[r] -= 6
         seen = {}
         acc = {}
         pair_tiles = {}
@@ -298,6 +323,64 @@ def tile_selfattentionmodulev2_pb_kernel(tc, x, attn, v_w, v_b, w_w, w_b, out):
                 nc.tensor.transpose(vt[:, j * P : (j + 1) * P], val[:, j, start : start + ROW], ident_f[:])
             return vt
 
+        btv = bt[:].rearrange("p (g i) j -> p i g j", g=4)
+        shifted_attn = {}
+        a_band = []
+        band_rhs = {}
+
+        def shift_attn(lvl, side):
+            dj = (2 * side - 1) * (1, 2, 4)[lvl]
+            pa_s = ps_m.tile([P, 8, P], BF16, tag="mx")
+            for i in range(8):
+                nc.tensor.transpose(
+                    pa_s[:, i, :], at3[:, APAD + i * ROW - dj : APAD + (i + 1) * ROW - dj], ident_b[:]
+                )
+            shifted_attn[(lvl, side)] = pa_s
+
+        def band_column(lvl, side):
+            dj = (2 * side - 1) * (1, 2, 4)[lvl]
+            n = 9 * lvl + 3 + 2 * side
+            nc.vector.tensor_scalar(
+                out=btv[:, :, :, 8 - dj],
+                in0=shifted_attn[(lvl, side)][:].rearrange("p i (g n) -> p i g n", g=4)[:, :, :, n],
+                scalar1=mk[:, 2 * lvl + 1 - side : 2 * lvl + 2 - side],
+                scalar2=None,
+                op0=ALU.mult,
+            )
+
+        def skew_band():
+            n_band = BAND_HI - BAND_LO
+            nc.sync.dma_start(
+                out=scratch[0 : n_band * BAND_PITCH].rearrange("(r p t) -> p r t", p=P, t=BAND_W + 1)[:, :, 0:16],
+                in_=bt[:, BAND_LO:BAND_HI, :],
+            )
+            for q in range(n_band // BAND_GROUP):
+                a_q = const.tile([P, BAND_GROUP, BAND_W], F32, name="a_band%d" % q)
+                nc.sync.dma_start(
+                    out=a_q[:],
+                    in_=scratch[q * BAND_GROUP * BAND_PITCH : (q + 1) * BAND_GROUP * BAND_PITCH]
+                    .rearrange("(r m) -> r m", m=BAND_PITCH)[:, 0 : P * BAND_W]
+                    .rearrange("r (p c) -> p r c", c=BAND_W),
+                )
+                a_band.append(a_q)
+
+        def band_prepare(r):
+            pt = shifted_tile(ps_m, "mx", r, 0)
+            band_rhs[r] = bpool.tile([P, C], F32, tag="vt0", name="vt0_%d" % r)
+            nc.scalar.copy(out=band_rhs[r][:], in_=pt[:])
+
+        def band_tile(pool, tag, r):
+            vt = pool.tile([P, C], F32, tag=tag)
+            ri = r - BAND_LO
+            nc.tensor.matmul(
+                out=vt[:],
+                lhsT=a_band[ri // BAND_GROUP][:, ri % BAND_GROUP, 8 : 8 + P],
+                rhs=band_rhs[r][:],
+                start=True,
+                stop=True,
+            )
+            return vt
+
         v_steps = band_steps(0, SPLIT_ROW, False)
         g_steps = band_steps(SPLIT_ROW, H, True)
         n_v, n_g = len(v_steps), len(g_steps)
@@ -317,11 +400,15 @@ def tile_selfattentionmodulev2_pb_kernel(tc, x, attn, v_w, v_b, w_w, w_b, out):
                 fn()
 
         def make_v_tile(k):
-            if k < n_v:
+            if k < n_v and v_steps[k][1] is None:
+                v_tiles[k] = band_tile(ps_v, "vt_v", v_steps[k][0])
+            elif k < n_v:
                 v_tiles[k] = shifted_tile(ps_v, "vt_v", v_steps[k][0], v_steps[k][1])
 
         def make_g_tile(m):
-            if m < n_g:
+            if m < n_g and g_steps[m][1] is None:
+                g_tiles[m] = band_tile(ps_s, "vt_s", g_steps[m][0])
+            elif m < n_g:
                 g_tiles[m] = shifted_tile(ps_s, "vt_s", g_steps[m][0], g_steps[m][1])
 
         def v_row_done(k, r, ctx_row):
@@ -347,7 +434,7 @@ def tile_selfattentionmodulev2_pb_kernel(tc, x, attn, v_w, v_b, w_w, w_b, out):
             if k < n_v:
                 vt = v_tiles[k]
                 for r, n in v_steps[k][2]:
-                    a = a_t[:, r % 8, r // 8, n : n + 1]
+                    a = 1.0 if n is None else a_t[:, r % 8, r // 8, n : n + 1]
                     seen[r] = seen.get(r, 0) + 1
                     if seen[r] == 1:
                         acc[r] = accp.tile([P, C], F32, tag="acc_v", name="acc_v%d" % r)
@@ -370,7 +457,7 @@ def tile_selfattentionmodulev2_pb_kernel(tc, x, attn, v_w, v_b, w_w, w_b, out):
             if m < n_g:
                 vt = g_tiles[m]
                 for r, n in g_steps[m][2]:
-                    a = a_t[:, r % 8, r // 8, n : n + 1]
+                    a = 1.0 if n is None else a_t[:, r % 8, r // 8, n : n + 1]
                     seen[r] = seen.get(r, 0) + 1
                     if seen[r] == 1:
                         acc[r] = accp.tile([P, C], F32, tag="acc_g", name="acc_g%d" % r)
@@ -400,14 +487,25 @@ def tile_selfattentionmodulev2_pb_kernel(tc, x, attn, v_w, v_b, w_w, w_b, out):
         defer(pe_tasks, 0, lambda: first_conv(7, (0, 1), False))
         defer(pe_tasks, 1, lambda: first_conv(7, (2, 3), False))
         defer(pe_tasks, G_START - 1, lambda: make_g_tile(0))
-        later_chunk(1, 5, 2)
+        defer(vec_tasks, 1, lambda: nc.vector.tensor_copy(out=btv[:, :, :, 8], in_=a_t[:, :, :, 4]))
+        for idx in range(6):
+            defer(pe_tasks, 2 + idx, lambda idx=idx: shift_attn(idx // 2, idx % 2))
+            defer(vec_tasks, 3 + idx, lambda idx=idx: band_column(idx // 2, idx % 2))
+        defer(vec_tasks, 9, skew_band)
+        for k, st in enumerate(v_steps):
+            if st[1] is None:
+                defer(pe_tasks, k - 6, lambda r=st[0]: band_prepare(r))
+        for m, st in enumerate(g_steps):
+            if st[1] is None:
+                defer(g_pe_tasks, m - 3, lambda r=st[0]: band_prepare(r))
+        later_chunk(1, 9, 2)
         defer(pe_tasks, 10, lambda: ww_grouped.append(transpose_weight(ww_sb, (nc.scalar.copy, nc.scalar.copy))))
         defer(vec_tasks, 14, lambda: ww_q.append(quantise_weight(ww_grouped[0], "ww")))
-        later_chunk(6, 12, 5)
-        later_chunk(2, 22, 3)
-        later_chunk(5, 32, 4)
-        later_chunk(3, 42, None)
-        later_chunk(4, 52, None)
+        later_chunk(6, 18, 5)
+        later_chunk(2, 27, 3)
+        later_chunk(5, 36, 4)
+        later_chunk(3, 45, None)
+        later_chunk(4, 54, None)
 
         for k in range(V_BANKS - 1):
             make_v_tile(k)

@@ -22,9 +22,14 @@ CHUNK = CHUNK_ROWS * ROW
 SPLIT_ROW = 23
 V_BANKS = 3
 S_BANKS = 2
+M_BANKS = 3
+S_AHEAD = 1
+V_AHEAD = 2
+HALF_GAP = 1
 V_LAG = 2
 G_START = 3
 BAND_LO, BAND_HI = 3, 28
+BAND_FIRST = 8
 BAND_GROUP = 5
 APAD = 16
 BAND_W = 144
@@ -62,7 +67,7 @@ def tile_selfattentionmodulev2_pb_kernel(tc, x, attn, v_w, v_b, w_w, w_b, out):
                 ]
                 if uses:
                     steps.append((src, dj, uses))
-            if lo <= src < hi and BAND_LO <= src < BAND_HI:
+            if lo <= src < hi and BAND_LO <= src < BAND_HI and (descending or src < BAND_FIRST):
                 steps.append((src, None, [(src, None)]))
         return steps
 
@@ -70,7 +75,7 @@ def tile_selfattentionmodulev2_pb_kernel(tc, x, attn, v_w, v_b, w_w, w_b, out):
         const = ctx.enter_context(tc.tile_pool(name="const", bufs=1))
         wpool = ctx.enter_context(tc.tile_pool(name="wpool", bufs=1))
         xpool = ctx.enter_context(tc.tile_pool(name="xpool", bufs=2))
-        accp = ctx.enter_context(tc.tile_pool(name="accp", bufs=10))
+        accp = ctx.enter_context(tc.tile_pool(name="accp", bufs=11))
         prodp = ctx.enter_context(tc.tile_pool(name="prodp", bufs=4))
         cpool = ctx.enter_context(tc.tile_pool(name="cpool", bufs=2))
         gpool = ctx.enter_context(tc.tile_pool(name="gpool", bufs=3))
@@ -78,8 +83,7 @@ def tile_selfattentionmodulev2_pb_kernel(tc, x, attn, v_w, v_b, w_w, w_b, out):
         bpool = ctx.enter_context(tc.tile_pool(name="bpool", bufs=3))
         ps_v = ctx.enter_context(tc.psum_pool(name="ps_v", bufs=V_BANKS))
         ps_s = ctx.enter_context(tc.psum_pool(name="ps_s", bufs=S_BANKS))
-        ps_m = ctx.enter_context(tc.psum_pool(name="ps_m", bufs=2))
-        ps_c = ctx.enter_context(tc.psum_pool(name="ps_c", bufs=1))
+        ps_m = ctx.enter_context(tc.psum_pool(name="ps_m", bufs=M_BANKS))
         ctx.enter_context(tc.manual_schedule())
 
         def load_weight(w_dram, label):
@@ -184,8 +188,8 @@ def tile_selfattentionmodulev2_pb_kernel(tc, x, attn, v_w, v_b, w_w, w_b, out):
             load_attn(nc.scalar, g, 0)
             load_attn(nc.sync, g, 1)
         load_x(7)
+        load_x(2)
         load_x(1)
-        load_x(6)
         ww_sb = load_weight(w_w, "ww")
         for ri in range(BAND_HI - BAND_LO):
             nc.sync.dma_start(
@@ -202,7 +206,7 @@ def tile_selfattentionmodulev2_pb_kernel(tc, x, attn, v_w, v_b, w_w, w_b, out):
         nc.vector.tensor_copy(out=wb[:], in_=wb_bf[:])
         quantise_x(0)
 
-        pa = ps_c.tile([P, 8, P], BF16, tag="ct")
+        pa = ps_m.tile([P, 8, P], BF16, tag="mx")
         for i in range(8):
             nc.tensor.transpose(pa[:, i, :], at3[:, APAD + i * ROW : APAD + (i + 1) * ROW], ident_b[:])
         first_conv(0, range(4), False)
@@ -266,7 +270,7 @@ def tile_selfattentionmodulev2_pb_kernel(tc, x, attn, v_w, v_b, w_w, w_b, out):
                         [P, 2, ROW, 4], BF16, tag="g2", name="g2_%d" % pair, bufs=4, align_bytes=64
                     )
                 pair_done[pair] = 0
-            ct = ps_c.tile([P, 4, P], BF16, tag="ct")
+            ct = ps_m.tile([P, 4, P], BF16, tag="mx")
             for j in range(4):
                 nc.tensor.transpose(ct[:, j, :], ctx_row[:, j * P : (j + 1) * P], ident_b[:])
             nc.scalar.copy(out=pair_tiles[pair][:, r % 2], in_=ct[:].rearrange("q j x -> q x j"))
@@ -369,17 +373,24 @@ def tile_selfattentionmodulev2_pb_kernel(tc, x, attn, v_w, v_b, w_w, w_b, out):
             band_rhs[r] = bpool.tile([P, C], F32, tag="vt0", name="vt0_%d" % r)
             nc.scalar.copy(out=band_rhs[r][:], in_=pt[:])
 
-        def band_tile(pool, tag, r):
-            vt = pool.tile([P, C], F32, tag=tag)
+        band_psum = {}
+
+        def band_half(r, half):
+            if half == 0:
+                band_psum[r] = ps_m.tile([P, C], F32, tag="mx", name="pb%d" % r)
             ri = r - BAND_LO
+            cols = slice(half * (C // 2), (half + 1) * (C // 2))
             nc.tensor.matmul(
-                out=vt[:],
+                out=band_psum[r][:, cols],
                 lhsT=a_band[ri // BAND_GROUP][:, ri % BAND_GROUP, 8 : 8 + P],
-                rhs=band_rhs[r][:],
+                rhs=band_rhs[r][:, cols],
                 start=True,
                 stop=True,
             )
-            return vt
+            if half == 1 and BAND_FIRST <= r < SPLIT_ROW:
+                acc[r] = accp.tile([P, C], F32, tag="acc_v", name="acc_v%d" % r)
+                nc.scalar.copy(out=acc[r][:], in_=band_psum[r][:])
+                seen[r] = 1
 
         v_steps = band_steps(0, SPLIT_ROW, False)
         g_steps = band_steps(SPLIT_ROW, H, True)
@@ -401,13 +412,13 @@ def tile_selfattentionmodulev2_pb_kernel(tc, x, attn, v_w, v_b, w_w, w_b, out):
 
         def make_v_tile(k):
             if k < n_v and v_steps[k][1] is None:
-                v_tiles[k] = band_tile(ps_v, "vt_v", v_steps[k][0])
+                v_tiles[k] = band_psum[v_steps[k][0]]
             elif k < n_v:
                 v_tiles[k] = shifted_tile(ps_v, "vt_v", v_steps[k][0], v_steps[k][1])
 
         def make_g_tile(m):
             if m < n_g and g_steps[m][1] is None:
-                g_tiles[m] = band_tile(ps_s, "vt_s", g_steps[m][0])
+                g_tiles[m] = band_psum[g_steps[m][0]]
             elif m < n_g:
                 g_tiles[m] = shifted_tile(ps_s, "vt_s", g_steps[m][0], g_steps[m][1])
 
@@ -429,7 +440,7 @@ def tile_selfattentionmodulev2_pb_kernel(tc, x, attn, v_w, v_b, w_w, w_b, out):
 
         def vector_step(k):
             cursor["v"] = k + 1
-            make_v_tile(k + V_BANKS - 1)
+            make_v_tile(k + V_AHEAD)
             run(pe_tasks, k)
             if k < n_v:
                 vt = v_tiles[k]
@@ -452,7 +463,7 @@ def tile_selfattentionmodulev2_pb_kernel(tc, x, attn, v_w, v_b, w_w, w_b, out):
             run(vec_tasks, k)
 
         def gpsimd_step(m):
-            make_g_tile(m + S_BANKS - 1)
+            make_g_tile(m + S_AHEAD)
             run(g_pe_tasks, m)
             if m < n_g:
                 vt = g_tiles[m]
@@ -490,24 +501,36 @@ def tile_selfattentionmodulev2_pb_kernel(tc, x, attn, v_w, v_b, w_w, w_b, out):
         defer(vec_tasks, 1, lambda: nc.vector.tensor_copy(out=btv[:, :, :, 8], in_=a_t[:, :, :, 4]))
         for idx in range(6):
             defer(pe_tasks, 2 + idx, lambda idx=idx: shift_attn(idx // 2, idx % 2))
-            defer(vec_tasks, 3 + idx, lambda idx=idx: band_column(idx // 2, idx % 2))
-        defer(vec_tasks, 9, skew_band)
+            defer(vec_tasks, 4 + idx, lambda idx=idx: band_column(idx // 2, idx % 2))
+        defer(vec_tasks, 10, skew_band)
+        opened = {}
         for k, st in enumerate(v_steps):
             if st[1] is None:
-                defer(pe_tasks, k - 6, lambda r=st[0]: band_prepare(r))
+                defer(pe_tasks, k - 9, lambda r=st[0]: band_prepare(r))
+                defer(pe_tasks, k - 5, lambda r=st[0]: band_half(r, 0))
+                defer(pe_tasks, k - 5 + HALF_GAP, lambda r=st[0]: band_half(r, 1))
+            for r, n in st[2]:
+                if r not in opened:
+                    opened[r] = k
+                    if BAND_FIRST <= r < BAND_HI:
+                        defer(pe_tasks, k - 10, lambda r=r: band_prepare(r))
+                        defer(pe_tasks, k - 7, lambda r=r: band_half(r, 0))
+                        defer(pe_tasks, k - 7 + HALF_GAP, lambda r=r: band_half(r, 1))
         for m, st in enumerate(g_steps):
             if st[1] is None:
-                defer(g_pe_tasks, m - 3, lambda r=st[0]: band_prepare(r))
-        later_chunk(1, 9, 2)
-        defer(pe_tasks, 10, lambda: ww_grouped.append(transpose_weight(ww_sb, (nc.scalar.copy, nc.scalar.copy))))
-        defer(vec_tasks, 14, lambda: ww_q.append(quantise_weight(ww_grouped[0], "ww")))
-        later_chunk(6, 18, 5)
-        later_chunk(2, 27, 3)
-        later_chunk(5, 36, 4)
-        later_chunk(3, 45, None)
-        later_chunk(4, 54, None)
+                defer(g_pe_tasks, m - 4, lambda r=st[0]: band_prepare(r))
+                defer(g_pe_tasks, m - 2, lambda r=st[0]: band_half(r, 0))
+                defer(g_pe_tasks, m - 1, lambda r=st[0]: band_half(r, 1))
+        later_chunk(2, 2, 3)
+        defer(pe_tasks, 16, lambda: ww_grouped.append(transpose_weight(ww_sb, (nc.scalar.copy, nc.scalar.copy))))
+        defer(vec_tasks, 20, lambda: ww_q.append(quantise_weight(ww_grouped[0], "ww")))
+        later_chunk(1, 10, 6)
+        later_chunk(3, 24, 4)
+        later_chunk(6, 34, 5)
+        later_chunk(4, 44, None)
+        later_chunk(5, 54, None)
 
-        for k in range(V_BANKS - 1):
+        for k in range(V_AHEAD):
             make_v_tile(k)
         iv, ig = 0, 0
         tv, tg = 0.0, 0.0

@@ -27,7 +27,7 @@ S_AHEAD = 1
 V_AHEAD = 2
 HALF_GAP = 1
 V_LAG = 2
-G_START = 3
+G_START = 2
 BAND_LO, BAND_HI = 3, 28
 BAND_FIRST = 8
 BAND_GROUP = 5
@@ -76,7 +76,7 @@ def tile_selfattentionmodulev2_pb_kernel(tc, x, attn, v_w, v_b, w_w, w_b, out):
         wpool = ctx.enter_context(tc.tile_pool(name="wpool", bufs=1))
         xpool = ctx.enter_context(tc.tile_pool(name="xpool", bufs=2))
         accp = ctx.enter_context(tc.tile_pool(name="accp", bufs=11))
-        prodp = ctx.enter_context(tc.tile_pool(name="prodp", bufs=4))
+        prodp = ctx.enter_context(tc.tile_pool(name="prodp", bufs=3))
         cpool = ctx.enter_context(tc.tile_pool(name="cpool", bufs=2))
         gpool = ctx.enter_context(tc.tile_pool(name="gpool", bufs=3))
         opool = ctx.enter_context(tc.tile_pool(name="opool", bufs=2))
@@ -242,6 +242,9 @@ def tile_selfattentionmodulev2_pb_kernel(tc, x, attn, v_w, v_b, w_w, w_b, out):
         regroup_x(7, 0, gpsimd_copy)
         regroup_x(7, 1, gpsimd_copy)
         quantise_x(7)
+        regroup_x(2, 0, gpsimd_copy)
+        regroup_x(2, 1, gpsimd_copy)
+        load_x(3)
 
         total = {}
         for dj in shifts:
@@ -306,14 +309,14 @@ def tile_selfattentionmodulev2_pb_kernel(tc, x, attn, v_w, v_b, w_w, w_b, out):
                         start=True,
                         stop=True,
                     )
+            vector_free = cursor["v"] > n_v
             for j in range(4):
-                nc.scalar.activation(
-                    out=ot[:, j].rearrange("q b r c -> q r b c"),
-                    in_=banks[j // 2][:, j % 2, :].rearrange("q (r b c) -> q r b c", r=2, b=B),
-                    func=ACT.Identity,
-                    bias=wb[:, j : j + 1],
-                    scale=1.0,
-                )
+                dst = ot[:, j].rearrange("q b r c -> q r b c")
+                res = banks[j // 2][:, j % 2, :].rearrange("q (r b c) -> q r b c", r=2, b=B)
+                if vector_free and j % 2 == 1:
+                    nc.vector.tensor_scalar(out=dst, in0=res, scalar1=wb[:, j : j + 1], scalar2=None, op0=ALU.add)
+                else:
+                    nc.scalar.activation(out=dst, in_=res, func=ACT.Identity, bias=wb[:, j : j + 1], scale=1.0)
             for b in range(B):
                 nc.sync.dma_start(
                     out=out[b].rearrange("(q j) r c -> q j (r c)", j=4)[:, :, pair * 2 * W : (pair + 1) * 2 * W],
@@ -398,6 +401,7 @@ def tile_selfattentionmodulev2_pb_kernel(tc, x, attn, v_w, v_b, w_w, w_b, out):
         v_uses = sum([len(st[2]) for st in v_steps])
         g_uses = sum([len(st[2]) for st in g_steps])
         v_tiles, g_tiles = {}, {}
+        acc_g = const.tile([P, H - SPLIT_ROW, C], F32)
         pe_tasks, vec_tasks, g_pe_tasks = {}, {}, {}
         cursor = {"v": 0}
 
@@ -462,26 +466,44 @@ def tile_selfattentionmodulev2_pb_kernel(tc, x, attn, v_w, v_b, w_w, w_b, out):
                         v_row_done(k, r, ctx_row)
             run(vec_tasks, k)
 
+        def weight(r, n):
+            return 1.0 if n is None else a_t[:, r % 8, r // 8, n : n + 1]
+
         def gpsimd_step(m):
             make_g_tile(m + S_AHEAD)
             run(g_pe_tasks, m)
-            if m < n_g:
-                vt = g_tiles[m]
-                for r, n in g_steps[m][2]:
-                    a = 1.0 if n is None else a_t[:, r % 8, r // 8, n : n + 1]
-                    seen[r] = seen.get(r, 0) + 1
-                    if seen[r] == 1:
-                        acc[r] = accp.tile([P, C], F32, tag="acc_g", name="acc_g%d" % r)
-                        nc.scalar.activation(out=acc[r][:], in_=vt[:], func=ACT.Copy, scale=a)
-                        continue
-                    prod = prodp.tile([P, C], F32, tag="prod")
-                    nc.scalar.activation(out=prod[:], in_=vt[:], func=ACT.Copy, scale=a)
-                    if seen[r] < total[r]:
-                        nc.gpsimd.tensor_tensor(out=acc[r][:], in0=acc[r][:], in1=prod[:], op=ALU.add)
-                    else:
-                        ctx_row = cpool.tile([P, C], BF16, tag="ctx_g", name="ctx_g%d" % r)
-                        nc.gpsimd.tensor_tensor(out=ctx_row[:], in0=acc[r][:], in1=prod[:], op=ALU.add)
-                        g_row_done(m, r, ctx_row)
+            if m >= n_g:
+                return
+            vt = g_tiles[m]
+            middle = []
+            for r, n in g_steps[m][2]:
+                seen[r] = seen.get(r, 0) + 1
+                if seen[r] == 1:
+                    nc.scalar.activation(out=acc_g[:, r - SPLIT_ROW, :], in_=vt[:], func=ACT.Copy, scale=weight(r, n))
+                elif seen[r] < total[r]:
+                    middle.append((r, n))
+                else:
+                    prod = prodp.tile([P, 2, C], F32, tag="prod")
+                    nc.scalar.activation(out=prod[:, 0, :], in_=vt[:], func=ACT.Copy, scale=weight(r, n))
+                    ctx_row = cpool.tile([P, C], BF16, tag="ctx_g", name="ctx_g%d" % r)
+                    nc.gpsimd.tensor_tensor(
+                        out=ctx_row[:], in0=acc_g[:, r - SPLIT_ROW, :], in1=prod[:, 0, :], op=ALU.add
+                    )
+                    g_row_done(m, r, ctx_row)
+            for first in range(0, len(middle), 2):
+                group = sorted(middle[first : first + 2])
+                prod = prodp.tile([P, 2, C], F32, tag="prod")
+                for slot, (r, n) in enumerate(group):
+                    nc.scalar.activation(out=prod[:, slot, :], in_=vt[:], func=ACT.Copy, scale=weight(r, n))
+                lo = group[0][0] - SPLIT_ROW
+                if len(group) == 2:
+                    hi = group[1][0] - SPLIT_ROW
+                    rows = acc_g[:, lo : hi + 1 : hi - lo, :]
+                    nc.gpsimd.tensor_tensor(out=rows, in0=rows, in1=prod[:], op=ALU.add)
+                else:
+                    nc.gpsimd.tensor_tensor(
+                        out=acc_g[:, lo, :], in0=acc_g[:, lo, :], in1=prod[:, 0, :], op=ALU.add
+                    )
 
         def later_chunk(s, k0, next_load):
             def regroup():
@@ -495,8 +517,7 @@ def tile_selfattentionmodulev2_pb_kernel(tc, x, attn, v_w, v_b, w_w, w_b, out):
             defer(pe_tasks, k0 + 5, lambda: first_conv(s, (0, 1), False))
             defer(pe_tasks, k0 + 7, lambda: first_conv(s, (2, 3), False))
 
-        defer(pe_tasks, 0, lambda: first_conv(7, (0, 1), False))
-        defer(pe_tasks, 1, lambda: first_conv(7, (2, 3), False))
+        defer(pe_tasks, 0, lambda: first_conv(7, range(4), False))
         defer(pe_tasks, G_START - 1, lambda: make_g_tile(0))
         defer(vec_tasks, 1, lambda: nc.vector.tensor_copy(out=btv[:, :, :, 8], in_=a_t[:, :, :, 4]))
         for idx in range(6):
@@ -521,7 +542,9 @@ def tile_selfattentionmodulev2_pb_kernel(tc, x, attn, v_w, v_b, w_w, w_b, out):
                 defer(g_pe_tasks, m - 4, lambda r=st[0]: band_prepare(r))
                 defer(g_pe_tasks, m - 2, lambda r=st[0]: band_half(r, 0))
                 defer(g_pe_tasks, m - 1, lambda r=st[0]: band_half(r, 1))
-        later_chunk(2, 2, 3)
+        defer(vec_tasks, 2, lambda: quantise_x(2))
+        defer(pe_tasks, 3, lambda: first_conv(2, (0, 1), False))
+        defer(pe_tasks, 5, lambda: first_conv(2, (2, 3), False))
         defer(pe_tasks, 16, lambda: ww_grouped.append(transpose_weight(ww_sb, (nc.scalar.copy, nc.scalar.copy))))
         defer(vec_tasks, 20, lambda: ww_q.append(quantise_weight(ww_grouped[0], "ww")))
         later_chunk(1, 10, 6)

@@ -16,74 +16,81 @@ P = 128
 B, C, H, W = 2, 512, 32, 64
 ROW = B * W
 NPIX = H * ROW
-PAD = 8
 CHUNK_ROWS = 4
 CHUNK = CHUNK_ROWS * ROW
-SPLIT_ROW = 23
-V_BANKS = 3
-S_BANKS = 2
-M_BANKS = 3
-S_AHEAD = 1
-V_AHEAD = 2
-HALF_GAP = 1
-V_LAG = 2
-G_START = 2
 BAND_LO, BAND_HI = 3, 28
-BAND_FIRST = 8
 BAND_GROUP = 5
 APAD = 16
 BAND_W = 144
 BAND_PITCH = P * (BAND_W + 1)
+SHIFTS = (-4, -2, -1, 1, 2, 4)
+LEVEL = {1: 0, 2: 1, 4: 2}
+FIRST_STEP = -3
 
 FLOPS = 2 * 2 * C * C * B * H * W + 2 * 27 * C * B * H * W
+
+
+def in_band(r):
+    return BAND_LO <= r < BAND_HI
+
+
+def group_taps(r, dj):
+    if dj == 0:
+        cand = (-4, -2, -1, 0, 1, 2, 4)
+    else:
+        cand = (-abs(dj), 0, abs(dj))
+    return [di for di in cand if 0 <= r + di < H and not (di == 0 and in_band(r))]
+
+
+def merged_groups(r):
+    if r < BAND_LO:
+        return ()
+    if r >= BAND_HI:
+        return (-4, 4)
+    if r % 2 == 1:
+        return (-4, 4, 2)
+    return (-4, 4)
 
 
 def tile_selfattentionmodulev2_pb_kernel(tc, x, attn, v_w, v_b, w_w, w_b, out):
     nc = tc.nc
 
-    taps = {}
-    for lvl, d in enumerate((1, 2, 4)):
-        for i in range(3):
-            for jj in range(3):
-                di, dj = (i - 1) * d, (jj - 1) * d
-                if di == 0 and dj == 0 and lvl > 0:
-                    continue
-                if dj not in taps:
-                    taps[dj] = []
-                taps[dj].append((di, 9 * lvl + 3 * i + jj))
-    shifts = (0, -1, 1, -2, 2, -4, 4)
-
-    def band_steps(lo, hi, descending):
-        steps = []
-        rows = list(range(max(0, lo - 4), min(H, hi + 4)))
-        if descending:
-            rows = list(reversed(rows))
-        for src in rows:
-            for dj in shifts:
-                uses = [
-                    (src - di, n)
-                    for (di, n) in taps[dj]
-                    if lo <= src - di < hi and not (di == 0 and BAND_LO <= src < BAND_HI)
-                ]
-                if uses:
-                    steps.append((src, dj, uses))
-            if lo <= src < hi and BAND_LO <= src < BAND_HI and (descending or src < BAND_FIRST):
-                steps.append((src, None, [(src, None)]))
-        return steps
+    vec_plan, prod_plan, row_terms = {}, {}, {}
+    for r in range(H):
+        plain, joined = [], []
+        for dj in SHIFTS:
+            taps = group_taps(r, dj)
+            if dj in merged_groups(r) and len(taps) > 1:
+                step = max(FIRST_STEP, r + taps[1] - 1)
+                prod_plan.setdefault(step, []).append((r, dj, taps[0], True))
+                for di in taps[1:]:
+                    vec_plan.setdefault(r + di, []).append((r, dj, di))
+                joined.append((taps[-1], dj))
+            else:
+                for di in taps:
+                    prod_plan.setdefault(r + 3, []).append((r, dj, di, False))
+                    plain.append((r, dj, di))
+        for di in group_taps(r, 0):
+            vec_plan.setdefault(r + di, []).append((r, 0, di))
+        row_terms[r] = plain + [(r, dj, None) for (last, dj) in sorted(joined)] + [(r, 0, None)]
+    for step in vec_plan:
+        vec_plan[step] = sorted(vec_plan[step], key=lambda tap: (-tap[2], tap[1] == 0))
+    for step in prod_plan:
+        prod_plan[step] = sorted(prod_plan[step], key=lambda tap: not tap[3])
 
     with ExitStack() as ctx:
         const = ctx.enter_context(tc.tile_pool(name="const", bufs=1))
         wpool = ctx.enter_context(tc.tile_pool(name="wpool", bufs=1))
         xpool = ctx.enter_context(tc.tile_pool(name="xpool", bufs=2))
-        accp = ctx.enter_context(tc.tile_pool(name="accp", bufs=11))
-        prodp = ctx.enter_context(tc.tile_pool(name="prodp", bufs=3))
-        cpool = ctx.enter_context(tc.tile_pool(name="cpool", bufs=2))
+        vpool = ctx.enter_context(tc.tile_pool(name="vpool", bufs=12))
+        upool = ctx.enter_context(tc.tile_pool(name="upool", bufs=11))
+        mpool = ctx.enter_context(tc.tile_pool(name="mpool", bufs=14))
+        ppool = ctx.enter_context(tc.tile_pool(name="ppool", bufs=20))
         gpool = ctx.enter_context(tc.tile_pool(name="gpool", bufs=3))
         opool = ctx.enter_context(tc.tile_pool(name="opool", bufs=2))
-        bpool = ctx.enter_context(tc.tile_pool(name="bpool", bufs=3))
-        ps_v = ctx.enter_context(tc.psum_pool(name="ps_v", bufs=V_BANKS))
-        ps_s = ctx.enter_context(tc.psum_pool(name="ps_s", bufs=S_BANKS))
-        ps_m = ctx.enter_context(tc.psum_pool(name="ps_m", bufs=M_BANKS))
+        ps_v = ctx.enter_context(tc.psum_pool(name="ps_v", bufs=4))
+        ps_c = ctx.enter_context(tc.psum_pool(name="ps_c", bufs=2))
+        ps_o = ctx.enter_context(tc.psum_pool(name="ps_o", bufs=2))
         ctx.enter_context(tc.manual_schedule())
 
         def load_weight(w_dram, label):
@@ -96,7 +103,7 @@ def tile_selfattentionmodulev2_pb_kernel(tc, x, attn, v_w, v_b, w_w, w_b, out):
             grouped = wpool.tile([P, 4 * C], BF16, tag="w_grouped", align_bytes=64)
             gwords = grouped[:].bitcast(F32).rearrange("q (j o u) -> q j o u", j=4, u=2)
             for half in range(2):
-                pt = ps_m.tile([P, 4, P], F32, tag="mx")
+                pt = ps_o.tile([P, 4, P], F32, tag="o")
                 for a in range(2):
                     for u in range(2):
                         nc.tensor.transpose(pt[:, 2 * a + u, :], words[:, 2 * half + a, u, :], ident_f[:])
@@ -112,7 +119,7 @@ def tile_selfattentionmodulev2_pb_kernel(tc, x, attn, v_w, v_b, w_w, w_b, out):
         raw_tiles, gx_tiles = {}, {}
 
         def load_x(s):
-            raw_tiles[s] = xpool.tile([P, B, 4, CHUNK_ROWS * W], BF16, tag="raw", name="raw%d" % s, bufs=4)
+            raw_tiles[s] = xpool.tile([P, B, 4, CHUNK_ROWS * W], BF16, tag="raw", name="raw%d" % s, bufs=3)
             for b in range(B):
                 nc.sync.dma_start(
                     out=raw_tiles[s][:, b],
@@ -134,25 +141,6 @@ def tile_selfattentionmodulev2_pb_kernel(tc, x, attn, v_w, v_b, w_w, w_b, out):
                 in_=gx_tiles[s][:].rearrange("q r b c j -> q (r b c j)"),
             )
 
-        def first_conv(s, chunks, vector_helps):
-            pix = slice(s * CHUNK, (s + 1) * CHUNK)
-            for j in chunks:
-                ps = ps_m.tile([P, CHUNK], F32, tag="mx")
-                nc.tensor.matmul_mx(
-                    out=ps[:],
-                    lhsT=vw_codes[:, j * P : (j + 1) * P].bitcast(FP8X4),
-                    lhsT_scale=vw_plane[:, j * P : (j + 1) * P],
-                    rhs=x_codes[:, pix].bitcast(FP8X4),
-                    rhs_scale=x_plane[:, pix],
-                    start=True,
-                    stop=True,
-                )
-                dst = val[:, j, PAD + s * CHUNK : PAD + (s + 1) * CHUNK]
-                if vector_helps and j % 2 == 1:
-                    nc.vector.tensor_scalar(out=dst, in0=ps[:], scalar1=vb[:, j : j + 1], scalar2=None, op0=ALU.add)
-                else:
-                    nc.scalar.activation(out=dst, in_=ps[:], func=ACT.Identity, bias=vb[:, j : j + 1], scale=1.0)
-
         ident_f = const.tile([P, P], F32)
         make_identity(nc, ident_f[:])
         ident_b = const.tile([P, P], BF16)
@@ -164,9 +152,6 @@ def tile_selfattentionmodulev2_pb_kernel(tc, x, attn, v_w, v_b, w_w, w_b, out):
         zeros = const.tile([P, BAND_W + 1], F32)
         nc.gpsimd.memset(zeros[:], 0.0)
         scratch = out.rearrange("b o r c -> (b o r c)")
-        val = const.tile([P, 4, NPIX + 2 * PAD], F32)
-        nc.vector.memset(val[:, :, 0:PAD], 0.0)
-        nc.vector.memset(val[:, :, PAD + NPIX : PAD + NPIX + PAD], 0.0)
         x_codes = const.tile([P, NPIX], U32, align_bytes=64)
         x_plane = const.tile([P, NPIX], U8, align_bytes=64)
 
@@ -178,19 +163,18 @@ def tile_selfattentionmodulev2_pb_kernel(tc, x, attn, v_w, v_b, w_w, w_b, out):
                 in_=attn[b, :, 8 * g : 8 * g + 8, :],
             )
 
-        vb_bf = const.tile([P, 4], BF16)
         wb_bf = const.tile([P, 4], BF16)
-        nc.scalar.dma_start(out=vb_bf[:], in_=v_b.rearrange("(q j) -> q j", j=4))
+        vb_raw = const.tile([P, C], BF16)
         nc.scalar.dma_start(out=wb_bf[:], in_=w_b.rearrange("(q j) -> q j", j=4))
         vw_sb = load_weight(v_w, "vw")
         load_x(0)
         for g in range(4):
             load_attn(nc.scalar, g, 0)
             load_attn(nc.sync, g, 1)
-        load_x(7)
-        load_x(2)
+        nc.scalar.dma_start(out=vb_raw[:], in_=v_b.partition_broadcast(P))
         load_x(1)
         ww_sb = load_weight(w_w, "ww")
+        load_x(2)
         for ri in range(BAND_HI - BAND_LO):
             nc.sync.dma_start(
                 out=scratch[ri * BAND_PITCH : (ri + 1) * BAND_PITCH].rearrange("(p f) -> p f", p=P), in_=zeros[:]
@@ -200,16 +184,20 @@ def tile_selfattentionmodulev2_pb_kernel(tc, x, attn, v_w, v_b, w_w, w_b, out):
         regroup_x(0, 0, nc.vector.tensor_copy)
         regroup_x(0, 1, nc.scalar.copy)
         vw_codes, vw_plane = quantise_weight(vw_grouped, "vw")
-        vb = const.tile([P, 4], F32)
-        wb = const.tile([P, 4], F32)
-        nc.vector.tensor_copy(out=vb[:], in_=vb_bf[:])
-        nc.vector.tensor_copy(out=wb[:], in_=wb_bf[:])
         quantise_x(0)
 
-        pa = ps_m.tile([P, 8, P], BF16, tag="mx")
+        rot = {0: ident_f}
+        for dj in SHIFTS:
+            rot[dj] = const.tile([P, P], F32, name="rot%d" % (dj + 4))
+            cut = dj % P
+            nc.gpsimd.tensor_copy(out=rot[dj][:, 0 : P - cut], in_=ident_f[:, cut:P])
+            nc.gpsimd.tensor_copy(out=rot[dj][:, P - cut : P], in_=ident_f[:, 0:cut])
+        vb_all = const.tile([P, 4, P], F32)
+        nc.gpsimd.tensor_copy(out=vb_all[:], in_=vb_raw[:].rearrange("p (q j) -> p j q", j=4))
+
+        pa = ps_c.tile([P, 8, P], BF16, tag="ctx")
         for i in range(8):
             nc.tensor.transpose(pa[:, i, :], at3[:, APAD + i * ROW : APAD + (i + 1) * ROW], ident_b[:])
-        first_conv(0, range(4), False)
         a_t = const.tile([P, 8, 4, 32], F32)
         nc.vector.tensor_copy(out=a_t[:].rearrange("p i g n -> p i (g n)"), in_=pa[:])
         mk = const.tile([P, 8], F32)
@@ -233,52 +221,156 @@ def tile_selfattentionmodulev2_pb_kernel(tc, x, attn, v_w, v_b, w_w, w_b, out):
                     scalar2=None,
                     op0=ALU.mult,
                 )
+        for lvl, d in enumerate((1, 2, 4)):
+            nc.vector.memset(a_t[:, 0:d, 0, 9 * lvl : 9 * lvl + 3], 0.0)
+            nc.vector.memset(a_t[:, 8 - d : 8, 3, 9 * lvl + 6 : 9 * lvl + 9], 0.0)
+        a_sum = const.tile([P, 8, 4], F32)
+        nc.vector.tensor_reduce(out=a_sum[:], in_=a_t[:, :, :, 0:27], axis=AX.X, op=ALU.add)
         for n in (13, 22):
             nc.vector.tensor_tensor(out=a_t[:, :, :, 4], in0=a_t[:, :, :, 4], in1=a_t[:, :, :, n], op=ALU.add)
+        wb = const.tile([P, 4], F32)
+        nc.vector.tensor_copy(out=wb[:], in_=wb_bf[:])
 
-        def gpsimd_copy(out, in_):
-            nc.gpsimd.tensor_scalar(out=out, in0=in_, scalar1=1.0, scalar2=0.0, op0=ALU.mult, op1=ALU.add)
+        btv = bt[:].rearrange("p (g i) j -> p i g j", g=4)
+        as_w = {}
+        nc.gpsimd.tensor_copy(out=btv[:, :, :, 8], in_=a_t[:, :, :, 4])
+        for idx, dj in enumerate(SHIFTS):
+            lvl, side = LEVEL[abs(dj)], (1 if dj > 0 else 0)
+            if idx % 2 == 0:
+                pa_s = ps_o.tile([P, 8, P], BF16, tag="o")
+            else:
+                pa_s = ps_c.tile([P, 8, P], BF16, tag="ctx")
+            for i in range(8):
+                nc.tensor.transpose(
+                    pa_s[:, i, :], at3[:, APAD + i * ROW - dj : APAD + (i + 1) * ROW - dj], ident_b[:]
+                )
+            as_w[dj] = const.tile([P, 8, 4, 4], F32, name="as_w%d" % (dj + 4))
+            first = 9 * lvl + 2 * side
+            nc.vector.tensor_scalar(
+                out=as_w[dj][:, :, :, 0:3],
+                in0=pa_s[:].rearrange("p i (g n) -> p i g n", g=4)[:, :, :, first : first + 7 : 3],
+                scalar1=mk[:, 2 * lvl + 1 - side : 2 * lvl + 2 - side],
+                scalar2=None,
+                op0=ALU.mult,
+            )
+            nc.gpsimd.tensor_copy(out=btv[:, :, :, 8 - dj], in_=as_w[dj][:, :, :, 1])
 
-        regroup_x(7, 0, gpsimd_copy)
-        regroup_x(7, 1, gpsimd_copy)
-        quantise_x(7)
-        regroup_x(2, 0, gpsimd_copy)
-        regroup_x(2, 1, gpsimd_copy)
-        load_x(3)
+        a_band = []
+        n_band = BAND_HI - BAND_LO
+        nc.sync.dma_start(
+            out=scratch[0 : n_band * BAND_PITCH].rearrange("(r p t) -> p r t", p=P, t=BAND_W + 1)[:, :, 0:16],
+            in_=bt[:, BAND_LO:BAND_HI, :],
+        )
+        for q in range(n_band // BAND_GROUP):
+            a_q = const.tile([P, BAND_GROUP, BAND_W], F32, name="a_band%d" % q)
+            nc.sync.dma_start(
+                out=a_q[:],
+                in_=scratch[q * BAND_GROUP * BAND_PITCH : (q + 1) * BAND_GROUP * BAND_PITCH]
+                .rearrange("(r m) -> r m", m=BAND_PITCH)[:, 0 : P * BAND_W]
+                .rearrange("r (p c) -> p r c", c=BAND_W),
+            )
+            a_band.append(a_q)
 
-        total = {}
-        for dj in shifts:
-            for di, n in taps[dj]:
-                for r in range(H):
-                    if 0 <= r + di < H:
-                        total[r] = total.get(r, 0) + 1
-        for r in range(BAND_LO, BAND_HI):
-            total[r] -= 6
-        seen = {}
-        acc = {}
-        pair_tiles = {}
-        pair_done = {}
-        pair_codes = {}
+        def weight(r, di, dj):
+            if dj == 0:
+                n = 4 if di == 0 else 9 * LEVEL[abs(di)] + (0 if di < 0 else 6) + 1
+                return a_t[:, r % 8, r // 8, n : n + 1]
+            pos = 1 + di // abs(dj)
+            return as_w[dj][:, r % 8, r // 8, pos : pos + 1]
+
+        v_ps, v_sb, sums = {}, {}, {}
+        pair_tiles, pair_codes, pair_banks = {}, {}, {}
         ww_grouped, ww_q = [], []
 
-        def row_to_words(r, ctx_row):
+        def first_conv(s):
+            pix = slice(s * ROW, (s + 1) * ROW)
+            v_ps[s] = ps_v.tile([P, C], F32, tag="v0", name="v_ps%d" % s)
+            nc.tensor.matmul_mx(
+                out=v_ps[s][:],
+                lhsT=x_codes[:, pix].bitcast(FP8X4),
+                lhsT_scale=x_plane[:, pix],
+                rhs=vw_codes[:].bitcast(FP8X4),
+                rhs_scale=vw_plane[:],
+                start=True,
+                stop=True,
+            )
+
+        def copy_value(s):
+            v_sb[s] = vpool.tile([P, C], F32, tag="v_sb", name="v_sb%d" % s)
+            nc.scalar.copy(out=v_sb[s][:], in_=v_ps[s][:])
+
+        def start_row(r):
+            sums[(r, 0, None)] = upool.tile([P, C], F32, tag="u0", name="u0_%d" % r)
+            nc.gpsimd.tensor_scalar(
+                out=sums[(r, 0, None)][:],
+                in0=vb_all[:].rearrange("p j q -> p (j q)"),
+                scalar1=a_sum[:, r % 8, r // 8 : r // 8 + 1],
+                scalar2=0.0,
+                op0=ALU.mult,
+                op1=ALU.add,
+            )
+
+        def product(r, dj, di, joined, on_gpsimd):
+            if joined:
+                key = (r, dj, None)
+                sums[key] = mpool.tile([P, C], F32, tag="um", name="um_%d_%d" % (r, dj + 4))
+            else:
+                key = (r, dj, di)
+                sums[key] = ppool.tile([P, C], F32, tag="pr", name="pr_%d_%d_%d" % (r, dj + 4, di + 4))
+            if on_gpsimd:
+                nc.gpsimd.tensor_scalar(
+                    out=sums[key][:],
+                    in0=v_sb[r + di][:],
+                    scalar1=weight(r, di, dj),
+                    scalar2=0.0,
+                    op0=ALU.mult,
+                    op1=ALU.add,
+                )
+            else:
+                nc.scalar.activation(out=sums[key][:], in_=v_sb[r + di][:], func=ACT.Copy, scale=weight(r, di, dj))
+
+        def vector_tap(r, dj, di):
+            acc = sums[(r, dj, None)]
+            nc.vector.scalar_tensor_tensor(
+                out=acc[:], in0=v_ps[r + di][:], scalar=weight(r, di, dj), in1=acc[:], op0=ALU.mult, op1=ALU.add
+            )
+
+        ctx_banks = {}
+
+        def add_up(r):
+            ct = ps_c.tile([P, 4, P], F32, tag="ctx", name="ct%d" % r)
+            ctx_banks[r] = ct
+            keys = row_terms[r]
+            count = len(keys) + (1 if in_band(r) else 0)
+            done = 0
+            if in_band(r):
+                ri = r - BAND_LO
+                for j in range(4):
+                    nc.tensor.matmul(
+                        out=ct[:, j, :],
+                        lhsT=v_sb[r][:, j * P : (j + 1) * P],
+                        rhs=a_band[ri // BAND_GROUP][:, ri % BAND_GROUP, 8 : 8 + P],
+                        start=(j == 0),
+                        stop=False,
+                    )
+                done = 1
+            for key in keys:
+                done += 1
+                for j in range(4):
+                    nc.tensor.matmul(
+                        out=ct[:, j, :],
+                        lhsT=sums[key][:, j * P : (j + 1) * P],
+                        rhs=rot[key[1]][:],
+                        is_transpose=True,
+                        start=(done == 1 and j == 0),
+                        stop=(done == count and j == 3),
+                    )
+
+        def round_context(r):
             pair = r // 2
             if pair not in pair_tiles:
-                if 2 * pair < SPLIT_ROW < 2 * pair + 2:
-                    pair_tiles[pair] = gpool.tile(
-                        [P, 2, ROW, 4], BF16, tag="g2_split", name="g2_split", bufs=1, align_bytes=64
-                    )
-                else:
-                    pair_tiles[pair] = gpool.tile(
-                        [P, 2, ROW, 4], BF16, tag="g2", name="g2_%d" % pair, bufs=4, align_bytes=64
-                    )
-                pair_done[pair] = 0
-            ct = ps_m.tile([P, 4, P], BF16, tag="mx")
-            for j in range(4):
-                nc.tensor.transpose(ct[:, j, :], ctx_row[:, j * P : (j + 1) * P], ident_b[:])
-            nc.scalar.copy(out=pair_tiles[pair][:, r % 2], in_=ct[:].rearrange("q j x -> q x j"))
-            pair_done[pair] += 1
-            return pair_done[pair] == 2
+                pair_tiles[pair] = gpool.tile([P, 2, ROW, 4], BF16, tag="g2", name="g2_%d" % pair, align_bytes=64)
+            nc.scalar.copy(out=pair_tiles[pair][:, r % 2], in_=ctx_banks[r][:].rearrange("q j x -> q x j"))
 
         def quantise_pair(pair):
             c_codes = gpool.tile([P, 2 * ROW], U32, tag="c_codes", name="c_codes%d" % pair, align_bytes=64)
@@ -293,10 +385,9 @@ def tile_selfattentionmodulev2_pb_kernel(tc, x, attn, v_w, v_b, w_w, w_b, out):
         def second_conv(pair):
             c_codes, c_plane = pair_codes[pair]
             ww_codes, ww_plane = ww_q[0]
-            ot = opool.tile([P, 4, B, 2, W], F32, tag="ot")
             banks = []
             for half in range(2):
-                po = ps_m.tile([P, 2, 2 * ROW], F32, tag="mx")
+                po = ps_o.tile([P, 2, 2 * ROW], F32, tag="o")
                 banks.append(po)
                 for a in range(2):
                     j = 2 * half + a
@@ -309,263 +400,55 @@ def tile_selfattentionmodulev2_pb_kernel(tc, x, attn, v_w, v_b, w_w, w_b, out):
                         start=True,
                         stop=True,
                     )
-            vector_free = cursor["v"] > n_v
+            pair_banks[pair] = banks
+
+        def store_pair(pair):
+            banks = pair_banks[pair]
+            ot = opool.tile([P, 4, B, 2, W], F32, tag="ot")
             for j in range(4):
                 dst = ot[:, j].rearrange("q b r c -> q r b c")
                 res = banks[j // 2][:, j % 2, :].rearrange("q (r b c) -> q r b c", r=2, b=B)
-                if vector_free and j % 2 == 1:
-                    nc.vector.tensor_scalar(out=dst, in0=res, scalar1=wb[:, j : j + 1], scalar2=None, op0=ALU.add)
-                else:
-                    nc.scalar.activation(out=dst, in_=res, func=ACT.Identity, bias=wb[:, j : j + 1], scale=1.0)
+                nc.scalar.activation(out=dst, in_=res, func=ACT.Identity, bias=wb[:, j : j + 1], scale=1.0)
             for b in range(B):
                 nc.sync.dma_start(
                     out=out[b].rearrange("(q j) r c -> q j (r c)", j=4)[:, :, pair * 2 * W : (pair + 1) * 2 * W],
                     in_=ot[:, :, b].rearrange("q j r c -> q j (r c)"),
                 )
 
-        def shifted_tile(pool, tag, src, dj):
-            vt = pool.tile([P, C], F32, tag=tag)
-            start = PAD + src * ROW + dj
-            for j in range(4):
-                nc.tensor.transpose(vt[:, j * P : (j + 1) * P], val[:, j, start : start + ROW], ident_f[:])
-            return vt
-
-        btv = bt[:].rearrange("p (g i) j -> p i g j", g=4)
-        shifted_attn = {}
-        a_band = []
-        band_rhs = {}
-
-        def shift_attn(lvl, side):
-            dj = (2 * side - 1) * (1, 2, 4)[lvl]
-            pa_s = ps_m.tile([P, 8, P], BF16, tag="mx")
-            for i in range(8):
-                nc.tensor.transpose(
-                    pa_s[:, i, :], at3[:, APAD + i * ROW - dj : APAD + (i + 1) * ROW - dj], ident_b[:]
-                )
-            shifted_attn[(lvl, side)] = pa_s
-
-        def band_column(lvl, side):
-            dj = (2 * side - 1) * (1, 2, 4)[lvl]
-            n = 9 * lvl + 3 + 2 * side
-            nc.vector.tensor_scalar(
-                out=btv[:, :, :, 8 - dj],
-                in0=shifted_attn[(lvl, side)][:].rearrange("p i (g n) -> p i g n", g=4)[:, :, :, n],
-                scalar1=mk[:, 2 * lvl + 1 - side : 2 * lvl + 2 - side],
-                scalar2=None,
-                op0=ALU.mult,
-            )
-
-        def skew_band():
-            n_band = BAND_HI - BAND_LO
-            nc.sync.dma_start(
-                out=scratch[0 : n_band * BAND_PITCH].rearrange("(r p t) -> p r t", p=P, t=BAND_W + 1)[:, :, 0:16],
-                in_=bt[:, BAND_LO:BAND_HI, :],
-            )
-            for q in range(n_band // BAND_GROUP):
-                a_q = const.tile([P, BAND_GROUP, BAND_W], F32, name="a_band%d" % q)
-                nc.sync.dma_start(
-                    out=a_q[:],
-                    in_=scratch[q * BAND_GROUP * BAND_PITCH : (q + 1) * BAND_GROUP * BAND_PITCH]
-                    .rearrange("(r m) -> r m", m=BAND_PITCH)[:, 0 : P * BAND_W]
-                    .rearrange("r (p c) -> p r c", c=BAND_W),
-                )
-                a_band.append(a_q)
-
-        def band_prepare(r):
-            pt = shifted_tile(ps_m, "mx", r, 0)
-            band_rhs[r] = bpool.tile([P, C], F32, tag="vt0", name="vt0_%d" % r)
-            nc.scalar.copy(out=band_rhs[r][:], in_=pt[:])
-
-        band_psum = {}
-
-        def band_half(r, half):
-            if half == 0:
-                band_psum[r] = ps_m.tile([P, C], F32, tag="mx", name="pb%d" % r)
-            ri = r - BAND_LO
-            cols = slice(half * (C // 2), (half + 1) * (C // 2))
-            nc.tensor.matmul(
-                out=band_psum[r][:, cols],
-                lhsT=a_band[ri // BAND_GROUP][:, ri % BAND_GROUP, 8 : 8 + P],
-                rhs=band_rhs[r][:, cols],
-                start=True,
-                stop=True,
-            )
-            if half == 1 and BAND_FIRST <= r < SPLIT_ROW:
-                acc[r] = accp.tile([P, C], F32, tag="acc_v", name="acc_v%d" % r)
-                nc.scalar.copy(out=acc[r][:], in_=band_psum[r][:])
-                seen[r] = 1
-
-        v_steps = band_steps(0, SPLIT_ROW, False)
-        g_steps = band_steps(SPLIT_ROW, H, True)
-        n_v, n_g = len(v_steps), len(g_steps)
-        v_uses = sum([len(st[2]) for st in v_steps])
-        g_uses = sum([len(st[2]) for st in g_steps])
-        v_tiles, g_tiles = {}, {}
-        acc_g = const.tile([P, H - SPLIT_ROW, C], F32)
-        pe_tasks, vec_tasks, g_pe_tasks = {}, {}, {}
-        cursor = {"v": 0}
-
-        def defer(table, key, fn):
-            if key not in table:
-                table[key] = []
-            table[key].append(fn)
-
-        def run(table, key):
-            for fn in table.get(key, []):
-                fn()
-
-        def make_v_tile(k):
-            if k < n_v and v_steps[k][1] is None:
-                v_tiles[k] = band_psum[v_steps[k][0]]
-            elif k < n_v:
-                v_tiles[k] = shifted_tile(ps_v, "vt_v", v_steps[k][0], v_steps[k][1])
-
-        def make_g_tile(m):
-            if m < n_g and g_steps[m][1] is None:
-                g_tiles[m] = band_psum[g_steps[m][0]]
-            elif m < n_g:
-                g_tiles[m] = shifted_tile(ps_s, "vt_s", g_steps[m][0], g_steps[m][1])
-
-        def v_row_done(k, r, ctx_row):
-            def words():
-                if row_to_words(r, ctx_row):
-                    defer(vec_tasks, k + 1 + V_LAG, lambda: quantise_pair(r // 2))
-                    defer(pe_tasks, k + 2 + V_LAG, lambda: second_conv(r // 2))
-
-            defer(pe_tasks, k + 1, words)
-
-        def g_row_done(m, r, ctx_row):
-            def words():
-                if row_to_words(r, ctx_row):
-                    defer(vec_tasks, cursor["v"] + 1, lambda: quantise_pair(r // 2))
-                    defer(pe_tasks, cursor["v"] + 2, lambda: second_conv(r // 2))
-
-            defer(g_pe_tasks, m + 2, words)
-
-        def vector_step(k):
-            cursor["v"] = k + 1
-            make_v_tile(k + V_AHEAD)
-            run(pe_tasks, k)
-            if k < n_v:
-                vt = v_tiles[k]
-                for r, n in v_steps[k][2]:
-                    a = 1.0 if n is None else a_t[:, r % 8, r // 8, n : n + 1]
-                    seen[r] = seen.get(r, 0) + 1
-                    if seen[r] == 1:
-                        acc[r] = accp.tile([P, C], F32, tag="acc_v", name="acc_v%d" % r)
-                        nc.vector.tensor_scalar(out=acc[r][:], in0=vt[:], scalar1=a, scalar2=None, op0=ALU.mult)
-                    elif seen[r] < total[r]:
-                        nc.vector.scalar_tensor_tensor(
-                            out=acc[r][:], in0=vt[:], scalar=a, in1=acc[r][:], op0=ALU.mult, op1=ALU.add
-                        )
-                    else:
-                        ctx_row = cpool.tile([P, C], BF16, tag="ctx_v", name="ctx_v%d" % r)
-                        nc.vector.scalar_tensor_tensor(
-                            out=ctx_row[:], in0=vt[:], scalar=a, in1=acc[r][:], op0=ALU.mult, op1=ALU.add
-                        )
-                        v_row_done(k, r, ctx_row)
-            run(vec_tasks, k)
-
-        def weight(r, n):
-            return 1.0 if n is None else a_t[:, r % 8, r // 8, n : n + 1]
-
-        def gpsimd_step(m):
-            make_g_tile(m + S_AHEAD)
-            run(g_pe_tasks, m)
-            if m >= n_g:
-                return
-            vt = g_tiles[m]
-            middle = []
-            for r, n in g_steps[m][2]:
-                seen[r] = seen.get(r, 0) + 1
-                if seen[r] == 1:
-                    nc.scalar.activation(out=acc_g[:, r - SPLIT_ROW, :], in_=vt[:], func=ACT.Copy, scale=weight(r, n))
-                elif seen[r] < total[r]:
-                    middle.append((r, n))
-                else:
-                    prod = prodp.tile([P, 2, C], F32, tag="prod")
-                    nc.scalar.activation(out=prod[:, 0, :], in_=vt[:], func=ACT.Copy, scale=weight(r, n))
-                    ctx_row = cpool.tile([P, C], BF16, tag="ctx_g", name="ctx_g%d" % r)
-                    nc.gpsimd.tensor_tensor(
-                        out=ctx_row[:], in0=acc_g[:, r - SPLIT_ROW, :], in1=prod[:, 0, :], op=ALU.add
-                    )
-                    g_row_done(m, r, ctx_row)
-            for first in range(0, len(middle), 2):
-                group = sorted(middle[first : first + 2])
-                prod = prodp.tile([P, 2, C], F32, tag="prod")
-                for slot, (r, n) in enumerate(group):
-                    nc.scalar.activation(out=prod[:, slot, :], in_=vt[:], func=ACT.Copy, scale=weight(r, n))
-                lo = group[0][0] - SPLIT_ROW
-                if len(group) == 2:
-                    hi = group[1][0] - SPLIT_ROW
-                    rows = acc_g[:, lo : hi + 1 : hi - lo, :]
-                    nc.gpsimd.tensor_tensor(out=rows, in0=rows, in1=prod[:], op=ALU.add)
-                else:
-                    nc.gpsimd.tensor_tensor(
-                        out=acc_g[:, lo, :], in0=acc_g[:, lo, :], in1=prod[:, 0, :], op=ALU.add
-                    )
-
-        def later_chunk(s, k0, next_load):
-            def regroup():
-                regroup_x(s, 0, nc.scalar.copy)
-                regroup_x(s, 1, nc.scalar.copy)
-                if next_load is not None:
-                    load_x(next_load)
-
-            defer(pe_tasks, k0, regroup)
-            defer(vec_tasks, k0 + 4, lambda: quantise_x(s))
-            defer(pe_tasks, k0 + 5, lambda: first_conv(s, (0, 1), False))
-            defer(pe_tasks, k0 + 7, lambda: first_conv(s, (2, 3), False))
-
-        defer(pe_tasks, 0, lambda: first_conv(7, range(4), False))
-        defer(pe_tasks, G_START - 1, lambda: make_g_tile(0))
-        defer(vec_tasks, 1, lambda: nc.vector.tensor_copy(out=btv[:, :, :, 8], in_=a_t[:, :, :, 4]))
-        for idx in range(6):
-            defer(pe_tasks, 2 + idx, lambda idx=idx: shift_attn(idx // 2, idx % 2))
-            defer(vec_tasks, 4 + idx, lambda idx=idx: band_column(idx // 2, idx % 2))
-        defer(vec_tasks, 10, skew_band)
-        opened = {}
-        for k, st in enumerate(v_steps):
-            if st[1] is None:
-                defer(pe_tasks, k - 9, lambda r=st[0]: band_prepare(r))
-                defer(pe_tasks, k - 5, lambda r=st[0]: band_half(r, 0))
-                defer(pe_tasks, k - 5 + HALF_GAP, lambda r=st[0]: band_half(r, 1))
-            for r, n in st[2]:
-                if r not in opened:
-                    opened[r] = k
-                    if BAND_FIRST <= r < BAND_HI:
-                        defer(pe_tasks, k - 10, lambda r=r: band_prepare(r))
-                        defer(pe_tasks, k - 7, lambda r=r: band_half(r, 0))
-                        defer(pe_tasks, k - 7 + HALF_GAP, lambda r=r: band_half(r, 1))
-        for m, st in enumerate(g_steps):
-            if st[1] is None:
-                defer(g_pe_tasks, m - 4, lambda r=st[0]: band_prepare(r))
-                defer(g_pe_tasks, m - 2, lambda r=st[0]: band_half(r, 0))
-                defer(g_pe_tasks, m - 1, lambda r=st[0]: band_half(r, 1))
-        defer(vec_tasks, 2, lambda: quantise_x(2))
-        defer(pe_tasks, 3, lambda: first_conv(2, (0, 1), False))
-        defer(pe_tasks, 5, lambda: first_conv(2, (2, 3), False))
-        defer(pe_tasks, 16, lambda: ww_grouped.append(transpose_weight(ww_sb, (nc.scalar.copy, nc.scalar.copy))))
-        defer(vec_tasks, 20, lambda: ww_q.append(quantise_weight(ww_grouped[0], "ww")))
-        later_chunk(1, 10, 6)
-        later_chunk(3, 24, 4)
-        later_chunk(6, 34, 5)
-        later_chunk(4, 44, None)
-        later_chunk(5, 54, None)
-
-        for k in range(V_AHEAD):
-            make_v_tile(k)
-        iv, ig = 0, 0
-        tv, tg = 0.0, 0.0
-        for step in range(n_v + n_g + 3):
-            take_v = ig >= n_g + 3 or iv < G_START or (iv < n_v and tv <= tg)
-            if take_v:
-                vector_step(iv)
-                tv += len(v_steps[iv][2]) / v_uses
-                iv += 1
-            else:
-                gpsimd_step(ig)
-                tg += (len(g_steps[ig][2]) if ig < n_g else 1) / g_uses
-                ig += 1
-        for k in range(n_v, n_v + 2 * V_LAG + 4):
-            vector_step(k)
+        for t in range(FIRST_STEP, H + 6):
+            pair = (t - 7) // 2
+            if t % 2 == 1:
+                for s in (t + 2, t + 3):
+                    if 0 <= s < H:
+                        first_conv(s)
+                if 0 <= pair < H // 2:
+                    second_conv(pair)
+            if t == 0:
+                ww_grouped.append(transpose_weight(ww_sb, (nc.scalar.copy, nc.scalar.copy)))
+            if 0 <= t - 5 < H:
+                round_context(t - 5)
+            if 0 <= t + 2 < H:
+                copy_value(t + 2)
+            if t % 2 == 1 and 0 <= pair < H // 2:
+                store_pair(pair)
+            for r, dj, di in vec_plan.get(t, []):
+                vector_tap(r, dj, di)
+            if t % 2 == 0 and 0 <= (t - 6) // 2 < H // 2:
+                quantise_pair((t - 6) // 2)
+            if t == 1:
+                ww_q.append(quantise_weight(ww_grouped[0], "ww"))
+            if 0 <= t - 4 < H:
+                add_up(t - 4)
+            for r in range(H):
+                if max(FIRST_STEP, r - 5) == t:
+                    start_row(r)
+            for k, (r, dj, di, joined) in enumerate(prod_plan.get(t, [])):
+                product(r, dj, di, joined, k % 2 == 0)
+            chunk, phase = (t + 7) // 4, (t + 7) % 4
+            if 1 <= chunk < H // CHUNK_ROWS:
+                if phase < 2:
+                    regroup_x(chunk, phase, nc.vector.tensor_copy if chunk == 1 else nc.scalar.copy)
+                    if phase == 1 and chunk + 2 < H // CHUNK_ROWS:
+                        load_x(chunk + 2)
+                if phase == 2:
+                    quantise_x(chunk)

@@ -341,29 +341,26 @@ def tile_selfattentionmodulev2_pb_kernel(tc, x, attn, v_w, v_b, w_w, w_b, out):
             ct = ps_c.tile([P, 4, P], F32, tag="ctx", name="ct%d" % r)
             ctx_banks[r] = ct
             keys = row_terms[r]
-            count = len(keys) + (1 if in_band(r) else 0)
-            done = 0
-            if in_band(r):
-                ri = r - BAND_LO
-                for j in range(4):
+            ri = r - BAND_LO
+            places = [(j * len(keys)) // 4 for j in range(4)]
+            for k, key in enumerate(keys):
+                if in_band(r) and k in places:
+                    j = places.index(k)
                     nc.tensor.matmul(
                         out=ct[:, j, :],
                         lhsT=v_sb[r][:, j * P : (j + 1) * P],
                         rhs=a_band[ri // BAND_GROUP][:, ri % BAND_GROUP, 8 : 8 + P],
-                        start=(j == 0),
+                        start=(k == 0),
                         stop=False,
                     )
-                done = 1
-            for key in keys:
-                done += 1
                 for j in range(4):
                     nc.tensor.matmul(
                         out=ct[:, j, :],
                         lhsT=sums[key][:, j * P : (j + 1) * P],
                         rhs=rot[key[1]][:],
                         is_transpose=True,
-                        start=(done == 1 and j == 0),
-                        stop=(done == count and j == 3),
+                        start=(k == 0 and j == 0 and not in_band(r)),
+                        stop=(k == len(keys) - 1 and j == 3),
                     )
 
         def round_context(r):

@@ -440,7 +440,7 @@ def tile_selfattentionmodulev2_pb_kernel(tc, x, attn, v_w, v_b, w_w, w_b, out):
                 if max(FIRST_STEP, r - 5) == t:
                     start_row(r)
             for k, (r, dj, di, joined) in enumerate(prod_plan.get(t, [])):
-                product(r, dj, di, joined, k % 2 == 0)
+                product(r, dj, di, joined, k % 3 == 0)
             chunk, phase = (t + 7) // 4, (t + 7) % 4
             if 1 <= chunk < H // CHUNK_ROWS:
                 if phase < 2:

@@ -7,6 +7,7 @@ FP8X4 = mybir.dt.float8_e4m3fn_x4
 F32 = mybir.dt.float32
 BF16 = mybir.dt.bfloat16
 U32 = mybir.dt.uint32
+I32 = mybir.dt.int32
 U8 = mybir.dt.uint8
 ALU = mybir.AluOpType
 ACT = mybir.ActivationFunctionType
@@ -14,81 +15,108 @@ AX = mybir.AxisListType
 
 P = 128
 B, C, H, W = 2, 512, 32, 64
-ROW = B * W
-NPIX = H * ROW
-CHUNK_ROWS = 4
-CHUNK = CHUNK_ROWS * ROW
-BAND_LO, BAND_HI = 3, 28
-BAND_GROUP = 5
-APAD = 16
-BAND_W = 144
+NT = 32
+NPIX = NT * P
+HALF = NPIX // B
+APAD = 80
+BAND_W = 272
 BAND_PITCH = P * (BAND_W + 1)
+BAND_PAD = 72
+BAND_GROUP = 5
 SHIFTS = (-4, -2, -1, 1, 2, 4)
+TURNS = (63, 64, 65)
 LEVEL = {1: 0, 2: 1, 4: 2}
 FIRST_STEP = -3
+OUTER = 1
+OUTER_ON_VECTOR = False
+BAND_RANGES = ((2, 0, 12), (18, 12, 13))
 
 FLOPS = 2 * 2 * C * C * B * H * W + 2 * 27 * C * B * H * W
 
 
-def in_band(r):
-    return BAND_LO <= r < BAND_HI
+def in_band(s):
+    return 4 <= s <= 27 or s == 29
 
 
-def group_taps(r, dj):
-    if dj == 0:
-        cand = (-4, -2, -1, 0, 1, 2, 4)
+def band_index(s):
+    return s // 2 - 2 + (12 if s % 2 == 1 else 0)
+
+
+def group_taps(s, turn):
+    own = [] if in_band(s) else [0]
+    if turn == 0:
+        cand = [-4, -2] + own + [OUTER, 2, 4]
+    elif abs(turn) == 1:
+        cand = own + [OUTER]
+    elif turn in TURNS:
+        cand = own
     else:
-        cand = (-abs(dj), 0, abs(dj))
-    return [di for di in cand if 0 <= r + di < H and not (di == 0 and in_band(r))]
+        cand = [-abs(turn)] + own + [abs(turn)]
+    return [o for o in cand if 0 <= s + o < NT or o == OUTER]
 
 
-def merged_groups(r):
-    if r < BAND_LO:
-        return ()
-    if r >= BAND_HI:
+def merged_groups(s):
+    if s >= 26:
+        return (-4, 4, -2, 2)
+    if not in_band(s):
         return (-4, 4)
-    if r % 2 == 1:
-        return (-4, 4, 2)
-    return (-4, 4)
+    return (-4, 4, -2, 2)
+
+
+def main_columns(s):
+    m, b = s // 2, s % 2
+    return b * HALF + (m % 2) * (HALF // 2) + (m // 2) * P
+
+
+def outer_columns(s):
+    m, b = s // 2, s % 2
+    return b * HALF + (m if m % 2 == 1 else 15 + m) * W
 
 
 def tile_selfattentionmodulev2_pb_kernel(tc, x, attn, v_w, v_b, w_w, w_b, out):
     nc = tc.nc
 
     vec_plan, prod_plan, row_terms = {}, {}, {}
-    for r in range(H):
+    for s in range(NT):
         plain, joined = [], []
-        for dj in SHIFTS:
-            taps = group_taps(r, dj)
-            if dj in merged_groups(r) and len(taps) > 1:
-                step = max(FIRST_STEP, r + taps[1] - 1)
-                prod_plan.setdefault(step, []).append((r, dj, taps[0], True))
-                for di in taps[1:]:
-                    vec_plan.setdefault(r + di, []).append((r, dj, di))
-                joined.append((taps[-1], dj))
+        for turn in SHIFTS + TURNS:
+            taps = group_taps(s, turn)
+            if turn in merged_groups(s) and len(taps) > 1:
+                step = max(FIRST_STEP, s + taps[1] - 1)
+                prod_plan.setdefault(step, []).append((s, turn, taps[0], True))
+                for o in taps[1:]:
+                    vec_plan.setdefault(s + o, []).append((s, turn, o))
+                joined.append((taps[-1], turn))
             else:
-                for di in taps:
-                    prod_plan.setdefault(r + 3, []).append((r, dj, di, False))
-                    plain.append((r, dj, di))
-        for di in group_taps(r, 0):
-            vec_plan.setdefault(r + di, []).append((r, 0, di))
-        row_terms[r] = plain + [(r, dj, None) for (last, dj) in sorted(joined)] + [(r, 0, None)]
+                for o in taps:
+                    prod_plan.setdefault(s + 3, []).append((s, turn, o, False))
+                    plain.append((s, turn, o))
+        for o in group_taps(s, 0):
+            if o == OUTER and OUTER_ON_VECTOR:
+                vec_plan.setdefault(s + 3, []).append((s, 0, o))
+            elif o == OUTER:
+                prod_plan.setdefault(s + 3, []).append((s, 0, o, False))
+                plain.append((s, 0, o))
+            else:
+                vec_plan.setdefault(s + o, []).append((s, 0, o))
+        row_terms[s] = plain + [(s, turn, None) for (last, turn) in sorted(joined)] + [(s, 0, None)]
     for step in vec_plan:
-        vec_plan[step] = sorted(vec_plan[step], key=lambda tap: (-tap[2], tap[1] == 0))
+        vec_plan[step] = sorted(vec_plan[step], key=lambda tap: (tap[2] != OUTER, -tap[2], tap[1] == 0))
     for step in prod_plan:
-        prod_plan[step] = sorted(prod_plan[step], key=lambda tap: not tap[3])
+        prod_plan[step] = sorted(prod_plan[step], key=lambda tap: (tap[2] != OUTER, not tap[3]))
 
     with ExitStack() as ctx:
         const = ctx.enter_context(tc.tile_pool(name="const", bufs=1))
         wpool = ctx.enter_context(tc.tile_pool(name="wpool", bufs=1))
         xpool = ctx.enter_context(tc.tile_pool(name="xpool", bufs=2))
-        vpool = ctx.enter_context(tc.tile_pool(name="vpool", bufs=12))
-        upool = ctx.enter_context(tc.tile_pool(name="upool", bufs=11))
-        mpool = ctx.enter_context(tc.tile_pool(name="mpool", bufs=14))
-        ppool = ctx.enter_context(tc.tile_pool(name="ppool", bufs=20))
-        gpool = ctx.enter_context(tc.tile_pool(name="gpool", bufs=3))
+        vpool = ctx.enter_context(tc.tile_pool(name="vpool", bufs=10))
+        upool = ctx.enter_context(tc.tile_pool(name="upool", bufs=10))
+        mpool = ctx.enter_context(tc.tile_pool(name="mpool", bufs=19))
+        ppool = ctx.enter_context(tc.tile_pool(name="ppool", bufs=18))
+        gpool = ctx.enter_context(tc.tile_pool(name="gpool", bufs=2))
         opool = ctx.enter_context(tc.tile_pool(name="opool", bufs=2))
-        ps_v = ctx.enter_context(tc.psum_pool(name="ps_v", bufs=4))
+        ps_v = ctx.enter_context(tc.psum_pool(name="ps_v", bufs=3))
+        ps_w = ctx.enter_context(tc.psum_pool(name="ps_w", bufs=1))
         ps_c = ctx.enter_context(tc.psum_pool(name="ps_c", bufs=2))
         ps_o = ctx.enter_context(tc.psum_pool(name="ps_o", bufs=2))
         ctx.enter_context(tc.manual_schedule())
@@ -118,86 +146,105 @@ def tile_selfattentionmodulev2_pb_kernel(tc, x, attn, v_w, v_b, w_w, w_b, out):
 
         raw_tiles, gx_tiles = {}, {}
 
-        def load_x(s):
-            raw_tiles[s] = xpool.tile([P, B, 4, CHUNK_ROWS * W], BF16, tag="raw", name="raw%d" % s, bufs=3)
-            for b in range(B):
-                nc.sync.dma_start(
-                    out=raw_tiles[s][:, b],
-                    in_=x[b].rearrange("(q j) r c -> q j (r c)", j=4)[
-                        :, :, s * CHUNK_ROWS * W : (s + 1) * CHUNK_ROWS * W
-                    ],
-                )
+        def load_x(ch):
+            raw_tiles[ch] = xpool.tile([P, 4, 8 * W], BF16, tag="raw", name="raw%d" % ch, bufs=4)
+            nc.sync.dma_start(
+                out=raw_tiles[ch][:],
+                in_=x[ch % 2].rearrange("(q j) r c -> q j (r c)", j=4)[:, :, (ch // 2) * 8 * W : (ch // 2 + 1) * 8 * W],
+            )
 
-        def regroup_x(s, b, copy):
-            if s not in gx_tiles:
-                gx_tiles[s] = xpool.tile([P, CHUNK_ROWS, B, W, 4], BF16, tag="gx", name="gx%d" % s, align_bytes=64)
-            copy(out=gx_tiles[s][:, :, b], in_=raw_tiles[s][:, b].rearrange("q j (r c) -> q r c j", r=CHUNK_ROWS))
+        def regroup_x(ch, h, copy):
+            if ch not in gx_tiles:
+                gx_tiles[ch] = xpool.tile([P, 2, 2 * P, 4], BF16, tag="gx", name="gx%d" % ch, align_bytes=64)
+            copy(
+                out=gx_tiles[ch][:, h].rearrange("q (k n) j -> q k n j", k=2),
+                in_=raw_tiles[ch][:].rearrange("q j (k h n) -> q h k n j", k=2, h=2)[:, h],
+            )
 
-        def quantise_x(s):
-            cols = slice(s * CHUNK, (s + 1) * CHUNK)
+        def quantise_x(ch, h):
+            first = (ch % 2) * HALF + h * (HALF // 2) + (ch // 2) * 2 * P
             nc.vector.quantize_mx(
-                out=x_codes[:, cols].bitcast(FP8X4),
-                scales=x_plane[:, cols],
-                in_=gx_tiles[s][:].rearrange("q r b c j -> q (r b c j)"),
+                out=x_codes[:, first : first + 2 * P].bitcast(FP8X4),
+                scales=x_plane[:, first : first + 2 * P],
+                in_=gx_tiles[ch][:, h].rearrange("q n j -> q (n j)"),
             )
 
         ident_f = const.tile([P, P], F32)
         make_identity(nc, ident_f[:])
         ident_b = const.tile([P, P], BF16)
         make_identity(nc, ident_b[:])
-        at3 = const.tile([P, 8 * ROW + 2 * APAD], BF16)
+        at3 = const.tile([P, 8 * P + 2 * APAD], BF16)
         nc.vector.memset(at3[:], 0.0)
-        bt = const.tile([P, H, 16], F32)
+        bt = const.tile([P, NT, 3, 16], F32)
         nc.gpsimd.memset(bt[:], 0.0)
         zeros = const.tile([P, BAND_W + 1], F32)
         nc.gpsimd.memset(zeros[:], 0.0)
         scratch = out.rearrange("b o r c -> (b o r c)")
         x_codes = const.tile([P, NPIX], U32, align_bytes=64)
         x_plane = const.tile([P, NPIX], U8, align_bytes=64)
-
-        def load_attn(queue, g, b):
-            queue.dma_start(
-                out=at3[32 * g : 32 * g + 27, APAD : APAD + 8 * ROW].rearrange("n (i b c) -> n i b c", i=8, b=B)[
-                    :, :, b, :
-                ],
-                in_=attn[b, :, 8 * g : 8 * g + 8, :],
-            )
+        for b in range(B):
+            hole = slice(b * HALF + 15 * W, b * HALF + 16 * W)
+            nc.vector.memset(x_codes[:, hole].bitcast(I32), 0)
+            nc.vector.memset(x_plane[:, hole].bitcast(I32), 0)
 
         wb_bf = const.tile([P, 4], BF16)
         vb_raw = const.tile([P, C], BF16)
         nc.scalar.dma_start(out=wb_bf[:], in_=w_b.rearrange("(q j) -> q j", j=4))
         vw_sb = load_weight(v_w, "vw")
         load_x(0)
-        for g in range(4):
-            load_attn(nc.scalar, g, 0)
-            load_attn(nc.sync, g, 1)
-        nc.scalar.dma_start(out=vb_raw[:], in_=v_b.partition_broadcast(P))
         load_x(1)
-        ww_sb = load_weight(w_w, "ww")
+        for g in range(4):
+            queue = nc.scalar if g % 2 == 0 else nc.sync
+            queue.dma_start(
+                out=at3[32 * g : 32 * g + 27, APAD : APAD + 8 * P],
+                in_=attn[g // 2, :, 16 * (g % 2) : 16 * (g % 2) + 16, :].rearrange("n r c -> n (r c)"),
+            )
+        nc.scalar.dma_start(out=vb_raw[:], in_=v_b.partition_broadcast(P))
         load_x(2)
-        for ri in range(BAND_HI - BAND_LO):
+        load_x(3)
+        ww_sb = load_weight(w_w, "ww")
+        for ri in range(25):
             nc.sync.dma_start(
                 out=scratch[ri * BAND_PITCH : (ri + 1) * BAND_PITCH].rearrange("(p f) -> p f", p=P), in_=zeros[:]
             )
 
         vw_grouped = transpose_weight(vw_sb, (nc.vector.tensor_copy, nc.scalar.copy))
         regroup_x(0, 0, nc.vector.tensor_copy)
-        regroup_x(0, 1, nc.scalar.copy)
+        regroup_x(1, 0, nc.scalar.copy)
         vw_codes, vw_plane = quantise_weight(vw_grouped, "vw")
-        quantise_x(0)
+        regroup_x(0, 1, nc.vector.tensor_copy)
+        quantise_x(0, 0)
+        regroup_x(1, 1, nc.scalar.copy)
+        quantise_x(1, 0)
+        quantise_x(0, 1)
+        quantise_x(1, 1)
+        load_x(4)
+        load_x(5)
 
         rot = {0: ident_f}
-        for dj in SHIFTS:
-            rot[dj] = const.tile([P, P], F32, name="rot%d" % (dj + 4))
-            cut = dj % P
-            nc.gpsimd.tensor_copy(out=rot[dj][:, 0 : P - cut], in_=ident_f[:, cut:P])
-            nc.gpsimd.tensor_copy(out=rot[dj][:, P - cut : P], in_=ident_f[:, 0:cut])
+        for turn in SHIFTS + TURNS:
+            rot[turn] = const.tile([P, P], F32, name="rot%d" % (turn + 4))
+            cut = turn % P
+            nc.gpsimd.tensor_copy(out=rot[turn][:, 0 : P - cut], in_=ident_f[:, cut:P])
+            nc.gpsimd.tensor_copy(out=rot[turn][:, P - cut : P], in_=ident_f[:, 0:cut])
         vb_all = const.tile([P, 4, P], F32)
         nc.gpsimd.tensor_copy(out=vb_all[:], in_=vb_raw[:].rearrange("p (q j) -> p j q", j=4))
 
-        pa = ps_c.tile([P, 8, P], BF16, tag="ctx")
-        for i in range(8):
-            nc.tensor.transpose(pa[:, i, :], at3[:, APAD + i * ROW : APAD + (i + 1) * ROW], ident_b[:])
+        spare = {"n": 0}
+
+        def windows(shift):
+            spare["n"] += 1
+            if spare["n"] % 2 == 0:
+                pt = ps_o.tile([P, 8, P], BF16, tag="o")
+            else:
+                pt = ps_c.tile([P, 8, P], BF16, tag="ctx")
+            for i in range(8):
+                nc.tensor.transpose(
+                    pt[:, i, :], at3[:, APAD + i * P + shift : APAD + (i + 1) * P + shift], ident_b[:]
+                )
+            return pt
+
+        pa = windows(0)
         a_t = const.tile([P, 8, 4, 32], F32)
         nc.vector.tensor_copy(out=a_t[:].rearrange("p i g n -> p i (g n)"), in_=pa[:])
         mk = const.tile([P, 8], F32)
@@ -221,9 +268,12 @@ def tile_selfattentionmodulev2_pb_kernel(tc, x, attn, v_w, v_b, w_w, w_b, out):
                     scalar2=None,
                     op0=ALU.mult,
                 )
-        for lvl, d in enumerate((1, 2, 4)):
-            nc.vector.memset(a_t[:, 0:d, 0, 9 * lvl : 9 * lvl + 3], 0.0)
-            nc.vector.memset(a_t[:, 8 - d : 8, 3, 9 * lvl + 6 : 9 * lvl + 9], 0.0)
+        nc.vector.memset(a_t[0:64, 0, 0:3:2, 0:3], 0.0)
+        nc.vector.memset(a_t[64:128, 7, 1:4:2, 6:9], 0.0)
+        nc.vector.memset(a_t[:, 0, 0:3:2, 9:12], 0.0)
+        nc.vector.memset(a_t[:, 7, 1:4:2, 15:18], 0.0)
+        nc.vector.memset(a_t[:, 0:2, 0:3:2, 18:21], 0.0)
+        nc.vector.memset(a_t[:, 6:8, 1:4:2, 24:27], 0.0)
         a_sum = const.tile([P, 8, 4], F32)
         nc.vector.tensor_reduce(out=a_sum[:], in_=a_t[:, :, :, 0:27], axis=AX.X, op=ALU.add)
         for n in (13, 22):
@@ -231,19 +281,13 @@ def tile_selfattentionmodulev2_pb_kernel(tc, x, attn, v_w, v_b, w_w, w_b, out):
         wb = const.tile([P, 4], F32)
         nc.vector.tensor_copy(out=wb[:], in_=wb_bf[:])
 
-        btv = bt[:].rearrange("p (g i) j -> p i g j", g=4)
-        as_w = {}
-        nc.gpsimd.tensor_copy(out=btv[:, :, :, 8], in_=a_t[:, :, :, 4])
-        for idx, dj in enumerate(SHIFTS):
+        btv = bt[:].rearrange("p (g i) u t -> p i g u t", g=4)
+        as_w, w_out, x_in, a_band = {}, {}, {}, []
+        nc.gpsimd.tensor_copy(out=btv[:, :, :, 1, 8], in_=a_t[:, :, :, 4])
+
+        def shifted_weights(dj):
             lvl, side = LEVEL[abs(dj)], (1 if dj > 0 else 0)
-            if idx % 2 == 0:
-                pa_s = ps_o.tile([P, 8, P], BF16, tag="o")
-            else:
-                pa_s = ps_c.tile([P, 8, P], BF16, tag="ctx")
-            for i in range(8):
-                nc.tensor.transpose(
-                    pa_s[:, i, :], at3[:, APAD + i * ROW - dj : APAD + (i + 1) * ROW - dj], ident_b[:]
-                )
+            pa_s = windows(-dj)
             as_w[dj] = const.tile([P, 8, 4, 4], F32, name="as_w%d" % (dj + 4))
             first = 9 * lvl + 2 * side
             nc.vector.tensor_scalar(
@@ -253,129 +297,181 @@ def tile_selfattentionmodulev2_pb_kernel(tc, x, attn, v_w, v_b, w_w, w_b, out):
                 scalar2=None,
                 op0=ALU.mult,
             )
-            nc.gpsimd.tensor_copy(out=btv[:, :, :, 8 - dj], in_=as_w[dj][:, :, :, 1])
+            nc.gpsimd.tensor_copy(out=btv[:, :, :, 1, 8 - dj], in_=as_w[dj][:, :, :, 1])
 
-        a_band = []
-        n_band = BAND_HI - BAND_LO
-        nc.sync.dma_start(
-            out=scratch[0 : n_band * BAND_PITCH].rearrange("(r p t) -> p r t", p=P, t=BAND_W + 1)[:, :, 0:16],
-            in_=bt[:, BAND_LO:BAND_HI, :],
-        )
-        for q in range(n_band // BAND_GROUP):
-            a_q = const.tile([P, BAND_GROUP, BAND_W], F32, name="a_band%d" % q)
-            nc.sync.dma_start(
-                out=a_q[:],
-                in_=scratch[q * BAND_GROUP * BAND_PITCH : (q + 1) * BAND_GROUP * BAND_PITCH]
-                .rearrange("(r m) -> r m", m=BAND_PITCH)[:, 0 : P * BAND_W]
-                .rearrange("r (p c) -> p r c", c=BAND_W),
-            )
-            a_band.append(a_q)
-
-        def weight(r, di, dj):
+        def outer_weights(dj):
+            w_out[dj] = const.tile([P, 8, 4], F32, name="w_out%d" % (dj + 1))
             if dj == 0:
-                n = 4 if di == 0 else 9 * LEVEL[abs(di)] + (0 if di < 0 else 6) + 1
-                return a_t[:, r % 8, r // 8, n : n + 1]
-            pos = 1 + di // abs(dj)
-            return as_w[dj][:, r % 8, r // 8, pos : pos + 1]
+                nc.gpsimd.tensor_copy(out=w_out[dj][0:64], in_=a_t[0:64, :, :, 1])
+                nc.gpsimd.tensor_copy(out=w_out[dj][64:128], in_=a_t[64:128, :, :, 7])
+            else:
+                nc.gpsimd.tensor_copy(out=w_out[dj][0:64], in_=as_w[dj][0:64, :, :, 0])
+                nc.gpsimd.tensor_copy(out=w_out[dj][64:128], in_=as_w[dj][64:128, :, :, 2])
+                nc.gpsimd.memset(w_out[dj][0:64, 0, 0:3:2], 0.0)
+                nc.gpsimd.memset(w_out[dj][64:128, 7, 1:4:2], 0.0)
 
-        v_ps, v_sb, sums = {}, {}, {}
+        def inner_weights(dj):
+            x_in[dj] = const.tile([P, 8, 4], F32, name="x_in%d" % (dj + 1))
+            for lo, hi, shift, n in ((64, 128, -(64 + dj), 7 + dj), (0, 64, 64 - dj, 1 + dj)):
+                pa_x = windows(shift)
+                nc.vector.tensor_scalar(
+                    out=x_in[dj][lo:hi],
+                    in0=pa_x[lo:hi].rearrange("p i (g n) -> p i g n", g=4)[:, :, :, n],
+                    scalar1=(1.0 if dj == 0 else mk[lo:hi, (1 - dj) // 2 : (1 - dj) // 2 + 1]),
+                    scalar2=None,
+                    op0=ALU.mult,
+                )
+                nc.gpsimd.tensor_copy(out=btv[lo:hi, :, :, (0 if lo == 64 else 2), 8 - dj], in_=x_in[dj][lo:hi])
+
+        def band_matrices():
+            for first_t, first_r, count in BAND_RANGES:
+                for u in range(3):
+                    nc.sync.dma_start(
+                        out=scratch[first_r * BAND_PITCH : (first_r + count) * BAND_PITCH].rearrange(
+                            "(r p t) -> p r t", p=P, t=BAND_W + 1
+                        )[:, :, 64 * u : 64 * u + 16],
+                        in_=bt[:, first_t : first_t + count, u, :],
+                    )
+            for q in range(25 // BAND_GROUP):
+                a_q = const.tile([P, BAND_GROUP, P], F32, name="a_band%d" % q)
+                nc.sync.dma_start(
+                    out=a_q[:],
+                    in_=scratch[q * BAND_GROUP * BAND_PITCH : (q + 1) * BAND_GROUP * BAND_PITCH]
+                    .rearrange("(r m) -> r m", m=BAND_PITCH)[:, 0 : P * BAND_W]
+                    .rearrange("r (p c) -> p r c", c=BAND_W)[:, :, BAND_PAD : BAND_PAD + P],
+                )
+                a_band.append(a_q)
+
+        background = {
+            -3: [lambda: shifted_weights(-1), lambda: shifted_weights(1)],
+            -2: [lambda: shifted_weights(-2), lambda: shifted_weights(2)],
+            -1: [lambda: shifted_weights(-4), lambda: shifted_weights(4)],
+            0: [lambda: outer_weights(-1), lambda: outer_weights(0), lambda: outer_weights(1), lambda: inner_weights(-1)],
+            1: [lambda: inner_weights(0), lambda: inner_weights(1)],
+            2: [band_matrices],
+        }
+
+        def weight(s, turn, o):
+            i, g = (s // 2) % 8, 2 * (s % 2) + (s // 2) // 8
+            if o == OUTER:
+                return w_out[turn][:, i, g : g + 1]
+            if turn in TURNS:
+                return x_in[turn - 64][:, i, g : g + 1]
+            if turn == 0:
+                n = 4 if o == 0 else 9 * LEVEL[abs(o)] + (0 if o < 0 else 6) + 1
+                return a_t[:, i, g, n : n + 1]
+            pos = 1 + o // abs(turn)
+            return as_w[turn][:, i, g, pos : pos + 1]
+
+        v_ps, v_sb, w_ps, sums = {}, {}, {}, {}
         pair_tiles, pair_codes, pair_banks = {}, {}, {}
         ww_grouped, ww_q = [], []
 
-        def first_conv(s):
-            pix = slice(s * ROW, (s + 1) * ROW)
-            v_ps[s] = ps_v.tile([P, C], F32, tag="v0", name="v_ps%d" % s)
+        def first_conv(dst, first):
             nc.tensor.matmul_mx(
-                out=v_ps[s][:],
-                lhsT=x_codes[:, pix].bitcast(FP8X4),
-                lhsT_scale=x_plane[:, pix],
+                out=dst[:],
+                lhsT=x_codes[:, first : first + P].bitcast(FP8X4),
+                lhsT_scale=x_plane[:, first : first + P],
                 rhs=vw_codes[:].bitcast(FP8X4),
                 rhs_scale=vw_plane[:],
                 start=True,
                 stop=True,
             )
 
+        def main_value(s):
+            v_ps[s] = ps_v.tile([P, C], F32, tag="v0", name="v_ps%d" % s)
+            first_conv(v_ps[s], main_columns(s))
+
+        def outer_value(s):
+            w_ps[s] = ps_w.tile([P, C], F32, tag="w", name="w_ps%d" % s)
+            first_conv(w_ps[s], outer_columns(s))
+
         def copy_value(s):
             v_sb[s] = vpool.tile([P, C], F32, tag="v_sb", name="v_sb%d" % s)
             nc.scalar.copy(out=v_sb[s][:], in_=v_ps[s][:])
 
-        def start_row(r):
-            sums[(r, 0, None)] = upool.tile([P, C], F32, tag="u0", name="u0_%d" % r)
+        def start_row(s):
+            i, g = (s // 2) % 8, 2 * (s % 2) + (s // 2) // 8
+            sums[(s, 0, None)] = upool.tile([P, C], F32, tag="u0", name="u0_%d" % s)
             nc.gpsimd.tensor_scalar(
-                out=sums[(r, 0, None)][:],
+                out=sums[(s, 0, None)][:],
                 in0=vb_all[:].rearrange("p j q -> p (j q)"),
-                scalar1=a_sum[:, r % 8, r // 8 : r // 8 + 1],
+                scalar1=a_sum[:, i, g : g + 1],
                 scalar2=0.0,
                 op0=ALU.mult,
                 op1=ALU.add,
             )
 
-        def product(r, dj, di, joined, on_gpsimd):
+        def product(s, turn, o, joined, on_gpsimd):
             if joined:
-                key = (r, dj, None)
-                sums[key] = mpool.tile([P, C], F32, tag="um", name="um_%d_%d" % (r, dj + 4))
+                key = (s, turn, None)
+                sums[key] = mpool.tile([P, C], F32, tag="um", name="um_%d_%d" % (s, turn + 4))
             else:
-                key = (r, dj, di)
-                sums[key] = ppool.tile([P, C], F32, tag="pr", name="pr_%d_%d_%d" % (r, dj + 4, di + 4))
+                key = (s, turn, o)
+                sums[key] = ppool.tile([P, C], F32, tag="pr", name="pr_%d_%d_%d" % (s, turn + 4, o + 4))
+            source = w_ps[s] if o == OUTER else v_sb[s + o]
             if on_gpsimd:
                 nc.gpsimd.tensor_scalar(
                     out=sums[key][:],
-                    in0=v_sb[r + di][:],
-                    scalar1=weight(r, di, dj),
+                    in0=source[:],
+                    scalar1=weight(s, turn, o),
                     scalar2=0.0,
                     op0=ALU.mult,
                     op1=ALU.add,
                 )
             else:
-                nc.scalar.activation(out=sums[key][:], in_=v_sb[r + di][:], func=ACT.Copy, scale=weight(r, di, dj))
+                nc.scalar.activation(out=sums[key][:], in_=source[:], func=ACT.Copy, scale=weight(s, turn, o))
 
-        def vector_tap(r, dj, di):
-            acc = sums[(r, dj, None)]
+        def vector_tap(s, turn, o):
+            acc = sums[(s, turn, None)]
+            source = w_ps[s] if o == OUTER else v_ps[s + o]
             nc.vector.scalar_tensor_tensor(
-                out=acc[:], in0=v_ps[r + di][:], scalar=weight(r, di, dj), in1=acc[:], op0=ALU.mult, op1=ALU.add
+                out=acc[:], in0=source[:], scalar=weight(s, turn, o), in1=acc[:], op0=ALU.mult, op1=ALU.add
             )
 
         ctx_banks = {}
 
-        def add_up(r):
-            ct = ps_c.tile([P, 4, P], F32, tag="ctx", name="ct%d" % r)
-            ctx_banks[r] = ct
-            keys = row_terms[r]
-            ri = r - BAND_LO
+        def add_up(s, mx_work):
+            ct = ps_c.tile([P, 4, P], F32, tag="ctx", name="ct%d" % s)
+            ctx_banks[s] = ct
+            keys = row_terms[s]
+            ri = band_index(s)
             places = [(j * len(keys)) // 4 for j in range(4)]
             for k, key in enumerate(keys):
-                if in_band(r) and k in places:
+                if in_band(s) and k in places:
                     j = places.index(k)
                     nc.tensor.matmul(
                         out=ct[:, j, :],
-                        lhsT=v_sb[r][:, j * P : (j + 1) * P],
-                        rhs=a_band[ri // BAND_GROUP][:, ri % BAND_GROUP, 8 : 8 + P],
+                        lhsT=v_sb[s][:, j * P : (j + 1) * P],
+                        rhs=a_band[ri // BAND_GROUP][:, ri % BAND_GROUP, :],
                         start=(k == 0),
                         stop=False,
                     )
+                if k == places[2]:
+                    mx_work()
                 for j in range(4):
                     nc.tensor.matmul(
                         out=ct[:, j, :],
                         lhsT=sums[key][:, j * P : (j + 1) * P],
                         rhs=rot[key[1]][:],
                         is_transpose=True,
-                        start=(k == 0 and j == 0 and not in_band(r)),
+                        start=(k == 0 and j == 0 and not in_band(s)),
                         stop=(k == len(keys) - 1 and j == 3),
                     )
 
-        def round_context(r):
-            pair = r // 2
+        def round_context(s):
+            pair = s // 2
             if pair not in pair_tiles:
-                pair_tiles[pair] = gpool.tile([P, 2, ROW, 4], BF16, tag="g2", name="g2_%d" % pair, align_bytes=64)
-            nc.scalar.copy(out=pair_tiles[pair][:, r % 2], in_=ctx_banks[r][:].rearrange("q j x -> q x j"))
+                pair_tiles[pair] = gpool.tile([P, 2, P, 4], BF16, tag="g2", name="g2_%d" % pair, align_bytes=64)
+            nc.scalar.copy(out=pair_tiles[pair][:, s % 2], in_=ctx_banks[s][:].rearrange("q j n -> q n j"))
 
         def quantise_pair(pair):
-            c_codes = gpool.tile([P, 2 * ROW], U32, tag="c_codes", name="c_codes%d" % pair, align_bytes=64)
-            c_plane = gpool.tile([P, 2 * ROW], U8, tag="c_plane", name="c_plane%d" % pair, align_bytes=64)
+            c_codes = gpool.tile([P, 2 * P], U32, tag="c_codes", name="c_codes%d" % pair, align_bytes=64)
+            c_plane = gpool.tile([P, 2 * P], U8, tag="c_plane", name="c_plane%d" % pair, align_bytes=64)
             nc.vector.quantize_mx(
                 out=c_codes[:].bitcast(FP8X4),
                 scales=c_plane[:],
-                in_=pair_tiles[pair][:].rearrange("q r x j -> q (r x j)"),
+                in_=pair_tiles[pair][:].rearrange("q b n j -> q (b n j)"),
             )
             pair_codes[pair] = (c_codes, c_plane)
 
@@ -384,7 +480,7 @@ def tile_selfattentionmodulev2_pb_kernel(tc, x, attn, v_w, v_b, w_w, w_b, out):
             ww_codes, ww_plane = ww_q[0]
             banks = []
             for half in range(2):
-                po = ps_o.tile([P, 2, 2 * ROW], F32, tag="o")
+                po = ps_o.tile([P, 2, 2 * P], F32, tag="o")
                 banks.append(po)
                 for a in range(2):
                     j = 2 * half + a
@@ -401,51 +497,62 @@ def tile_selfattentionmodulev2_pb_kernel(tc, x, attn, v_w, v_b, w_w, w_b, out):
 
         def store_pair(pair):
             banks = pair_banks[pair]
-            ot = opool.tile([P, 4, B, 2, W], F32, tag="ot")
+            ot = opool.tile([P, 4, 2 * P], F32, tag="ot")
             for j in range(4):
-                dst = ot[:, j].rearrange("q b r c -> q r b c")
-                res = banks[j // 2][:, j % 2, :].rearrange("q (r b c) -> q r b c", r=2, b=B)
-                nc.scalar.activation(out=dst, in_=res, func=ACT.Identity, bias=wb[:, j : j + 1], scale=1.0)
+                nc.scalar.activation(
+                    out=ot[:, j, :], in_=banks[j // 2][:, j % 2, :], func=ACT.Identity, bias=wb[:, j : j + 1], scale=1.0
+                )
             for b in range(B):
                 nc.sync.dma_start(
-                    out=out[b].rearrange("(q j) r c -> q j (r c)", j=4)[:, :, pair * 2 * W : (pair + 1) * 2 * W],
-                    in_=ot[:, :, b].rearrange("q j r c -> q j (r c)"),
+                    out=out[b].rearrange("(q j) r c -> q j (r c)", j=4)[:, :, pair * P : (pair + 1) * P],
+                    in_=ot[:, :, b * P : (b + 1) * P],
                 )
 
-        for t in range(FIRST_STEP, H + 6):
-            pair = (t - 7) // 2
-            if t % 2 == 1:
-                for s in (t + 2, t + 3):
-                    if 0 <= s < H:
-                        first_conv(s)
-                if 0 <= pair < H // 2:
-                    second_conv(pair)
+        def mx_run(t):
+            if 0 <= t + 2 < NT:
+                main_value(t + 2)
+            if 0 <= t - 2 < NT:
+                outer_value(t - 2)
+            if t % 2 == 1 and 0 <= (t - 7) // 2 < NT // 2:
+                second_conv((t - 7) // 2)
+
+        for t in range(FIRST_STEP, NT + 7):
             if t == 0:
                 ww_grouped.append(transpose_weight(ww_sb, (nc.scalar.copy, nc.scalar.copy)))
-            if 0 <= t - 5 < H:
+            for s, turn, o, joined in prod_plan.get(t, []):
+                if o == OUTER:
+                    product(s, turn, o, joined, False)
+            if 0 <= t - 5 < NT:
                 round_context(t - 5)
-            if 0 <= t + 2 < H:
-                copy_value(t + 2)
-            if t % 2 == 1 and 0 <= pair < H // 2:
-                store_pair(pair)
-            for r, dj, di in vec_plan.get(t, []):
-                vector_tap(r, dj, di)
-            if t % 2 == 0 and 0 <= (t - 6) // 2 < H // 2:
+            if 0 <= t + 1 < NT:
+                copy_value(t + 1)
+            if t % 2 == 0 and 0 <= (t - 8) // 2 < NT // 2:
+                store_pair((t - 8) // 2)
+            for s, turn, o in vec_plan.get(t, []):
+                vector_tap(s, turn, o)
+            if t % 2 == 0 and 0 <= (t - 6) // 2 < NT // 2:
                 quantise_pair((t - 6) // 2)
             if t == 1:
                 ww_q.append(quantise_weight(ww_grouped[0], "ww"))
-            if 0 <= t - 4 < H:
-                add_up(t - 4)
-            for r in range(H):
-                if max(FIRST_STEP, r - 5) == t:
-                    start_row(r)
-            for k, (r, dj, di, joined) in enumerate(prod_plan.get(t, [])):
-                product(r, dj, di, joined, k % 3 == 0)
-            chunk, phase = (t + 7) // 4, (t + 7) % 4
-            if 1 <= chunk < H // CHUNK_ROWS:
-                if phase < 2:
-                    regroup_x(chunk, phase, nc.vector.tensor_copy if chunk == 1 else nc.scalar.copy)
-                    if phase == 1 and chunk + 2 < H // CHUNK_ROWS:
-                        load_x(chunk + 2)
-                if phase == 2:
-                    quantise_x(chunk)
+            if 0 <= t - 4 < NT:
+                add_up(t - 4, lambda step=t: mx_run(step))
+            else:
+                mx_run(t)
+            for s in range(NT):
+                if max(FIRST_STEP, s - 5) == t:
+                    start_row(s)
+            turn_of_gpsimd = 0
+            for s, turn, o, joined in prod_plan.get(t, []):
+                if o != OUTER:
+                    product(s, turn, o, joined, turn_of_gpsimd % 2 == 0)
+                    turn_of_gpsimd += 1
+            for job in background.get(t, []):
+                job()
+            for kk in range(1, 4):
+                u = t - (8 * kk - 11)
+                if 0 <= u < 4:
+                    regroup_x(2 * kk + u // 2, u % 2, nc.scalar.copy)
+                    if u % 2 == 1 and kk == 1:
+                        load_x(2 * kk + u // 2 + 4)
+                if 0 <= u - 2 < 4:
+                    quantise_x(2 * kk + (u - 2) // 2, (u - 2) % 2)

@@ -16,6 +16,7 @@ AX = mybir.AxisListType
 P = 128
 B, C, H, W = 2, 512, 32, 64
 NT = 32
+TB = NT // B
 NPIX = NT * P
 HALF = NPIX // B
 APAD = 80
@@ -27,56 +28,52 @@ SHIFTS = (-4, -2, -1, 1, 2, 4)
 TURNS = (63, 64, 65)
 LEVEL = {1: 0, 2: 1, 4: 2}
 FIRST_STEP = -3
-OUTER = 1
-OUTER_ON_VECTOR = False
-BAND_RANGES = ((2, 0, 12), (18, 12, 13))
+OUTER = 7
+LAG = 2
+BAND_RANGES = ((7, 0, 25),)
 
 FLOPS = 2 * 2 * C * C * B * H * W + 2 * 27 * C * B * H * W
 
 
 def in_band(s):
-    return 4 <= s <= 27 or s == 29
+    return s >= 7
 
 
 def band_index(s):
-    return s // 2 - 2 + (12 if s % 2 == 1 else 0)
+    return s - 7
 
 
 def group_taps(s, turn):
     own = [] if in_band(s) else [0]
     if turn == 0:
-        cand = [-4, -2] + own + [OUTER, 2, 4]
+        cand = [-2, -1] + own + [OUTER, 1, 2]
     elif abs(turn) == 1:
         cand = own + [OUTER]
     elif turn in TURNS:
         cand = own
     else:
-        cand = [-abs(turn)] + own + [abs(turn)]
-    return [o for o in cand if 0 <= s + o < NT or o == OUTER]
+        cand = [-abs(turn) // 2] + own + [abs(turn) // 2]
+    return [o for o in cand if o == OUTER or 0 <= s % TB + o < TB]
 
 
 def merged_groups(s):
-    if s >= 26:
-        return (-4, 4, -2, 2)
-    if not in_band(s):
-        return (-4, 4)
     return (-4, 4, -2, 2)
 
 
 def main_columns(s):
-    m, b = s // 2, s % 2
+    m, b = s % TB, s // TB
     return b * HALF + (m % 2) * (HALF // 2) + (m // 2) * P
 
 
 def outer_columns(s):
-    m, b = s // 2, s % 2
+    m, b = s % TB, s // TB
     return b * HALF + (m if m % 2 == 1 else 15 + m) * W
 
 
 def tile_selfattentionmodulev2_pb_kernel(tc, x, attn, v_w, v_b, w_w, w_b, out):
     nc = tc.nc
 
-    vec_plan, prod_plan, row_terms = {}, {}, {}
+    vec_plan, prod_plan, row_terms, join_plan = {}, {}, {}, {}
     for s in range(NT):
         plain, joined = [], []
         for turn in SHIFTS + TURNS:
@@ -89,19 +86,20 @@ def tile_selfattentionmodulev2_pb_kernel(tc, x, attn, v_w, v_b, w_w, w_b, out):
                 joined.append((taps[-1], turn))
             else:
                 for o in taps:
-                    prod_plan.setdefault(s + 3, []).append((s, turn, o, False))
+                    prod_plan.setdefault(s if o == OUTER else s + LAG - 1, []).append((s, turn, o, False))
                     plain.append((s, turn, o))
         for o in group_taps(s, 0):
-            if o == OUTER and OUTER_ON_VECTOR:
-                vec_plan.setdefault(s + 3, []).append((s, 0, o))
-            elif o == OUTER:
-                prod_plan.setdefault(s + 3, []).append((s, 0, o, False))
-                plain.append((s, 0, o))
+            if o == OUTER:
+                prod_plan.setdefault(s, []).append((s, 0, o, False))
+                if in_band(s):
+                    join_plan.setdefault(s, []).append((s, 0, o))
+                else:
+                    plain.append((s, 0, o))
             else:
                 vec_plan.setdefault(s + o, []).append((s, 0, o))
         row_terms[s] = plain + [(s, turn, None) for (last, turn) in sorted(joined)] + [(s, 0, None)]
     for step in vec_plan:
-        vec_plan[step] = sorted(vec_plan[step], key=lambda tap: (tap[2] != OUTER, -tap[2], tap[1] == 0))
+        vec_plan[step] = sorted(vec_plan[step], key=lambda tap: (-tap[2], tap[1] == 0))
     for step in prod_plan:
         prod_plan[step] = sorted(prod_plan[step], key=lambda tap: (tap[2] != OUTER, not tap[3]))
 
@@ -150,7 +148,7 @@ def tile_selfattentionmodulev2_pb_kernel(tc, x, attn, v_w, v_b, w_w, w_b, out):
             raw_tiles[ch] = xpool.tile([P, 4, 8 * W], BF16, tag="raw", name="raw%d" % ch, bufs=4)
             nc.sync.dma_start(
                 out=raw_tiles[ch][:],
-                in_=x[ch % 2].rearrange("(q j) r c -> q j (r c)", j=4)[:, :, (ch // 2) * 8 * W : (ch // 2 + 1) * 8 * W],
+                in_=x[ch // 4].rearrange("(q j) r c -> q j (r c)", j=4)[:, :, (ch % 4) * 8 * W : (ch % 4 + 1) * 8 * W],
             )
 
         def regroup_x(ch, h, copy):
@@ -162,7 +160,7 @@ def tile_selfattentionmodulev2_pb_kernel(tc, x, attn, v_w, v_b, w_w, w_b, out):
             )
 
         def quantise_x(ch, h):
-            first = (ch % 2) * HALF + h * (HALF // 2) + (ch // 2) * 2 * P
+            first = (ch // 4) * HALF + h * (HALF // 2) + (ch % 4) * 2 * P
             nc.vector.quantize_mx(
                 out=x_codes[:, first : first + 2 * P].bitcast(FP8X4),
                 scales=x_plane[:, first : first + 2 * P],
@@ -343,24 +341,28 @@ def tile_selfattentionmodulev2_pb_kernel(tc, x, attn, v_w, v_b, w_w, w_b, out):
                 a_band.append(a_q)
 
         background = {
-            -3: [lambda: shifted_weights(-1), lambda: shifted_weights(1)],
-            -2: [lambda: shifted_weights(-2), lambda: shifted_weights(2)],
-            -1: [lambda: shifted_weights(-4), lambda: shifted_weights(4)],
-            0: [lambda: outer_weights(-1), lambda: outer_weights(0), lambda: outer_weights(1), lambda: inner_weights(-1)],
-            1: [lambda: inner_weights(0), lambda: inner_weights(1)],
-            2: [band_matrices],
+            -3: [lambda: shifted_weights(-1), lambda: shifted_weights(1), lambda: outer_weights(0)],
+            -2: [
+                lambda: outer_weights(-1),
+                lambda: outer_weights(1),
+                lambda: shifted_weights(-2),
+                lambda: shifted_weights(2),
+            ],
+            -1: [lambda: shifted_weights(-4), lambda: shifted_weights(4), lambda: inner_weights(-1)],
+            0: [lambda: inner_weights(0), lambda: inner_weights(1)],
+            1: [band_matrices],
         }
 
         def weight(s, turn, o):
-            i, g = (s // 2) % 8, 2 * (s % 2) + (s // 2) // 8
+            i, g = s % 8, s // 8
             if o == OUTER:
                 return w_out[turn][:, i, g : g + 1]
             if turn in TURNS:
                 return x_in[turn - 64][:, i, g : g + 1]
             if turn == 0:
-                n = 4 if o == 0 else 9 * LEVEL[abs(o)] + (0 if o < 0 else 6) + 1
+                n = 4 if o == 0 else 9 * LEVEL[2 * abs(o)] + (0 if o < 0 else 6) + 1
                 return a_t[:, i, g, n : n + 1]
-            pos = 1 + o // abs(turn)
+            pos = 1 + (1 if o > 0 else 0) - (1 if o < 0 else 0)
             return as_w[turn][:, i, g, pos : pos + 1]
 
         v_ps, v_sb, w_ps, sums = {}, {}, {}, {}
@@ -391,7 +393,7 @@ def tile_selfattentionmodulev2_pb_kernel(tc, x, attn, v_w, v_b, w_w, w_b, out):
             nc.scalar.copy(out=v_sb[s][:], in_=v_ps[s][:])
 
         def start_row(s):
-            i, g = (s // 2) % 8, 2 * (s % 2) + (s // 2) // 8
+            i, g = s % 8, s // 8
             sums[(s, 0, None)] = upool.tile([P, C], F32, tag="u0", name="u0_%d" % s)
             nc.gpsimd.tensor_scalar(
                 out=sums[(s, 0, None)][:],
@@ -422,11 +424,14 @@ def tile_selfattentionmodulev2_pb_kernel(tc, x, attn, v_w, v_b, w_w, w_b, out):
             else:
                 nc.scalar.activation(out=sums[key][:], in_=source[:], func=ACT.Copy, scale=weight(s, turn, o))
 
+        def gpsimd_join(s, turn, o):
+            acc = sums[(s, turn, None)]
+            nc.gpsimd.tensor_tensor(out=acc[:], in0=acc[:], in1=sums[(s, turn, o)][:], op=ALU.add)
+
         def vector_tap(s, turn, o):
             acc = sums[(s, turn, None)]
-            source = w_ps[s] if o == OUTER else v_ps[s + o]
             nc.vector.scalar_tensor_tensor(
-                out=acc[:], in0=source[:], scalar=weight(s, turn, o), in1=acc[:], op0=ALU.mult, op1=ALU.add
+                out=acc[:], in0=v_ps[s + o][:], scalar=weight(s, turn, o), in1=acc[:], op0=ALU.mult, op1=ALU.add
             )
 
         ctx_banks = {}
@@ -502,57 +507,59 @@ def tile_selfattentionmodulev2_pb_kernel(tc, x, attn, v_w, v_b, w_w, w_b, out):
                 nc.scalar.activation(
                     out=ot[:, j, :], in_=banks[j // 2][:, j % 2, :], func=ACT.Identity, bias=wb[:, j : j + 1], scale=1.0
                 )
-            for b in range(B):
-                nc.sync.dma_start(
-                    out=out[b].rearrange("(q j) r c -> q j (r c)", j=4)[:, :, pair * P : (pair + 1) * P],
-                    in_=ot[:, :, b * P : (b + 1) * P],
-                )
+            first = (2 * pair % TB) * P
+            nc.sync.dma_start(
+                out=out[2 * pair // TB].rearrange("(q j) r c -> q j (r c)", j=4)[:, :, first : first + 2 * P],
+                in_=ot[:],
+            )
 
         def mx_run(t):
             if 0 <= t + 2 < NT:
                 main_value(t + 2)
-            if 0 <= t - 2 < NT:
-                outer_value(t - 2)
-            if t % 2 == 1 and 0 <= (t - 7) // 2 < NT // 2:
-                second_conv((t - 7) // 2)
+            if 0 <= t + 1 < NT:
+                outer_value(t + 1)
+            if t % 2 == 1 and 0 <= (t - 5) // 2 < NT // 2:
+                second_conv((t - 5) // 2)
 
-        for t in range(FIRST_STEP, NT + 7):
+        for t in range(FIRST_STEP, NT + 5):
             if t == 0:
                 ww_grouped.append(transpose_weight(ww_sb, (nc.scalar.copy, nc.scalar.copy)))
             for s, turn, o, joined in prod_plan.get(t, []):
                 if o == OUTER:
                     product(s, turn, o, joined, False)
-            if 0 <= t - 5 < NT:
-                round_context(t - 5)
+            if 0 <= t - LAG - 1 < NT:
+                round_context(t - LAG - 1)
             if 0 <= t + 1 < NT:
                 copy_value(t + 1)
-            if t % 2 == 0 and 0 <= (t - 8) // 2 < NT // 2:
-                store_pair((t - 8) // 2)
+            if t % 2 == 0 and 0 <= (t - 6) // 2 < NT // 2:
+                store_pair((t - 6) // 2)
             for s, turn, o in vec_plan.get(t, []):
                 vector_tap(s, turn, o)
-            if t % 2 == 0 and 0 <= (t - 6) // 2 < NT // 2:
-                quantise_pair((t - 6) // 2)
+            if t % 2 == 0 and 0 <= (t - 4) // 2 < NT // 2:
+                quantise_pair((t - 4) // 2)
             if t == 1:
                 ww_q.append(quantise_weight(ww_grouped[0], "ww"))
-            if 0 <= t - 4 < NT:
-                add_up(t - 4, lambda step=t: mx_run(step))
+            if 0 <= t - LAG < NT:
+                add_up(t - LAG, lambda step=t: mx_run(step))
             else:
                 mx_run(t)
             for s in range(NT):
-                if max(FIRST_STEP, s - 5) == t:
+                if max(FIRST_STEP, s - LAG - 1) == t:
                     start_row(s)
             turn_of_gpsimd = 0
             for s, turn, o, joined in prod_plan.get(t, []):
                 if o != OUTER:
-                    product(s, turn, o, joined, turn_of_gpsimd % 2 == 0)
+                    product(s, turn, o, joined, turn_of_gpsimd % 3 != 2)
                     turn_of_gpsimd += 1
+            for s, turn, o in join_plan.get(t, []):
+                gpsimd_join(s, turn, o)
             for job in background.get(t, []):
                 job()
-            for kk in range(1, 4):
-                u = t - (8 * kk - 11)
-                if 0 <= u < 4:
-                    regroup_x(2 * kk + u // 2, u % 2, nc.scalar.copy)
-                    if u % 2 == 1 and kk == 1:
-                        load_x(2 * kk + u // 2 + 4)
-                if 0 <= u - 2 < 4:
-                    quantise_x(2 * kk + (u - 2) // 2, (u - 2) % 2)
+            for ch in range(2, 8):
+                u = t - (4 * ch - 8)
+                if 0 <= u < 2:
+                    regroup_x(ch, u, nc.scalar.copy)
+                    if u == 1 and ch + 4 < 8:
+                        load_x(ch + 4)
+                if 0 <= u - 2 < 2:
+                    quantise_x(ch, u - 2)

@@ -549,7 +549,7 @@ def tile_selfattentionmodulev2_pb_kernel(tc, x, attn, v_w, v_b, w_w, w_b, out):
             turn_of_gpsimd = 0
             for s, turn, o, joined in prod_plan.get(t, []):
                 if o != OUTER:
-                    product(s, turn, o, joined, turn_of_gpsimd % 3 != 2)
+                    product(s, turn, o, joined, turn_of_gpsimd % 2 == 0)
                     turn_of_gpsimd += 1
             for s, turn, o in join_plan.get(t, []):
                 gpsimd_join(s, turn, o)

@@ -30,17 +30,17 @@ LEVEL = {1: 0, 2: 1, 4: 2}
 FIRST_STEP = -3
 OUTER = 7
 LAG = 2
-BAND_RANGES = ((7, 0, 25),)
+BAND_RANGES = ((3, 0, 11), (18, 11, 14))
 
 FLOPS = 2 * 2 * C * C * B * H * W + 2 * 27 * C * B * H * W
 
 
 def in_band(s):
-    return s >= 7
+    return s not in (0, 1, 2, 14, 15, 16, 17)
 
 
 def band_index(s):
-    return s - 7
+    return s - 3 if s < 14 else s - 7
 
 
 def group_taps(s, turn):
@@ -171,6 +171,16 @@ def tile_selfattentionmodulev2_pb_kernel(tc, x, attn, v_w, v_b, w_w, w_b, out):
         make_identity(nc, ident_f[:])
         ident_b = const.tile([P, P], BF16)
         make_identity(nc, ident_b[:])
+        mk = const.tile([P, 8], F32)
+        idv = ident_f[:].rearrange("p (h c) -> p h c", h=2)
+        for lvl, d in enumerate((1, 2, 4)):
+            nc.vector.tensor_reduce(out=mk[:, 2 * lvl : 2 * lvl + 1], in_=idv[:, :, 0:d], axis=AX.XY, op=ALU.add)
+            nc.vector.tensor_reduce(
+                out=mk[:, 2 * lvl + 1 : 2 * lvl + 2], in_=idv[:, :, W - d : W], axis=AX.XY, op=ALU.add
+            )
+        nc.vector.tensor_scalar(
+            out=mk[:, 0:6], in0=mk[:, 0:6], scalar1=-1.0, scalar2=1.0, op0=ALU.mult, op1=ALU.add
+        )
         at3 = const.tile([P, 8 * P + 2 * APAD], BF16)
         nc.vector.memset(at3[:], 0.0)
         bt = const.tile([P, NT, 3, 16], F32)
@@ -213,9 +223,7 @@ def tile_selfattentionmodulev2_pb_kernel(tc, x, attn, v_w, v_b, w_w, w_b, out):
         regroup_x(0, 1, nc.vector.tensor_copy)
         quantise_x(0, 0)
         regroup_x(1, 1, nc.scalar.copy)
-        quantise_x(1, 0)
         quantise_x(0, 1)
-        quantise_x(1, 1)
         load_x(4)
         load_x(5)
 
@@ -245,16 +253,6 @@ def tile_selfattentionmodulev2_pb_kernel(tc, x, attn, v_w, v_b, w_w, w_b, out):
         pa = windows(0)
         a_t = const.tile([P, 8, 4, 32], F32)
         nc.vector.tensor_copy(out=a_t[:].rearrange("p i g n -> p i (g n)"), in_=pa[:])
-        mk = const.tile([P, 8], F32)
-        idv = ident_f[:].rearrange("p (h c) -> p h c", h=2)
-        for lvl, d in enumerate((1, 2, 4)):
-            nc.vector.tensor_reduce(out=mk[:, 2 * lvl : 2 * lvl + 1], in_=idv[:, :, 0:d], axis=AX.XY, op=ALU.add)
-            nc.vector.tensor_reduce(
-                out=mk[:, 2 * lvl + 1 : 2 * lvl + 2], in_=idv[:, :, W - d : W], axis=AX.XY, op=ALU.add
-            )
-        nc.vector.tensor_scalar(
-            out=mk[:, 0:6], in0=mk[:, 0:6], scalar1=-1.0, scalar2=1.0, op0=ALU.mult, op1=ALU.add
-        )
         a_taps = a_t[:, :, :, 0:27].rearrange("p i g (l a j) -> p i g l a j", l=3, a=3)
         for lvl in range(3):
             for side in range(2):
@@ -288,12 +286,11 @@ def tile_selfattentionmodulev2_pb_kernel(tc, x, attn, v_w, v_b, w_w, w_b, out):
             pa_s = windows(-dj)
             as_w[dj] = const.tile([P, 8, 4, 4], F32, name="as_w%d" % (dj + 4))
             first = 9 * lvl + 2 * side
-            nc.vector.tensor_scalar(
+            nc.scalar.activation(
                 out=as_w[dj][:, :, :, 0:3],
-                in0=pa_s[:].rearrange("p i (g n) -> p i g n", g=4)[:, :, :, first : first + 7 : 3],
-                scalar1=mk[:, 2 * lvl + 1 - side : 2 * lvl + 2 - side],
-                scalar2=None,
-                op0=ALU.mult,
+                in_=pa_s[:].rearrange("p i (g n) -> p i g n", g=4)[:, :, :, first : first + 7 : 3],
+                func=ACT.Copy,
+                scale=mk[:, 2 * lvl + 1 - side : 2 * lvl + 2 - side],
             )
             nc.gpsimd.tensor_copy(out=btv[:, :, :, 1, 8 - dj], in_=as_w[dj][:, :, :, 1])
 
@@ -312,12 +309,11 @@ def tile_selfattentionmodulev2_pb_kernel(tc, x, attn, v_w, v_b, w_w, w_b, out):
             x_in[dj] = const.tile([P, 8, 4], F32, name="x_in%d" % (dj + 1))
             for lo, hi, shift, n in ((64, 128, -(64 + dj), 7 + dj), (0, 64, 64 - dj, 1 + dj)):
                 pa_x = windows(shift)
-                nc.vector.tensor_scalar(
+                nc.scalar.activation(
                     out=x_in[dj][lo:hi],
-                    in0=pa_x[lo:hi].rearrange("p i (g n) -> p i g n", g=4)[:, :, :, n],
-                    scalar1=(1.0 if dj == 0 else mk[lo:hi, (1 - dj) // 2 : (1 - dj) // 2 + 1]),
-                    scalar2=None,
-                    op0=ALU.mult,
+                    in_=pa_x[lo:hi].rearrange("p i (g n) -> p i g n", g=4)[:, :, :, n],
+                    func=ACT.Copy,
+                    scale=(1.0 if dj == 0 else mk[lo:hi, (1 - dj) // 2 : (1 - dj) // 2 + 1]),
                 )
                 nc.gpsimd.tensor_copy(out=btv[lo:hi, :, :, (0 if lo == 64 else 2), 8 - dj], in_=x_in[dj][lo:hi])
 
@@ -347,9 +343,16 @@ def tile_selfattentionmodulev2_pb_kernel(tc, x, attn, v_w, v_b, w_w, w_b, out):
                 lambda: outer_weights(1),
                 lambda: shifted_weights(-2),
                 lambda: shifted_weights(2),
+                lambda: shifted_weights(-4),
+                lambda: shifted_weights(4),
             ],
-            -1: [lambda: shifted_weights(-4), lambda: shifted_weights(4), lambda: inner_weights(-1)],
-            0: [lambda: inner_weights(0), lambda: inner_weights(1)],
+            -1: [
+                lambda: inner_weights(-1),
+                lambda: inner_weights(0),
+                lambda: inner_weights(1),
+                lambda: quantise_x(1, 0),
+                lambda: quantise_x(1, 1),
+            ],
             1: [band_matrices],
         }
 
@@ -504,6 +507,11 @@ def tile_selfattentionmodulev2_pb_kernel(tc, x, attn, v_w, v_b, w_w, w_b, out):
             banks = pair_banks[pair]
             ot = opool.tile([P, 4, 2 * P], F32, tag="ot")
             for j in range(4):
+                if pair >= NT // 2 - 2 and j >= 2:
+                    nc.vector.tensor_scalar(
+                        out=ot[:, j, :], in0=banks[1][:, j % 2, :], scalar1=wb[:, j : j + 1], scalar2=None, op0=ALU.add
+                    )
+                    continue
                 nc.scalar.activation(
                     out=ot[:, j, :], in_=banks[j // 2][:, j % 2, :], func=ACT.Identity, bias=wb[:, j : j + 1], scale=1.0
                 )

@@ -444,18 +444,18 @@ def tile_selfattentionmodulev2_pb_kernel(tc, x, attn, v_w, v_b, w_w, w_b, out):
             ctx_banks[s] = ct
             keys = row_terms[s]
             ri = band_index(s)
-            places = [(j * len(keys)) // 4 for j in range(4)]
+            middle = len(keys) // 2
             for k, key in enumerate(keys):
-                if in_band(s) and k in places:
-                    j = places.index(k)
-                    nc.tensor.matmul(
-                        out=ct[:, j, :],
-                        lhsT=v_sb[s][:, j * P : (j + 1) * P],
-                        rhs=a_band[ri // BAND_GROUP][:, ri % BAND_GROUP, :],
-                        start=(k == 0),
-                        stop=False,
-                    )
-                if k == places[2]:
+                if k == middle:
+                    if in_band(s):
+                        for j in range(4):
+                            nc.tensor.matmul(
+                                out=ct[:, j, :],
+                                lhsT=v_sb[s][:, j * P : (j + 1) * P],
+                                rhs=a_band[ri // BAND_GROUP][:, ri % BAND_GROUP, :],
+                                start=False,
+                                stop=False,
+                            )
                     mx_work()
                 for j in range(4):
                     nc.tensor.matmul(
@@ -463,7 +463,7 @@ def tile_selfattentionmodulev2_pb_kernel(tc, x, attn, v_w, v_b, w_w, w_b, out):
                         lhsT=sums[key][:, j * P : (j + 1) * P],
                         rhs=rot[key[1]][:],
                         is_transpose=True,
-                        start=(k == 0 and j == 0 and not in_band(s)),
+                        start=(k == 0 and j == 0),
                         stop=(k == len(keys) - 1 and j == 3),
                     )
 

@@ -167,47 +167,27 @@ def tile_selfattentionmodulev2_pb_kernel(tc, x, attn, v_w, v_b, w_w, w_b, out):
                 in_=gx_tiles[ch][:, h].rearrange("q n j -> q (n j)"),
             )
 
-        ident_f = const.tile([P, P], F32)
-        make_identity(nc, ident_f[:])
-        ident_b = const.tile([P, P], BF16)
-        make_identity(nc, ident_b[:])
-        mk = const.tile([P, 8], F32)
-        idv = ident_f[:].rearrange("p (h c) -> p h c", h=2)
-        for lvl, d in enumerate((1, 2, 4)):
-            nc.vector.tensor_reduce(out=mk[:, 2 * lvl : 2 * lvl + 1], in_=idv[:, :, 0:d], axis=AX.XY, op=ALU.add)
-            nc.vector.tensor_reduce(
-                out=mk[:, 2 * lvl + 1 : 2 * lvl + 2], in_=idv[:, :, W - d : W], axis=AX.XY, op=ALU.add
-            )
-        nc.vector.tensor_scalar(
-            out=mk[:, 0:6], in0=mk[:, 0:6], scalar1=-1.0, scalar2=1.0, op0=ALU.mult, op1=ALU.add
-        )
         at3 = const.tile([P, 8 * P + 2 * APAD], BF16)
         nc.vector.memset(at3[:], 0.0)
-        bt = const.tile([P, NT, 3, 16], F32)
-        nc.gpsimd.memset(bt[:], 0.0)
+        ident_f = const.tile([P, P], F32)
+        make_identity(nc, ident_f[:])
         zeros = const.tile([P, BAND_W + 1], F32)
         nc.gpsimd.memset(zeros[:], 0.0)
         scratch = out.rearrange("b o r c -> (b o r c)")
-        x_codes = const.tile([P, NPIX], U32, align_bytes=64)
-        x_plane = const.tile([P, NPIX], U8, align_bytes=64)
-        for b in range(B):
-            hole = slice(b * HALF + 15 * W, b * HALF + 16 * W)
-            nc.vector.memset(x_codes[:, hole].bitcast(I32), 0)
-            nc.vector.memset(x_plane[:, hole].bitcast(I32), 0)
 
         wb_bf = const.tile([P, 4], BF16)
-        vb_raw = const.tile([P, C], BF16)
-        nc.scalar.dma_start(out=wb_bf[:], in_=w_b.rearrange("(q j) -> q j", j=4))
+        vb_bf = const.tile([P, 4], BF16)
         vw_sb = load_weight(v_w, "vw")
         load_x(0)
-        load_x(1)
         for g in range(4):
             queue = nc.scalar if g % 2 == 0 else nc.sync
             queue.dma_start(
                 out=at3[32 * g : 32 * g + 27, APAD : APAD + 8 * P],
                 in_=attn[g // 2, :, 16 * (g % 2) : 16 * (g % 2) + 16, :].rearrange("n r c -> n (r c)"),
             )
-        nc.scalar.dma_start(out=vb_raw[:], in_=v_b.partition_broadcast(P))
+        nc.scalar.dma_start(out=vb_bf[:], in_=v_b.rearrange("(q j) -> q j", j=4))
+        nc.scalar.dma_start(out=wb_bf[:], in_=w_b.rearrange("(q j) -> q j", j=4))
+        load_x(1)
         load_x(2)
         load_x(3)
         ww_sb = load_weight(w_w, "ww")
@@ -216,25 +196,49 @@ def tile_selfattentionmodulev2_pb_kernel(tc, x, attn, v_w, v_b, w_w, w_b, out):
                 out=scratch[ri * BAND_PITCH : (ri + 1) * BAND_PITCH].rearrange("(p f) -> p f", p=P), in_=zeros[:]
             )
 
-        vw_grouped = transpose_weight(vw_sb, (nc.vector.tensor_copy, nc.scalar.copy))
-        regroup_x(0, 0, nc.vector.tensor_copy)
-        regroup_x(1, 0, nc.scalar.copy)
-        vw_codes, vw_plane = quantise_weight(vw_grouped, "vw")
-        regroup_x(0, 1, nc.vector.tensor_copy)
-        quantise_x(0, 0)
-        regroup_x(1, 1, nc.scalar.copy)
-        quantise_x(0, 1)
-        load_x(4)
-        load_x(5)
-
-        rot = {0: ident_f}
-        for turn in SHIFTS + TURNS:
-            rot[turn] = const.tile([P, P], F32, name="rot%d" % (turn + 4))
-            cut = turn % P
-            nc.gpsimd.tensor_copy(out=rot[turn][:, 0 : P - cut], in_=ident_f[:, cut:P])
-            nc.gpsimd.tensor_copy(out=rot[turn][:, P - cut : P], in_=ident_f[:, 0:cut])
-        vb_all = const.tile([P, 4, P], F32)
-        nc.gpsimd.tensor_copy(out=vb_all[:], in_=vb_raw[:].rearrange("p (q j) -> p j q", j=4))
+        valid = const.tile([P, 8, 4, 32], F32)
+        nc.vector.memset(valid[:], 1.0)
+        bt = const.tile([P, NT, 3, 16], F32)
+        nc.vector.memset(bt[:], 0.0)
+        mk = const.tile([P, 8], F32)
+        idv = ident_f[:].rearrange("p (h c) -> p h c", h=2)
+        for lvl, d in enumerate((1, 2, 4)):
+            nc.vector.tensor_reduce(out=mk[:, 2 * lvl : 2 * lvl + 1], in_=idv[:, :, 0:d], axis=AX.XY, op=ALU.add)
+            nc.vector.tensor_reduce(
+                out=mk[:, 2 * lvl + 1 : 2 * lvl + 2], in_=idv[:, :, W - d : W], axis=AX.XY, op=ALU.add
+            )
+        ident_b = const.tile([P, 2 * P], BF16)
+        ident2 = const.tile([P, 2 * P], F32)
+        for half in range(2):
+            nc.vector.tensor_copy(out=ident_b[:, half * P : (half + 1) * P], in_=ident_f[:])
+        nc.vector.tensor_scalar(
+            out=mk[:, 0:6], in0=mk[:, 0:6], scalar1=-1.0, scalar2=1.0, op0=ALU.mult, op1=ALU.add
+        )
+        for half in range(2):
+            nc.vector.tensor_copy(out=ident2[:, half * P : (half + 1) * P], in_=ident_f[:])
+        valid_taps = valid[:, :, :, 0:27].rearrange("p i g (l a j) -> p i g l a j", l=3, a=3)
+        for lvl in range(3):
+            for side in range(2):
+                view = valid_taps[:, :, :, lvl, :, 2 * side]
+                nc.vector.tensor_scalar(
+                    out=view,
+                    in0=view,
+                    scalar1=mk[:, 2 * lvl + side : 2 * lvl + side + 1],
+                    scalar2=None,
+                    op0=ALU.mult,
+                )
+        nc.vector.memset(valid[0:64, 0, 0:3:2, 0:3], 0.0)
+        nc.vector.memset(valid[64:128, 7, 1:4:2, 6:9], 0.0)
+        nc.vector.memset(valid[:, 0, 0:3:2, 9:12], 0.0)
+        nc.vector.memset(valid[:, 7, 1:4:2, 15:18], 0.0)
+        nc.vector.memset(valid[:, 0:2, 0:3:2, 18:21], 0.0)
+        nc.vector.memset(valid[:, 6:8, 1:4:2, 24:27], 0.0)
+        x_codes = const.tile([P, NPIX], U32, align_bytes=64)
+        x_plane = const.tile([P, NPIX], U8, align_bytes=64)
+        for b in range(B):
+            hole = slice(b * HALF + 15 * W, b * HALF + 16 * W)
+            nc.vector.memset(x_codes[:, hole].bitcast(I32), 0)
+            nc.vector.memset(x_plane[:, hole].bitcast(I32), 0)
 
         spare = {"n": 0}
 
@@ -246,76 +250,92 @@ def tile_selfattentionmodulev2_pb_kernel(tc, x, attn, v_w, v_b, w_w, w_b, out):
                 pt = ps_c.tile([P, 8, P], BF16, tag="ctx")
             for i in range(8):
                 nc.tensor.transpose(
-                    pt[:, i, :], at3[:, APAD + i * P + shift : APAD + (i + 1) * P + shift], ident_b[:]
+                    pt[:, i, :], at3[:, APAD + i * P + shift : APAD + (i + 1) * P + shift], ident_b[:, 0:P]
                 )
             return pt
 
+        vw_grouped = transpose_weight(vw_sb, (nc.vector.tensor_copy, nc.scalar.copy))
+        vb_ps = ps_c.tile([P, 4, P], BF16, tag="ctx")
+        for j in range(4):
+            nc.tensor.transpose(vb_ps[:, j, :], vb_bf[:, j : j + 1].to_broadcast([P, P]), ident_b[:, 0:P])
+        vb_all = const.tile([P, 4, P], F32)
         pa = windows(0)
+        regroup_x(0, 0, nc.vector.tensor_copy)
+        regroup_x(0, 1, nc.scalar.copy)
+        vw_codes, vw_plane = quantise_weight(vw_grouped, "vw")
+        nc.scalar.copy(out=vb_all[:], in_=vb_ps[:])
         a_t = const.tile([P, 8, 4, 32], F32)
-        nc.vector.tensor_copy(out=a_t[:].rearrange("p i g n -> p i (g n)"), in_=pa[:])
-        a_taps = a_t[:, :, :, 0:27].rearrange("p i g (l a j) -> p i g l a j", l=3, a=3)
-        for lvl in range(3):
-            for side in range(2):
-                view = a_taps[:, :, :, lvl, :, 2 * side]
-                nc.vector.tensor_scalar(
-                    out=view,
-                    in0=view,
-                    scalar1=mk[:, 2 * lvl + side : 2 * lvl + side + 1],
-                    scalar2=None,
-                    op0=ALU.mult,
-                )
-        nc.vector.memset(a_t[0:64, 0, 0:3:2, 0:3], 0.0)
-        nc.vector.memset(a_t[64:128, 7, 1:4:2, 6:9], 0.0)
-        nc.vector.memset(a_t[:, 0, 0:3:2, 9:12], 0.0)
-        nc.vector.memset(a_t[:, 7, 1:4:2, 15:18], 0.0)
-        nc.vector.memset(a_t[:, 0:2, 0:3:2, 18:21], 0.0)
-        nc.vector.memset(a_t[:, 6:8, 1:4:2, 24:27], 0.0)
+        nc.vector.tensor_tensor(
+            out=a_t[:].rearrange("p i g n -> p i (g n)"),
+            in0=pa[:],
+            in1=valid[:].rearrange("p i g n -> p i (g n)"),
+            op=ALU.mult,
+        )
+        near_w = const.tile([P, 3, 8, 4, 3], F32)
+        nc.vector.tensor_reduce(out=near_w[:, 1, :, :, 1], in_=a_t[:, :, :, 4:23:9], axis=AX.X, op=ALU.add)
+        quantise_x(0, 0)
         a_sum = const.tile([P, 8, 4], F32)
         nc.vector.tensor_reduce(out=a_sum[:], in_=a_t[:, :, :, 0:27], axis=AX.X, op=ALU.add)
-        for n in (13, 22):
-            nc.vector.tensor_tensor(out=a_t[:, :, :, 4], in0=a_t[:, :, :, 4], in1=a_t[:, :, :, n], op=ALU.add)
+        quantise_x(0, 1)
+        load_x(4)
+        for h in range(2):
+            regroup_x(2, h, nc.vector.tensor_copy)
+        load_x(6)
         wb = const.tile([P, 4], F32)
         nc.vector.tensor_copy(out=wb[:], in_=wb_bf[:])
 
+        rot = {turn: ident2[:, turn % P : turn % P + P] for turn in (0,) + SHIFTS + TURNS}
+
         btv = bt[:].rearrange("p (g i) u t -> p i g u t", g=4)
-        as_w, w_out, x_in, a_band = {}, {}, {}, []
-        nc.gpsimd.tensor_copy(out=btv[:, :, :, 1, 8], in_=a_t[:, :, :, 4])
+        w_out = const.tile([P, 3, 8, 4], F32)
+        x_in = const.tile([P, 3, 8, 4], F32)
+        far_w, a_band = {}, []
 
         def shifted_weights(dj):
             lvl, side = LEVEL[abs(dj)], (1 if dj > 0 else 0)
             pa_s = windows(-dj)
-            as_w[dj] = const.tile([P, 8, 4, 4], F32, name="as_w%d" % (dj + 4))
+            if lvl == 0:
+                dst = near_w[:, 1 - dj]
+            else:
+                far_w[dj] = const.tile([P, 8, 4, 3], F32, name="far_w%d" % (dj + 4))
+                dst = far_w[dj][:]
             first = 9 * lvl + 2 * side
             nc.scalar.activation(
-                out=as_w[dj][:, :, :, 0:3],
+                out=dst,
                 in_=pa_s[:].rearrange("p i (g n) -> p i g n", g=4)[:, :, :, first : first + 7 : 3],
                 func=ACT.Copy,
                 scale=mk[:, 2 * lvl + 1 - side : 2 * lvl + 2 - side],
             )
-            nc.gpsimd.tensor_copy(out=btv[:, :, :, 1, 8 - dj], in_=as_w[dj][:, :, :, 1])
 
-        def outer_weights(dj):
-            w_out[dj] = const.tile([P, 8, 4], F32, name="w_out%d" % (dj + 1))
-            if dj == 0:
-                nc.gpsimd.tensor_copy(out=w_out[dj][0:64], in_=a_t[0:64, :, :, 1])
-                nc.gpsimd.tensor_copy(out=w_out[dj][64:128], in_=a_t[64:128, :, :, 7])
-            else:
-                nc.gpsimd.tensor_copy(out=w_out[dj][0:64], in_=as_w[dj][0:64, :, :, 0])
-                nc.gpsimd.tensor_copy(out=w_out[dj][64:128], in_=as_w[dj][64:128, :, :, 2])
-                nc.gpsimd.memset(w_out[dj][0:64, 0, 0:3:2], 0.0)
-                nc.gpsimd.memset(w_out[dj][64:128, 7, 1:4:2], 0.0)
+        def near_weights():
+            nc.scalar.copy(out=near_w[:, 1, :, :, 0:3:2], in_=a_t[:, :, :, 1:8:6])
+            nc.scalar.copy(out=w_out[0:64], in_=near_w[0:64, :, :, :, 0])
+            nc.scalar.copy(out=w_out[64:128], in_=near_w[64:128, :, :, :, 2])
+            nc.gpsimd.memset(w_out[0:64, :, 0, 0:3:2], 0.0)
+            nc.gpsimd.memset(w_out[64:128, :, 7, 1:4:2], 0.0)
 
-        def inner_weights(dj):
-            x_in[dj] = const.tile([P, 8, 4], F32, name="x_in%d" % (dj + 1))
-            for lo, hi, shift, n in ((64, 128, -(64 + dj), 7 + dj), (0, 64, 64 - dj, 1 + dj)):
-                pa_x = windows(shift)
-                nc.scalar.activation(
-                    out=x_in[dj][lo:hi],
-                    in_=pa_x[lo:hi].rearrange("p i (g n) -> p i g n", g=4)[:, :, :, n],
-                    func=ACT.Copy,
-                    scale=(1.0 if dj == 0 else mk[lo:hi, (1 - dj) // 2 : (1 - dj) // 2 + 1]),
-                )
-                nc.gpsimd.tensor_copy(out=btv[lo:hi, :, :, (0 if lo == 64 else 2), 8 - dj], in_=x_in[dj][lo:hi])
+        swap_src = const.tile([P, 3, 8, 4], BF16)
+
+        def inner_weights():
+            nc.scalar.copy(out=swap_src[0:64], in_=near_w[0:64, :, :, :, 2])
+            nc.scalar.copy(out=swap_src[64:128], in_=near_w[64:128, :, :, :, 0])
+            swapped = ps_o.tile([P, 3 * NT], F32, tag="o")
+            nc.tensor.matmul(
+                out=swapped[:],
+                lhsT=ident_b[:, 64 : 64 + P],
+                rhs=swap_src[:].rearrange("p k i g -> p (k i g)"),
+                start=True,
+                stop=True,
+            )
+            nc.scalar.copy(out=x_in[:].rearrange("p k i g -> p (k i g)"), in_=swapped[:])
+
+        def band_tables():
+            for k in range(3):
+                nc.scalar.copy(out=btv[:, :, :, 1, 7 + k], in_=near_w[:, k, :, :, 1])
+                nc.scalar.copy(out=btv[64:128, :, :, 0, 7 + k], in_=x_in[64:128, k])
+                nc.scalar.copy(out=btv[0:64, :, :, 2, 7 + k], in_=x_in[0:64, k])
+            for dj in (-4, -2, 2, 4):
+                nc.scalar.copy(out=btv[:, :, :, 1, 8 - dj], in_=far_w[dj][:, :, :, 1])
 
         def band_matrices():
             for first_t, first_r, count in BAND_RANGES:
@@ -337,36 +357,42 @@ def tile_selfattentionmodulev2_pb_kernel(tc, x, attn, v_w, v_b, w_w, w_b, out):
                 a_band.append(a_q)
 
         background = {
-            -3: [lambda: shifted_weights(-1), lambda: shifted_weights(1), lambda: outer_weights(0)],
+            -3: [
+                lambda: shifted_weights(-1),
+                lambda: shifted_weights(1),
+                near_weights,
+            ],
             -2: [
-                lambda: outer_weights(-1),
-                lambda: outer_weights(1),
                 lambda: shifted_weights(-2),
+                lambda: regroup_x(1, 0, nc.scalar.copy),
                 lambda: shifted_weights(2),
-                lambda: shifted_weights(-4),
-                lambda: shifted_weights(4),
             ],
             -1: [
-                lambda: inner_weights(-1),
-                lambda: inner_weights(0),
-                lambda: inner_weights(1),
+                lambda: regroup_x(1, 1, nc.scalar.copy),
+                lambda: shifted_weights(-4),
                 lambda: quantise_x(1, 0),
+                lambda: shifted_weights(4),
                 lambda: quantise_x(1, 1),
+                inner_weights,
+                lambda: load_x(5),
             ],
+            0: [band_tables],
             1: [band_matrices],
         }
 
         def weight(s, turn, o):
             i, g = s % 8, s // 8
             if o == OUTER:
-                return w_out[turn][:, i, g : g + 1]
+                return w_out[:, 1 - turn, i, g : g + 1]
             if turn in TURNS:
-                return x_in[turn - 64][:, i, g : g + 1]
-            if turn == 0:
-                n = 4 if o == 0 else 9 * LEVEL[2 * abs(o)] + (0 if o < 0 else 6) + 1
+                return x_in[:, 65 - turn, i, g : g + 1]
+            if turn == 0 and o != 0:
+                n = 9 * LEVEL[2 * abs(o)] + (0 if o < 0 else 6) + 1
                 return a_t[:, i, g, n : n + 1]
             pos = 1 + (1 if o > 0 else 0) - (1 if o < 0 else 0)
-            return as_w[turn][:, i, g, pos : pos + 1]
+            if abs(turn) <= 1:
+                return near_w[:, 1 - turn, i, g, pos : pos + 1]
+            return far_w[turn][:, i, g, pos : pos + 1]
 
         v_ps, v_sb, w_ps, sums = {}, {}, {}, {}
         pair_tiles, pair_codes, pair_banks = {}, {}, {}
@@ -461,7 +487,7 @@ def tile_selfattentionmodulev2_pb_kernel(tc, x, attn, v_w, v_b, w_w, w_b, out):
                     nc.tensor.matmul(
                         out=ct[:, j, :],
                         lhsT=sums[key][:, j * P : (j + 1) * P],
-                        rhs=rot[key[1]][:],
+                        rhs=rot[key[1]],
                         is_transpose=True,
                         start=(k == 0 and j == 0),
                         stop=(k == len(keys) - 1 and j == 3),
@@ -530,7 +556,7 @@ def tile_selfattentionmodulev2_pb_kernel(tc, x, attn, v_w, v_b, w_w, w_b, out):
                 second_conv((t - 5) // 2)
 
         for t in range(FIRST_STEP, NT + 5):
-            if t == 0:
+            if t == 2:
                 ww_grouped.append(transpose_weight(ww_sb, (nc.scalar.copy, nc.scalar.copy)))
             for s, turn, o, joined in prod_plan.get(t, []):
                 if o == OUTER:
@@ -545,7 +571,7 @@ def tile_selfattentionmodulev2_pb_kernel(tc, x, attn, v_w, v_b, w_w, w_b, out):
                 vector_tap(s, turn, o)
             if t % 2 == 0 and 0 <= (t - 4) // 2 < NT // 2:
                 quantise_pair((t - 4) // 2)
-            if t == 1:
+            if t == 3:
                 ww_q.append(quantise_weight(ww_grouped[0], "ww"))
             if 0 <= t - LAG < NT:
                 add_up(t - LAG, lambda step=t: mx_run(step))
@@ -565,7 +591,7 @@ def tile_selfattentionmodulev2_pb_kernel(tc, x, attn, v_w, v_b, w_w, w_b, out):
                 job()
             for ch in range(2, 8):
                 u = t - (4 * ch - 8)
-                if 0 <= u < 2:
+                if ch > 2 and 0 <= u < 2:
                     regroup_x(ch, u, nc.scalar.copy)
                     if u == 1 and ch + 4 < 8:
                         load_x(ch + 4)

@@ -470,11 +470,11 @@ def tile_selfattentionmodulev2_pb_kernel(tc, x, attn, v_w, v_b, w_w, w_b, out):
             ctx_banks[s] = ct
             keys = row_terms[s]
             ri = band_index(s)
-            middle = len(keys) // 2
+            early, late = max(1, 3 * len(keys) // 10), 7 * len(keys) // 10
             for k, key in enumerate(keys):
-                if k == middle:
-                    if in_band(s):
-                        for j in range(4):
+                for place, blocks in ((early, (0, 1)), (late, (2, 3))):
+                    if in_band(s) and k == place:
+                        for j in blocks:
                             nc.tensor.matmul(
                                 out=ct[:, j, :],
                                 lhsT=v_sb[s][:, j * P : (j + 1) * P],
@@ -482,6 +482,7 @@ def tile_selfattentionmodulev2_pb_kernel(tc, x, attn, v_w, v_b, w_w, w_b, out):
                                 start=False,
                                 stop=False,
                             )
+                if k == late:
                     mx_work()
                 for j in range(4):
                     nc.tensor.matmul(
@@ -583,7 +584,7 @@ def tile_selfattentionmodulev2_pb_kernel(tc, x, attn, v_w, v_b, w_w, w_b, out):
             turn_of_gpsimd = 0
             for s, turn, o, joined in prod_plan.get(t, []):
                 if o != OUTER:
-                    product(s, turn, o, joined, turn_of_gpsimd % 2 == 0)
+                    product(s, turn, o, joined, turn_of_gpsimd % 3 != 1)
                     turn_of_gpsimd += 1
             for s, turn, o in join_plan.get(t, []):
                 gpsimd_join(s, turn, o)

@@ -29,6 +29,7 @@ TURNS = (63, 64, 65)
 LEVEL = {1: 0, 2: 1, 4: 2}
 FIRST_STEP = -3
 OUTER = 7
+HEAD_ROWS = 4
 LAG = 2
 BAND_RANGES = ((3, 0, 11), (18, 11, 14))
 
@@ -278,9 +279,6 @@ def tile_selfattentionmodulev2_pb_kernel(tc, x, attn, v_w, v_b, w_w, w_b, out):
         nc.vector.tensor_reduce(out=a_sum[:], in_=a_t[:, :, :, 0:27], axis=AX.X, op=ALU.add)
         quantise_x(0, 1)
         load_x(4)
-        for h in range(2):
-            regroup_x(2, h, nc.vector.tensor_copy)
-        load_x(6)
         wb = const.tile([P, 4], F32)
         nc.vector.tensor_copy(out=wb[:], in_=wb_bf[:])
 
@@ -291,9 +289,14 @@ def tile_selfattentionmodulev2_pb_kernel(tc, x, attn, v_w, v_b, w_w, w_b, out):
         x_in = const.tile([P, 3, 8, 4], F32)
         far_w, a_band = {}, []
 
+        shifted = {}
+
+        def shifted_windows(dj):
+            shifted[dj] = windows(-dj)
+
         def shifted_weights(dj):
             lvl, side = LEVEL[abs(dj)], (1 if dj > 0 else 0)
-            pa_s = windows(-dj)
+            pa_s = shifted[dj]
             if lvl == 0:
                 dst = near_w[:, 1 - dj]
             else:
@@ -358,26 +361,43 @@ def tile_selfattentionmodulev2_pb_kernel(tc, x, attn, v_w, v_b, w_w, w_b, out):
 
         background = {
             -3: [
+                lambda: shifted_windows(-1),
+                lambda: shifted_windows(1),
                 lambda: shifted_weights(-1),
                 lambda: shifted_weights(1),
                 near_weights,
             ],
             -2: [
-                lambda: shifted_weights(-2),
-                lambda: regroup_x(1, 0, nc.scalar.copy),
-                lambda: shifted_weights(2),
-            ],
-            -1: [
-                lambda: regroup_x(1, 1, nc.scalar.copy),
-                lambda: shifted_weights(-4),
-                lambda: quantise_x(1, 0),
-                lambda: shifted_weights(4),
-                lambda: quantise_x(1, 1),
-                inner_weights,
+                lambda: regroup_x(1, 0, nc.vector.tensor_copy),
+                lambda: regroup_x(1, 1, nc.vector.tensor_copy),
                 lambda: load_x(5),
             ],
-            0: [band_tables],
-            1: [band_matrices],
+            -1: [
+                lambda: shifted_windows(-2),
+                lambda: shifted_windows(2),
+                lambda: shifted_windows(-4),
+                lambda: shifted_windows(4),
+                lambda: regroup_x(2, 0, nc.vector.tensor_copy),
+                lambda: regroup_x(2, 1, nc.vector.tensor_copy),
+                lambda: load_x(6),
+                lambda: quantise_x(1, 0),
+                lambda: quantise_x(1, 1),
+            ],
+            0: [
+                inner_weights,
+                lambda: shifted_weights(-4),
+                lambda: shifted_weights(4),
+            ],
+            1: [
+                band_tables,
+                band_matrices,
+            ],
+        }
+        middle = {
+            0: [
+                lambda: shifted_weights(-2),
+                lambda: shifted_weights(2),
+            ],
         }
 
         def weight(s, turn, o):
@@ -424,7 +444,8 @@ def tile_selfattentionmodulev2_pb_kernel(tc, x, attn, v_w, v_b, w_w, w_b, out):
         def start_row(s):
             i, g = s % 8, s // 8
             sums[(s, 0, None)] = upool.tile([P, C], F32, tag="u0", name="u0_%d" % s)
-            nc.gpsimd.tensor_scalar(
+            engine = nc.vector if s < HEAD_ROWS else nc.gpsimd
+            engine.tensor_scalar(
                 out=sums[(s, 0, None)][:],
                 in0=vb_all[:].rearrange("p j q -> p (j q)"),
                 scalar1=a_sum[:, i, g : g + 1],
@@ -579,12 +600,14 @@ def tile_selfattentionmodulev2_pb_kernel(tc, x, attn, v_w, v_b, w_w, w_b, out):
             else:
                 mx_run(t)
             for s in range(NT):
-                if max(FIRST_STEP, s - LAG - 1) == t:
+                if (FIRST_STEP if s < HEAD_ROWS else s - LAG - 1) == t:
                     start_row(s)
+            for job in middle.get(t, []):
+                job()
             turn_of_gpsimd = 0
             for s, turn, o, joined in prod_plan.get(t, []):
                 if o != OUTER:
-                    product(s, turn, o, joined, turn_of_gpsimd % 3 != 1)
+                    product(s, turn, o, joined, (turn_of_gpsimd * 3) % 5 < 3)
                     turn_of_gpsimd += 1
             for s, turn, o in join_plan.get(t, []):
                 gpsimd_join(s, turn, o)

@@ -20,8 +20,8 @@ TB = NT // B
 NPIX = NT * P
 HALF = NPIX // B
 APAD = 80
-BAND_W = 272
-BAND_PITCH = P * (BAND_W + 1)
+BAND_W = 256
+BAND_PITCH = P * BAND_W
 BAND_PAD = 72
 BAND_GROUP = 5
 SHIFTS = (-4, -2, -1, 1, 2, 4)
@@ -172,9 +172,10 @@ def tile_selfattentionmodulev2_pb_kernel(tc, x, attn, v_w, v_b, w_w, w_b, out):
         nc.vector.memset(at3[:], 0.0)
         ident_f = const.tile([P, P], F32)
         make_identity(nc, ident_f[:])
-        zeros = const.tile([P, BAND_W + 1], F32)
-        nc.gpsimd.memset(zeros[:], 0.0)
-        scratch = out.rearrange("b o r c -> (b o r c)")
+        band_rows = [const.tile([P, BAND_GROUP, BAND_W], F32, name="band_rows%d" % k) for k in range(2)]
+        for rows in band_rows:
+            nc.gpsimd.memset(rows[:], 0.0)
+        scratch = out[1].rearrange("o r c -> (o r c)")
 
         wb_bf = const.tile([P, 4], BF16)
         vb_bf = const.tile([P, 4], BF16)
@@ -192,13 +193,9 @@ def tile_selfattentionmodulev2_pb_kernel(tc, x, attn, v_w, v_b, w_w, w_b, out):
         load_x(2)
         load_x(3)
         ww_sb = load_weight(w_w, "ww")
-        for ri in range(25):
-            nc.sync.dma_start(
-                out=scratch[ri * BAND_PITCH : (ri + 1) * BAND_PITCH].rearrange("(p f) -> p f", p=P), in_=zeros[:]
-            )
 
-        valid = const.tile([P, 8, 4, 32], F32)
-        nc.vector.memset(valid[:], 1.0)
+        inside = const.tile([P, 32], F32)
+        nc.vector.memset(inside[:], 1.0)
         bt = const.tile([P, NT, 3, 16], F32)
         nc.vector.memset(bt[:], 0.0)
         mk = const.tile([P, 8], F32)
@@ -217,23 +214,13 @@ def tile_selfattentionmodulev2_pb_kernel(tc, x, attn, v_w, v_b, w_w, w_b, out):
         )
         for half in range(2):
             nc.vector.tensor_copy(out=ident2[:, half * P : (half + 1) * P], in_=ident_f[:])
-        valid_taps = valid[:, :, :, 0:27].rearrange("p i g (l a j) -> p i g l a j", l=3, a=3)
+        inside_taps = inside[:, 0:27].rearrange("p (l a j) -> p l a j", l=3, a=3)
         for lvl in range(3):
             for side in range(2):
-                view = valid_taps[:, :, :, lvl, :, 2 * side]
-                nc.vector.tensor_scalar(
-                    out=view,
-                    in0=view,
-                    scalar1=mk[:, 2 * lvl + side : 2 * lvl + side + 1],
-                    scalar2=None,
-                    op0=ALU.mult,
+                nc.vector.tensor_copy(
+                    out=inside_taps[:, lvl, :, 2 * side],
+                    in_=mk[:, 2 * lvl + side : 2 * lvl + side + 1].to_broadcast([P, 3]),
                 )
-        nc.vector.memset(valid[0:64, 0, 0:3:2, 0:3], 0.0)
-        nc.vector.memset(valid[64:128, 7, 1:4:2, 6:9], 0.0)
-        nc.vector.memset(valid[:, 0, 0:3:2, 9:12], 0.0)
-        nc.vector.memset(valid[:, 7, 1:4:2, 15:18], 0.0)
-        nc.vector.memset(valid[:, 0:2, 0:3:2, 18:21], 0.0)
-        nc.vector.memset(valid[:, 6:8, 1:4:2, 24:27], 0.0)
         x_codes = const.tile([P, NPIX], U32, align_bytes=64)
         x_plane = const.tile([P, NPIX], U8, align_bytes=64)
         for b in range(B):
@@ -264,20 +251,27 @@ def tile_selfattentionmodulev2_pb_kernel(tc, x, attn, v_w, v_b, w_w, w_b, out):
         regroup_x(0, 0, nc.vector.tensor_copy)
         regroup_x(0, 1, nc.scalar.copy)
         vw_codes, vw_plane = quantise_weight(vw_grouped, "vw")
+        quantise_x(0, 0)
+        quantise_x(0, 1)
         nc.scalar.copy(out=vb_all[:], in_=vb_ps[:])
+        regroup_x(1, 0, nc.scalar.copy)
         a_t = const.tile([P, 8, 4, 32], F32)
         nc.vector.tensor_tensor(
-            out=a_t[:].rearrange("p i g n -> p i (g n)"),
-            in0=pa[:],
-            in1=valid[:].rearrange("p i g n -> p i (g n)"),
+            out=a_t[:].rearrange("p i g n -> p (i g) n"),
+            in0=pa[:].rearrange("p i (g n) -> p (i g) n", g=4),
+            in1=inside[:].unsqueeze(1).to_broadcast([P, NT, 32]),
             op=ALU.mult,
         )
+        nc.vector.memset(a_t[0:64, 0, 0:3:2, 0:3], 0.0)
+        nc.vector.memset(a_t[64:128, 7, 1:4:2, 6:9], 0.0)
+        nc.vector.memset(a_t[:, 0, 0:3:2, 9:12], 0.0)
+        nc.vector.memset(a_t[:, 7, 1:4:2, 15:18], 0.0)
+        nc.vector.memset(a_t[:, 0:2, 0:3:2, 18:21], 0.0)
+        nc.vector.memset(a_t[:, 6:8, 1:4:2, 24:27], 0.0)
         near_w = const.tile([P, 3, 8, 4, 3], F32)
         nc.vector.tensor_reduce(out=near_w[:, 1, :, :, 1], in_=a_t[:, :, :, 4:23:9], axis=AX.X, op=ALU.add)
-        quantise_x(0, 0)
         a_sum = const.tile([P, 8, 4], F32)
         nc.vector.tensor_reduce(out=a_sum[:], in_=a_t[:, :, :, 0:27], axis=AX.X, op=ALU.add)
-        quantise_x(0, 1)
         load_x(4)
         wb = const.tile([P, 4], F32)
         nc.vector.tensor_copy(out=wb[:], in_=wb_bf[:])
@@ -340,24 +334,28 @@ def tile_selfattentionmodulev2_pb_kernel(tc, x, attn, v_w, v_b, w_w, w_b, out):
             for dj in (-4, -2, 2, 4):
                 nc.scalar.copy(out=btv[:, :, :, 1, 8 - dj], in_=far_w[dj][:, :, :, 1])
 
-        def band_matrices():
+        def band_matrices(q):
+            rows = band_rows[q % 2]
+            place = rows[:].rearrange("p r (u t) -> p r u t", t=64)
             for first_t, first_r, count in BAND_RANGES:
-                for u in range(3):
-                    nc.sync.dma_start(
-                        out=scratch[first_r * BAND_PITCH : (first_r + count) * BAND_PITCH].rearrange(
-                            "(r p t) -> p r t", p=P, t=BAND_W + 1
-                        )[:, :, 64 * u : 64 * u + 16],
-                        in_=bt[:, first_t : first_t + count, u, :],
+                lo, hi = max(first_r, q * BAND_GROUP), min(first_r + count, (q + 1) * BAND_GROUP)
+                if lo < hi:
+                    nc.scalar.copy(
+                        out=place[:, lo - q * BAND_GROUP : hi - q * BAND_GROUP, 0:3, 0:16],
+                        in_=bt[:, first_t + lo - first_r : first_t + hi - first_r],
                     )
-            for q in range(25 // BAND_GROUP):
-                a_q = const.tile([P, BAND_GROUP, P], F32, name="a_band%d" % q)
-                nc.sync.dma_start(
-                    out=a_q[:],
-                    in_=scratch[q * BAND_GROUP * BAND_PITCH : (q + 1) * BAND_GROUP * BAND_PITCH]
-                    .rearrange("(r m) -> r m", m=BAND_PITCH)[:, 0 : P * BAND_W]
-                    .rearrange("r (p c) -> p r c", c=BAND_W)[:, :, BAND_PAD : BAND_PAD + P],
-                )
-                a_band.append(a_q)
+            area = scratch[q * BAND_GROUP * BAND_PITCH : (q + 1) * BAND_GROUP * BAND_PITCH].rearrange(
+                "(r m) -> r m", m=BAND_PITCH
+            )
+            nc.sync.dma_start(out=area.rearrange("r (p c) -> p r c", c=BAND_W), in_=rows[:])
+            a_q = const.tile([P, BAND_GROUP, P], F32, name="a_band%d" % q)
+            nc.sync.dma_start(
+                out=a_q[:],
+                in_=area[:, 0 : P * (BAND_W - 1)].rearrange("r (p c) -> p r c", c=BAND_W - 1)[
+                    :, :, BAND_PAD : BAND_PAD + P
+                ],
+            )
+            a_band.append(a_q)
 
         background = {
             -3: [
@@ -368,7 +366,6 @@ def tile_selfattentionmodulev2_pb_kernel(tc, x, attn, v_w, v_b, w_w, w_b, out):
                 near_weights,
             ],
             -2: [
-                lambda: regroup_x(1, 0, nc.vector.tensor_copy),
                 lambda: regroup_x(1, 1, nc.vector.tensor_copy),
                 lambda: load_x(5),
             ],
@@ -390,8 +387,12 @@ def tile_selfattentionmodulev2_pb_kernel(tc, x, attn, v_w, v_b, w_w, w_b, out):
             ],
             1: [
                 band_tables,
-                band_matrices,
+                lambda: band_matrices(0),
             ],
+            2: [lambda: band_matrices(1)],
+            4: [lambda: band_matrices(2)],
+            6: [lambda: band_matrices(3)],
+            8: [lambda: band_matrices(4)],
         }
         middle = {
             0: [

@@ -31,17 +31,16 @@ FIRST_STEP = -3
 OUTER = 7
 HEAD_ROWS = 4
 LAG = 2
-BAND_RANGES = ((3, 0, 11), (18, 11, 14))
 
 FLOPS = 2 * 2 * C * C * B * H * W + 2 * 27 * C * B * H * W
 
 
 def in_band(s):
-    return s not in (0, 1, 2, 14, 15, 16, 17)
+    return s not in (0, 1, 2, 6, 10, 15, 16)
 
 
 def band_index(s):
-    return s - 3 if s < 14 else s - 7
+    return sum(1 for k in range(s) if in_band(k))
 
 
 def group_taps(s, turn):
@@ -337,13 +336,14 @@ def tile_selfattentionmodulev2_pb_kernel(tc, x, attn, v_w, v_b, w_w, w_b, out):
         def band_matrices(q):
             rows = band_rows[q % 2]
             place = rows[:].rearrange("p r (u t) -> p r u t", t=64)
-            for first_t, first_r, count in BAND_RANGES:
-                lo, hi = max(first_r, q * BAND_GROUP), min(first_r + count, (q + 1) * BAND_GROUP)
-                if lo < hi:
-                    nc.scalar.copy(
-                        out=place[:, lo - q * BAND_GROUP : hi - q * BAND_GROUP, 0:3, 0:16],
-                        in_=bt[:, first_t + lo - first_r : first_t + hi - first_r],
-                    )
+            tiles = [s for s in range(NT) if in_band(s)][q * BAND_GROUP : (q + 1) * BAND_GROUP]
+            k = 0
+            while k < BAND_GROUP:
+                run = 1
+                while k + run < BAND_GROUP and tiles[k + run] == tiles[k] + run:
+                    run += 1
+                nc.scalar.copy(out=place[:, k : k + run, 0:3, 0:16], in_=bt[:, tiles[k] : tiles[k] + run])
+                k += run
             area = scratch[q * BAND_GROUP * BAND_PITCH : (q + 1) * BAND_GROUP * BAND_PITCH].rearrange(
                 "(r m) -> r m", m=BAND_PITCH
             )

@@ -154,10 +154,13 @@ def tile_selfattentionmodulev2_pb_kernel(tc, x, attn, v_w, v_b, w_w, w_b, out):
         def regroup_x(ch, h, copy):
             if ch not in gx_tiles:
                 gx_tiles[ch] = xpool.tile([P, 2, 2 * P, 4], BF16, tag="gx", name="gx%d" % ch, align_bytes=64)
-            copy(
-                out=gx_tiles[ch][:, h].rearrange("q (k n) j -> q k n j", k=2),
-                in_=raw_tiles[ch][:].rearrange("q j (k h n) -> q h k n j", k=2, h=2)[:, h],
-            )
+            for k in range(2):
+                copy(
+                    out=gx_tiles[ch][:, h, k * P : (k + 1) * P].rearrange("q (c i) j -> q c j i", i=4),
+                    in_=raw_tiles[ch][:, :, (2 * k + h) * P : (2 * k + h + 1) * P].rearrange(
+                        "q j (c i) -> q c j i", i=4
+                    ),
+                )
 
         def quantise_x(ch, h):
             first = (ch // 4) * HALF + h * (HALF // 2) + (ch % 4) * 2 * P
@@ -615,10 +618,10 @@ def tile_selfattentionmodulev2_pb_kernel(tc, x, attn, v_w, v_b, w_w, w_b, out):
             for job in background.get(t, []):
                 job()
             for ch in range(2, 8):
-                u = t - (4 * ch - 8)
-                if ch > 2 and 0 <= u < 2:
-                    regroup_x(ch, u, nc.scalar.copy)
-                    if u == 1 and ch + 4 < 8:
-                        load_x(ch + 4)
-                if 0 <= u - 2 < 2:
-                    quantise_x(ch, u - 2)
+                for h in range(2):
+                    if ch > 2 and t == 4 * ch - 10 + 2 * h:
+                        regroup_x(ch, h, nc.scalar.copy)
+                        if h == 1 and ch + 4 < 8:
+                            load_x(ch + 4)
+                    if t == 4 * ch - 8 + 2 * h:
+                        quantise_x(ch, h)

from contextlib import ExitStack

import concourse.mybir as mybir
from concourse.masks import make_identity

FP8X4 = mybir.dt.float8_e4m3fn_x4
F32 = mybir.dt.float32
BF16 = mybir.dt.bfloat16
U32 = mybir.dt.uint32
I32 = mybir.dt.int32
U8 = mybir.dt.uint8
ALU = mybir.AluOpType
ACT = mybir.ActivationFunctionType
AX = mybir.AxisListType

P = 128
B, C, H, W = 2, 512, 32, 64
NT = 32
TB = NT // B
NPIX = NT * P
HALF = NPIX // B
APAD = 80
BAND_W = 256
BAND_PITCH = P * BAND_W
BAND_PAD = 72
BAND_GROUP = 5
SHIFTS = (-4, -2, -1, 1, 2, 4)
TURNS = (63, 64, 65)
LEVEL = {1: 0, 2: 1, 4: 2}
FIRST_STEP = -3
OUTER = 7
HEAD_ROWS = 4
LAG = 2

FLOPS = 2 * 2 * C * C * B * H * W + 2 * 27 * C * B * H * W


def in_band(s):
    return s not in (0, 1, 2, 6, 10, 15, 16)


def band_index(s):
    return sum(1 for k in range(s) if in_band(k))


def group_taps(s, turn):
    own = [] if in_band(s) else [0]
    if turn == 0:
        cand = [-2, -1] + own + [OUTER, 1, 2]
    elif abs(turn) == 1:
        cand = own + [OUTER]
    elif turn in TURNS:
        cand = own
    else:
        cand = [-abs(turn) // 2] + own + [abs(turn) // 2]
    return [o for o in cand if o == OUTER or 0 <= s % TB + o < TB]


def merged_groups(s):
    return (-4, 4, -2, 2)


def main_columns(s):
    m, b = s % TB, s // TB
    return b * HALF + (m % 2) * (HALF // 2) + (m // 2) * P


def outer_columns(s):
    m, b = s % TB, s // TB
    return b * HALF + (m if m % 2 == 1 else 15 + m) * W


def tile_selfattentionmodulev2_pb_kernel(tc, x, attn, v_w, v_b, w_w, w_b, out):
    nc = tc.nc

    vec_plan, prod_plan, row_terms, join_plan = {}, {}, {}, {}
    for s in range(NT):
        plain, joined = [], []
        for turn in SHIFTS + TURNS:
            taps = group_taps(s, turn)
            if turn in merged_groups(s) and len(taps) > 1:
                step = max(FIRST_STEP, s + taps[1] - 1)
                prod_plan.setdefault(step, []).append((s, turn, taps[0], True))
                for o in taps[1:]:
                    vec_plan.setdefault(s + o, []).append((s, turn, o))
                joined.append((taps[-1], turn))
            else:
                for o in taps:
                    prod_plan.setdefault(s if o == OUTER else s + LAG - 1, []).append((s, turn, o, False))
                    plain.append((s, turn, o))
        for o in group_taps(s, 0):
            if o == OUTER:
                prod_plan.setdefault(s, []).append((s, 0, o, False))
                if in_band(s):
                    join_plan.setdefault(s, []).append((s, 0, o))
                else:
                    plain.append((s, 0, o))
            else:
                vec_plan.setdefault(s + o, []).append((s, 0, o))
        row_terms[s] = plain + [(s, turn, None) for (last, turn) in sorted(joined)] + [(s, 0, None)]
    for step in vec_plan:
        vec_plan[step] = sorted(vec_plan[step], key=lambda tap: (-tap[2], tap[1] == 0))
    for step in prod_plan:
        prod_plan[step] = sorted(prod_plan[step], key=lambda tap: (tap[2] != OUTER, not tap[3]))

    with ExitStack() as ctx:
        const = ctx.enter_context(tc.tile_pool(name="const", bufs=1))
        wpool = ctx.enter_context(tc.tile_pool(name="wpool", bufs=1))
        xpool = ctx.enter_context(tc.tile_pool(name="xpool", bufs=2))
        vpool = ctx.enter_context(tc.tile_pool(name="vpool", bufs=10))
        upool = ctx.enter_context(tc.tile_pool(name="upool", bufs=10))
        mpool = ctx.enter_context(tc.tile_pool(name="mpool", bufs=19))
        ppool = ctx.enter_context(tc.tile_pool(name="ppool", bufs=18))
        gpool = ctx.enter_context(tc.tile_pool(name="gpool", bufs=2))
        opool = ctx.enter_context(tc.tile_pool(name="opool", bufs=2))
        ps_v = ctx.enter_context(tc.psum_pool(name="ps_v", bufs=3))
        ps_w = ctx.enter_context(tc.psum_pool(name="ps_w", bufs=1))
        ps_c = ctx.enter_context(tc.psum_pool(name="ps_c", bufs=2))
        ps_o = ctx.enter_context(tc.psum_pool(name="ps_o", bufs=2))
        ctx.enter_context(tc.manual_schedule())

        def load_weight(w_dram, label):
            w_sb = wpool.tile([P, 4 * C], BF16, name="w_sb_" + label)
            nc.sync.dma_start(out=w_sb[:], in_=w_dram.rearrange("(q j) k -> q (j k)", j=4))
            return w_sb

        def transpose_weight(w_sb, copy):
            words = w_sb[:].bitcast(F32).rearrange("q (j w u) -> q j u w", j=4, u=2)
            grouped = wpool.tile([P, 4 * C], BF16, tag="w_grouped", align_bytes=64)
            gwords = grouped[:].bitcast(F32).rearrange("q (j o u) -> q j o u", j=4, u=2)
            for half in range(2):
                pt = ps_o.tile([P, 4, P], F32, tag="o")
                for a in range(2):
                    for u in range(2):
                        nc.tensor.transpose(pt[:, 2 * a + u, :], words[:, 2 * half + a, u, :], ident_f[:])
                copy[half](out=gwords[:, 2 * half : 2 * half + 2], in_=pt[:].rearrange("q (a u) o -> q a o u", u=2))
            return grouped

        def quantise_weight(grouped, label):
            codes = const.tile([P, C], U32, name="codes_" + label, align_bytes=64)
            plane = const.tile([P, C], U8, name="plane_" + label, align_bytes=64)
            nc.vector.quantize_mx(out=codes[:].bitcast(FP8X4), scales=plane[:], in_=grouped[:])
            return codes, plane

        raw_tiles, gx_tiles = {}, {}

        def load_x(ch):
            raw_tiles[ch] = xpool.tile([P, 4, 8 * W], BF16, tag="raw", name="raw%d" % ch, bufs=4)
            nc.sync.dma_start(
                out=raw_tiles[ch][:],
                in_=x[ch // 4].rearrange("(q j) r c -> q j (r c)", j=4)[:, :, (ch % 4) * 8 * W : (ch % 4 + 1) * 8 * W],
            )

        def regroup_x(ch, h, copy):
            if ch not in gx_tiles:
                gx_tiles[ch] = xpool.tile([P, 2, 2 * P, 4], BF16, tag="gx", name="gx%d" % ch, align_bytes=64)
            for k in range(2):
                copy(
                    out=gx_tiles[ch][:, h, k * P : (k + 1) * P].rearrange("q (c i) j -> q c j i", i=4),
                    in_=raw_tiles[ch][:, :, (2 * k + h) * P : (2 * k + h + 1) * P].rearrange(
                        "q j (c i) -> q c j i", i=4
                    ),
                )

        def quantise_x(ch, h):
            first = (ch // 4) * HALF + h * (HALF // 2) + (ch % 4) * 2 * P
            nc.vector.quantize_mx(
                out=x_codes[:, first : first + 2 * P].bitcast(FP8X4),
                scales=x_plane[:, first : first + 2 * P],
                in_=gx_tiles[ch][:, h].rearrange("q n j -> q (n j)"),
            )

        at3 = const.tile([P, 8 * P + 2 * APAD], BF16)
        nc.vector.memset(at3[:], 0.0)
        ident_f = const.tile([P, P], F32)
        make_identity(nc, ident_f[:])
        band_rows = [const.tile([P, BAND_GROUP, BAND_W], F32, name="band_rows%d" % k) for k in range(2)]
        for rows in band_rows:
            nc.gpsimd.memset(rows[:], 0.0)
        scratch = out[1].rearrange("o r c -> (o r c)")

        wb_bf = const.tile([P, 4], BF16)
        vb_bf = const.tile([P, 4], BF16)
        vw_sb = load_weight(v_w, "vw")
        load_x(0)
        for g in range(4):
            queue = nc.scalar if g % 2 == 0 else nc.sync
            queue.dma_start(
                out=at3[32 * g : 32 * g + 27, APAD : APAD + 8 * P],
                in_=attn[g // 2, :, 16 * (g % 2) : 16 * (g % 2) + 16, :].rearrange("n r c -> n (r c)"),
            )
        nc.scalar.dma_start(out=vb_bf[:], in_=v_b.rearrange("(q j) -> q j", j=4))
        nc.scalar.dma_start(out=wb_bf[:], in_=w_b.rearrange("(q j) -> q j", j=4))
        load_x(1)
        load_x(2)
        load_x(3)
        ww_sb = load_weight(w_w, "ww")

        inside = const.tile([P, 32], F32)
        nc.vector.memset(inside[:], 1.0)
        bt = const.tile([P, NT, 3, 16], F32)
        nc.vector.memset(bt[:], 0.0)
        mk = const.tile([P, 8], F32)
        idv = ident_f[:].rearrange("p (h c) -> p h c", h=2)
        for lvl, d in enumerate((1, 2, 4)):
            nc.vector.tensor_reduce(out=mk[:, 2 * lvl : 2 * lvl + 1], in_=idv[:, :, 0:d], axis=AX.XY, op=ALU.add)
            nc.vector.tensor_reduce(
                out=mk[:, 2 * lvl + 1 : 2 * lvl + 2], in_=idv[:, :, W - d : W], axis=AX.XY, op=ALU.add
            )
        ident_b = const.tile([P, 2 * P], BF16)
        ident2 = const.tile([P, 2 * P], F32)
        for half in range(2):
            nc.vector.tensor_copy(out=ident_b[:, half * P : (half + 1) * P], in_=ident_f[:])
        nc.vector.tensor_scalar(
            out=mk[:, 0:6], in0=mk[:, 0:6], scalar1=-1.0, scalar2=1.0, op0=ALU.mult, op1=ALU.add
        )
        for half in range(2):
            nc.vector.tensor_copy(out=ident2[:, half * P : (half + 1) * P], in_=ident_f[:])
        inside_taps = inside[:, 0:27].rearrange("p (l a j) -> p l a j", l=3, a=3)
        for lvl in range(3):
            for side in range(2):
                nc.vector.tensor_copy(
                    out=inside_taps[:, lvl, :, 2 * side],
                    in_=mk[:, 2 * lvl + side : 2 * lvl + side + 1].to_broadcast([P, 3]),
                )
        x_codes = const.tile([P, NPIX], U32, align_bytes=64)
        x_plane = const.tile([P, NPIX], U8, align_bytes=64)
        for b in range(B):
            hole = slice(b * HALF + 15 * W, b * HALF + 16 * W)
            nc.vector.memset(x_codes[:, hole].bitcast(I32), 0)
            nc.vector.memset(x_plane[:, hole].bitcast(I32), 0)

        spare = {"n": 0}

        def windows(shift):
            spare["n"] += 1
            if spare["n"] % 2 == 0:
                pt = ps_o.tile([P, 8, P], BF16, tag="o")
            else:
                pt = ps_c.tile([P, 8, P], BF16, tag="ctx")
            for i in range(8):
                nc.tensor.transpose(
                    pt[:, i, :], at3[:, APAD + i * P + shift : APAD + (i + 1) * P + shift], ident_b[:, 0:P]
                )
            return pt

        vw_grouped = transpose_weight(vw_sb, (nc.vector.tensor_copy, nc.scalar.copy))
        vb_ps = ps_c.tile([P, 4, P], BF16, tag="ctx")
        for j in range(4):
            nc.tensor.transpose(vb_ps[:, j, :], vb_bf[:, j : j + 1].to_broadcast([P, P]), ident_b[:, 0:P])
        vb_all = const.tile([P, 4, P], F32)
        pa = windows(0)
        regroup_x(0, 0, nc.vector.tensor_copy)
        regroup_x(0, 1, nc.scalar.copy)
        vw_codes, vw_plane = quantise_weight(vw_grouped, "vw")
        quantise_x(0, 0)
        quantise_x(0, 1)
        nc.scalar.copy(out=vb_all[:], in_=vb_ps[:])
        regroup_x(1, 0, nc.scalar.copy)
        a_t = const.tile([P, 8, 4, 32], F32)
        nc.vector.tensor_tensor(
            out=a_t[:].rearrange("p i g n -> p (i g) n"),
            in0=pa[:].rearrange("p i (g n) -> p (i g) n", g=4),
            in1=inside[:].unsqueeze(1).to_broadcast([P, NT, 32]),
            op=ALU.mult,
        )
        nc.vector.memset(a_t[0:64, 0, 0:3:2, 0:3], 0.0)
        nc.vector.memset(a_t[64:128, 7, 1:4:2, 6:9], 0.0)
        nc.vector.memset(a_t[:, 0, 0:3:2, 9:12], 0.0)
        nc.vector.memset(a_t[:, 7, 1:4:2, 15:18], 0.0)
        nc.vector.memset(a_t[:, 0:2, 0:3:2, 18:21], 0.0)
        nc.vector.memset(a_t[:, 6:8, 1:4:2, 24:27], 0.0)
        near_w = const.tile([P, 3, 8, 4, 3], F32)
        nc.vector.tensor_reduce(out=near_w[:, 1, :, :, 1], in_=a_t[:, :, :, 4:23:9], axis=AX.X, op=ALU.add)
        a_sum = const.tile([P, 8, 4], F32)
        nc.vector.tensor_reduce(out=a_sum[:], in_=a_t[:, :, :, 0:27], axis=AX.X, op=ALU.add)
        load_x(4)
        wb = const.tile([P, 4], F32)
        nc.vector.tensor_copy(out=wb[:], in_=wb_bf[:])

        rot = {turn: ident2[:, turn % P : turn % P + P] for turn in (0,) + SHIFTS + TURNS}

        btv = bt[:].rearrange("p (g i) u t -> p i g u t", g=4)
        w_out = const.tile([P, 3, 8, 4], F32)
        x_in = const.tile([P, 3, 8, 4], F32)
        far_w, a_band = {}, []

        shifted = {}

        def shifted_windows(dj):
            shifted[dj] = windows(-dj)

        def shifted_weights(dj):
            lvl, side = LEVEL[abs(dj)], (1 if dj > 0 else 0)
            pa_s = shifted[dj]
            if lvl == 0:
                dst = near_w[:, 1 - dj]
            else:
                far_w[dj] = const.tile([P, 8, 4, 3], F32, name="far_w%d" % (dj + 4))
                dst = far_w[dj][:]
            first = 9 * lvl + 2 * side
            nc.scalar.activation(
                out=dst,
                in_=pa_s[:].rearrange("p i (g n) -> p i g n", g=4)[:, :, :, first : first + 7 : 3],
                func=ACT.Copy,
                scale=mk[:, 2 * lvl + 1 - side : 2 * lvl + 2 - side],
            )

        def near_weights():
            nc.scalar.copy(out=near_w[:, 1, :, :, 0:3:2], in_=a_t[:, :, :, 1:8:6])
            nc.scalar.copy(out=w_out[0:64], in_=near_w[0:64, :, :, :, 0])
            nc.scalar.copy(out=w_out[64:128], in_=near_w[64:128, :, :, :, 2])
            nc.gpsimd.memset(w_out[0:64, :, 0, 0:3:2], 0.0)
            nc.gpsimd.memset(w_out[64:128, :, 7, 1:4:2], 0.0)

        swap_src = const.tile([P, 3, 8, 4], BF16)

        def inner_weights():
            nc.scalar.copy(out=swap_src[0:64], in_=near_w[0:64, :, :, :, 2])
            nc.scalar.copy(out=swap_src[64:128], in_=near_w[64:128, :, :, :, 0])
            swapped = ps_o.tile([P, 3 * NT], F32, tag="o")
            nc.tensor.matmul(
                out=swapped[:],
                lhsT=ident_b[:, 64 : 64 + P],
                rhs=swap_src[:].rearrange("p k i g -> p (k i g)"),
                start=True,
                stop=True,
            )
            nc.scalar.copy(out=x_in[:].rearrange("p k i g -> p (k i g)"), in_=swapped[:])

        def band_tables():
            for k in range(3):
                nc.scalar.copy(out=btv[:, :, :, 1, 7 + k], in_=near_w[:, k, :, :, 1])
                nc.scalar.copy(out=btv[64:128, :, :, 0, 7 + k], in_=x_in[64:128, k])
                nc.scalar.copy(out=btv[0:64, :, :, 2, 7 + k], in_=x_in[0:64, k])
            for dj in (-4, -2, 2, 4):
                nc.scalar.copy(out=btv[:, :, :, 1, 8 - dj], in_=far_w[dj][:, :, :, 1])

        def band_matrices(q):
            rows = band_rows[q % 2]
            place = rows[:].rearrange("p r (u t) -> p r u t", t=64)
            tiles = [s for s in range(NT) if in_band(s)][q * BAND_GROUP : (q + 1) * BAND_GROUP]
            k = 0
            while k < BAND_GROUP:
                run = 1
                while k + run < BAND_GROUP and tiles[k + run] == tiles[k] + run:
                    run += 1
                nc.scalar.copy(out=place[:, k : k + run, 0:3, 0:16], in_=bt[:, tiles[k] : tiles[k] + run])
                k += run
            area = scratch[q * BAND_GROUP * BAND_PITCH : (q + 1) * BAND_GROUP * BAND_PITCH].rearrange(
                "(r m) -> r m", m=BAND_PITCH
            )
            nc.sync.dma_start(out=area.rearrange("r (p c) -> p r c", c=BAND_W), in_=rows[:])
            a_q = const.tile([P, BAND_GROUP, P], F32, name="a_band%d" % q)
            nc.sync.dma_start(
                out=a_q[:],
                in_=area[:, 0 : P * (BAND_W - 1)].rearrange("r (p c) -> p r c", c=BAND_W - 1)[
                    :, :, BAND_PAD : BAND_PAD + P
                ],
            )
            a_band.append(a_q)

        background = {
            -3: [
                lambda: shifted_windows(-1),
                lambda: shifted_windows(1),
                lambda: shifted_weights(-1),
                lambda: shifted_weights(1),
                near_weights,
            ],
            -2: [
                lambda: regroup_x(1, 1, nc.vector.tensor_copy),
                lambda: load_x(5),
            ],
            -1: [
                lambda: shifted_windows(-2),
                lambda: shifted_windows(2),
                lambda: shifted_windows(-4),
                lambda: shifted_windows(4),
                lambda: regroup_x(2, 0, nc.vector.tensor_copy),
                lambda: regroup_x(2, 1, nc.vector.tensor_copy),
                lambda: load_x(6),
                lambda: quantise_x(1, 0),
                lambda: quantise_x(1, 1),
            ],
            0: [
                inner_weights,
                lambda: shifted_weights(-4),
                lambda: shifted_weights(4),
            ],
            1: [
                band_tables,
                lambda: band_matrices(0),
            ],
            2: [lambda: band_matrices(1)],
            4: [lambda: band_matrices(2)],
            6: [lambda: band_matrices(3)],
            8: [lambda: band_matrices(4)],
        }
        middle = {
            0: [
                lambda: shifted_weights(-2),
                lambda: shifted_weights(2),
            ],
        }

        def weight(s, turn, o):
            i, g = s % 8, s // 8
            if o == OUTER:
                return w_out[:, 1 - turn, i, g : g + 1]
            if turn in TURNS:
                return x_in[:, 65 - turn, i, g : g + 1]
            if turn == 0 and o != 0:
                n = 9 * LEVEL[2 * abs(o)] + (0 if o < 0 else 6) + 1
                return a_t[:, i, g, n : n + 1]
            pos = 1 + (1 if o > 0 else 0) - (1 if o < 0 else 0)
            if abs(turn) <= 1:
                return near_w[:, 1 - turn, i, g, pos : pos + 1]
            return far_w[turn][:, i, g, pos : pos + 1]

        v_ps, v_sb, w_ps, sums = {}, {}, {}, {}
        pair_tiles, pair_codes, pair_banks = {}, {}, {}
        ww_grouped, ww_q = [], []

        def first_conv(dst, first):
            nc.tensor.matmul_mx(
                out=dst[:],
                lhsT=x_codes[:, first : first + P].bitcast(FP8X4),
                lhsT_scale=x_plane[:, first : first + P],
                rhs=vw_codes[:].bitcast(FP8X4),
                rhs_scale=vw_plane[:],
                start=True,
                stop=True,
            )

        def main_value(s):
            v_ps[s] = ps_v.tile([P, C], F32, tag="v0", name="v_ps%d" % s)
            first_conv(v_ps[s], main_columns(s))

        def outer_value(s):
            w_ps[s] = ps_w.tile([P, C], F32, tag="w", name="w_ps%d" % s)
            first_conv(w_ps[s], outer_columns(s))

        def copy_value(s):
            v_sb[s] = vpool.tile([P, C], F32, tag="v_sb", name="v_sb%d" % s)
            nc.scalar.copy(out=v_sb[s][:], in_=v_ps[s][:])

        def start_row(s):
            i, g = s % 8, s // 8
            sums[(s, 0, None)] = upool.tile([P, C], F32, tag="u0", name="u0_%d" % s)
            engine = nc.vector if s < HEAD_ROWS else nc.gpsimd
            engine.tensor_scalar(
                out=sums[(s, 0, None)][:],
                in0=vb_all[:].rearrange("p j q -> p (j q)"),
                scalar1=a_sum[:, i, g : g + 1],
                scalar2=0.0,
                op0=ALU.mult,
                op1=ALU.add,
            )

        def product(s, turn, o, joined, on_gpsimd):
            if joined:
                key = (s, turn, None)
                sums[key] = mpool.tile([P, C], F32, tag="um", name="um_%d_%d" % (s, turn + 4))
            else:
                key = (s, turn, o)
                sums[key] = ppool.tile([P, C], F32, tag="pr", name="pr_%d_%d_%d" % (s, turn + 4, o + 4))
            source = w_ps[s] if o == OUTER else v_sb[s + o]
            if on_gpsimd:
                nc.gpsimd.tensor_scalar(
                    out=sums[key][:],
                    in0=source[:],
                    scalar1=weight(s, turn, o),
                    scalar2=0.0,
                    op0=ALU.mult,
                    op1=ALU.add,
                )
            else:
                nc.scalar.activation(out=sums[key][:], in_=source[:], func=ACT.Copy, scale=weight(s, turn, o))

        def gpsimd_join(s, turn, o):
            acc = sums[(s, turn, None)]
            nc.gpsimd.tensor_tensor(out=acc[:], in0=acc[:], in1=sums[(s, turn, o)][:], op=ALU.add)

        def vector_tap(s, turn, o):
            acc = sums[(s, turn, None)]
            nc.vector.scalar_tensor_tensor(
                out=acc[:], in0=v_ps[s + o][:], scalar=weight(s, turn, o), in1=acc[:], op0=ALU.mult, op1=ALU.add
            )

        ctx_banks = {}

        def add_up(s, mx_work):
            ct = ps_c.tile([P, 4, P], F32, tag="ctx", name="ct%d" % s)
            ctx_banks[s] = ct
            keys = row_terms[s]
            ri = band_index(s)
            early, late = max(1, 3 * len(keys) // 10), 7 * len(keys) // 10
            for k, key in enumerate(keys):
                for place, blocks in ((early, (0, 1)), (late, (2, 3))):
                    if in_band(s) and k == place:
                        for j in blocks:
                            nc.tensor.matmul(
                                out=ct[:, j, :],
                                lhsT=v_sb[s][:, j * P : (j + 1) * P],
                                rhs=a_band[ri // BAND_GROUP][:, ri % BAND_GROUP, :],
                                start=False,
                                stop=False,
                            )
                if k == late:
                    mx_work()
                for j in range(4):
                    nc.tensor.matmul(
                        out=ct[:, j, :],
                        lhsT=sums[key][:, j * P : (j + 1) * P],
                        rhs=rot[key[1]],
                        is_transpose=True,
                        start=(k == 0 and j == 0),
                        stop=(k == len(keys) - 1 and j == 3),
                    )

        def round_context(s):
            pair = s // 2
            if pair not in pair_tiles:
                pair_tiles[pair] = gpool.tile([P, 2, P, 4], BF16, tag="g2", name="g2_%d" % pair, align_bytes=64)
            nc.scalar.copy(out=pair_tiles[pair][:, s % 2], in_=ctx_banks[s][:].rearrange("q j n -> q n j"))

        def quantise_pair(pair):
            c_codes = gpool.tile([P, 2 * P], U32, tag="c_codes", name="c_codes%d" % pair, align_bytes=64)
            c_plane = gpool.tile([P, 2 * P], U8, tag="c_plane", name="c_plane%d" % pair, align_bytes=64)
            nc.vector.quantize_mx(
                out=c_codes[:].bitcast(FP8X4),
                scales=c_plane[:],
                in_=pair_tiles[pair][:].rearrange("q b n j -> q (b n j)"),
            )
            pair_codes[pair] = (c_codes, c_plane)

        def second_conv(pair):
            c_codes, c_plane = pair_codes[pair]
            ww_codes, ww_plane = ww_q[0]
            banks = []
            for half in range(2):
                po = ps_o.tile([P, 2, 2 * P], F32, tag="o")
                banks.append(po)
                for a in range(2):
                    j = 2 * half + a
                    nc.tensor.matmul_mx(
                        out=po[:, a, :],
                        lhsT=ww_codes[:, j * P : (j + 1) * P].bitcast(FP8X4),
                        lhsT_scale=ww_plane[:, j * P : (j + 1) * P],
                        rhs=c_codes[:].bitcast(FP8X4),
                        rhs_scale=c_plane[:],
                        start=True,
                        stop=True,
                    )
            pair_banks[pair] = banks

        def store_pair(pair):
            banks = pair_banks[pair]
            ot = opool.tile([P, 4, 2 * P], F32, tag="ot")
            for j in range(4):
                if pair >= NT // 2 - 2 and j >= 2:
                    nc.vector.tensor_scalar(
                        out=ot[:, j, :], in0=banks[1][:, j % 2, :], scalar1=wb[:, j : j + 1], scalar2=None, op0=ALU.add
                    )
                    continue
                nc.scalar.activation(
                    out=ot[:, j, :], in_=banks[j // 2][:, j % 2, :], func=ACT.Identity, bias=wb[:, j : j + 1], scale=1.0
                )
            first = (2 * pair % TB) * P
            nc.sync.dma_start(
                out=out[2 * pair // TB].rearrange("(q j) r c -> q j (r c)", j=4)[:, :, first : first + 2 * P],
                in_=ot[:],
            )

        def mx_run(t):
            if 0 <= t + 2 < NT:
                main_value(t + 2)
            if 0 <= t + 1 < NT:
                outer_value(t + 1)
            if t % 2 == 1 and 0 <= (t - 5) // 2 < NT // 2:
                second_conv((t - 5) // 2)

        for t in range(FIRST_STEP, NT + 5):
            if t == 2:
                ww_grouped.append(transpose_weight(ww_sb, (nc.scalar.copy, nc.scalar.copy)))
            for s, turn, o, joined in prod_plan.get(t, []):
                if o == OUTER:
                    product(s, turn, o, joined, False)
            if 0 <= t - LAG - 1 < NT:
                round_context(t - LAG - 1)
            if 0 <= t + 1 < NT:
                copy_value(t + 1)
            if t % 2 == 0 and 0 <= (t - 6) // 2 < NT // 2:
                store_pair((t - 6) // 2)
            for s, turn, o in vec_plan.get(t, []):
                vector_tap(s, turn, o)
            if t % 2 == 0 and 0 <= (t - 4) // 2 < NT // 2:
                quantise_pair((t - 4) // 2)
            if t == 3:
                ww_q.append(quantise_weight(ww_grouped[0], "ww"))
            if 0 <= t - LAG < NT:
                add_up(t - LAG, lambda step=t: mx_run(step))
            else:
                mx_run(t)
            for s in range(NT):
                if (FIRST_STEP if s < HEAD_ROWS else s - LAG - 1) == t:
                    start_row(s)
            for job in middle.get(t, []):
                job()
            turn_of_gpsimd = 0
            for s, turn, o, joined in prod_plan.get(t, []):
                if o != OUTER:
                    product(s, turn, o, joined, (turn_of_gpsimd * 3) % 5 < 3)
                    turn_of_gpsimd += 1
            for s, turn, o in join_plan.get(t, []):
                gpsimd_join(s, turn, o)
            for job in background.get(t, []):
                job()
            for ch in range(2, 8):
                for h in range(2):
                    if ch > 2 and t == 4 * ch - 10 + 2 * h:
                        regroup_x(ch, h, nc.scalar.copy)
                        if h == 1 and ch + 4 < 8:
                            load_x(ch + 4)
                    if t == 4 * ch - 8 + 2 * h:
                        quantise_x(ch, h)
